import numpy as np
import ml_dtypes


def mxq(x, axis, fmt="e4m3"):
    dtype, down = {"e4m3": (ml_dtypes.float8_e4m3fn, 7), "e5m2": (ml_dtypes.float8_e5m2, 14)}[fmt]
    v = np.moveaxis(np.asarray(x, np.float32).astype(ml_dtypes.bfloat16).astype(np.float64), axis, -1)
    blocks = v.reshape(v.shape[:-1] + (-1, 32))
    amax = np.abs(blocks).max(-1, keepdims=True)
    byte = np.maximum(np.where(amax > 0, np.frexp(amax)[1] - 1 + 127, 0) - down, 1)
    scale = np.exp2(byte - 127.0)
    codes = (blocks / scale).astype(np.float32).astype(dtype).astype(np.float64)
    return np.moveaxis((codes * scale).reshape(v.shape), -1, axis)


WIDE = False


def mx_kscale(k):
    if not WIDE:
        return np.ones(k)
    levels = np.array([10, -10, 5, -5, 0])
    a = np.random.permutation(np.resize(levels, k // 512 * 4)).reshape(k // 512, 4)
    idx = np.arange(k)
    return np.exp2(a[idx // 512, idx % 128 // 32])


BF16 = ml_dtypes.bfloat16


def bf(x):
    return np.asarray(x, np.float32).astype(BF16)


def f64(x):
    return np.asarray(x).astype(np.float64)


M, I, O, K = 8192, 32, 256, 32
DEG = 3


def bspline_basis(x, knots, degree):
    h = knots[1] - knots[0]
    t = np.concatenate([knots, knots[-1] + h * np.arange(1, degree + 2)])
    xe = x[..., None]
    Bp = np.where((xe >= t[:-1]) & (xe < t[1:]), 1.0, 0.0)
    for p in range(1, degree + 1):
        left = (xe - t[: -(p + 1)]) / (t[p:-1] - t[: -(p + 1)])
        right = (t[p + 1:] - xe) / (t[p + 1:] - t[1:-p])
        Bp = left * Bp[..., :-1] + right * Bp[..., 1:]
    return Bp


def setup_inputs():
    knots = bf(np.linspace(0.0, 1.0, K))
    kn = f64(knots)
    xmax = kn[-1] + (DEG + 1) * (kn[1] - kn[0])
    s = mx_kscale(I * K)[::K]
    c = np.exp2(np.round(np.log2(s / s.max()) / DEG))
    u = np.random.uniform(size=(M, I))
    x = np.where(c < 1.0, u * kn[1] * c, u * xmax)
    g = np.where(c < 1.0, 8.0 / c**DEG, 1.0)
    coeffs = np.random.standard_normal((I, O, K)) * 1.5 / np.sqrt(I) * g[:, None, None]
    return {"x": bf(x), "spline_coeffs": bf(coeffs), "spline_knots": knots}


def reference(x, spline_coeffs, spline_knots):
    basis = bspline_basis(f64(x), f64(spline_knots), DEG)
    a = basis.reshape(M, I * K)
    w = f64(spline_coeffs).transpose(0, 2, 1).reshape(I * K, O)
    return mxq(a, 1, "e4m3") @ mxq(w, 0, "e4m3")

@@ -1,0 +1,242 @@
+from contextlib import ExitStack
+
+import concourse.mybir as mybir
+from concourse.masks import make_identity
+
+F32 = mybir.dt.float32
+BF16 = mybir.dt.bfloat16
+U32 = mybir.dt.uint32
+U8 = mybir.dt.uint8
+FP8X4 = mybir.dt.float8_e4m3fn_x4
+ALU = mybir.AluOpType
+ACT = mybir.ActivationFunctionType
+
+P = 128
+PACK = 4
+ROWS = 8192
+FEATURES = 32
+OUTS = 256
+KNOTS = 32
+DEGREE = 3
+PASSES = 2
+FEATURES_PER_PASS = FEATURES // PASSES
+WORDS_PER_FEATURE = KNOTS // PACK
+CUBES = PACK + DEGREE + 1
+ROW_TILES = ROWS // P
+TILES_PER_CHUNK = 4
+CHUNKS = ROW_TILES // TILES_PER_CHUNK
+COLS = TILES_PER_CHUNK * PASSES * P
+
+FLOPS = 2 * ROWS * FEATURES * KNOTS * OUTS
+
+
+def load_knot_scalars(nc, const, identity, spline_knots):
+    knots_bf = const.tile([P, KNOTS], BF16)
+    nc.sync.dma_start(out=knots_bf[:], in_=spline_knots.partition_broadcast(P))
+    extended = const.tile([P, KNOTS + DEGREE + 1], F32)
+    nc.vector.tensor_copy(out=extended[:, 0:KNOTS], in_=knots_bf[:])
+    step = const.tile([P, 1], F32)
+    nc.vector.tensor_sub(out=step[:], in0=extended[:, 1:2], in1=extended[:, 0:1])
+    for j in range(DEGREE + 1):
+        nc.vector.tensor_scalar(
+            out=extended[:, KNOTS + j : KNOTS + j + 1],
+            in0=step[:],
+            scalar1=float(j + 1),
+            scalar2=extended[:, KNOTS - 1 : KNOTS],
+            op0=ALU.mult,
+            op1=ALU.add,
+        )
+
+    is_r = const.tile([P, WORDS_PER_FEATURE], F32)
+    nc.vector.tensor_reduce(
+        out=is_r[:],
+        in_=identity[:].rearrange("p (f r) -> p r f", r=WORDS_PER_FEATURE),
+        axis=mybir.AxisListType.X,
+        op=ALU.add,
+    )
+    windows = const.tile([P, CUBES, WORDS_PER_FEATURE], F32)
+    for half in range(CUBES // PACK):
+        nc.vector.tensor_tensor(
+            out=windows[:, PACK * half : PACK * half + PACK, :],
+            in0=extended[:, PACK * half : PACK * half + KNOTS].rearrange("p (r j) -> p j r", j=PACK),
+            in1=is_r[:].unsqueeze(1).to_broadcast([P, PACK, WORDS_PER_FEATURE]),
+            op=ALU.mult,
+        )
+    knot = const.tile([P, CUBES], F32)
+    nc.vector.tensor_reduce(out=knot[:], in_=windows[:], axis=mybir.AxisListType.X, op=ALU.add)
+    neg_knot = const.tile([P, CUBES], F32)
+    nc.vector.tensor_scalar_mul(out=neg_knot[:], in0=knot[:], scalar1=-1.0)
+
+    gap = {}
+    for n in range(1, DEGREE + 2):
+        gap[n] = const.tile([P, CUBES - n], F32, name="gap%d" % n)
+        nc.vector.tensor_sub(out=gap[n][:], in0=knot[:, n:CUBES], in1=knot[:, 0 : CUBES - n])
+
+    factors = {
+        "a0": [gap[1][:, 0:4], gap[2][:, 0:4], gap[3][:, 0:4]],
+        "a1": [gap[1][:, 0:4], gap[1][:, 1:5], gap[2][:, 1:5], gap[3][:, 1:5]],
+        "b4": [gap[3][:, 1:5], gap[2][:, 2:6], gap[1][:, 3:7]],
+        "b3": [gap[1][:, 3:7], gap[1][:, 2:6], gap[2][:, 1:5], gap[3][:, 0:4]],
+    }
+    inverse = {}
+    for key in ("a0", "a1", "b4", "b3"):
+        product = const.tile([P, PACK], F32, name="product_" + key)
+        nc.vector.tensor_mul(out=product[:], in0=factors[key][0], in1=factors[key][1])
+        for factor in factors[key][2:]:
+            nc.vector.tensor_mul(out=product[:], in0=product[:], in1=factor)
+        inverse[key] = const.tile([P, PACK], F32, name="inverse_" + key)
+        nc.vector.reciprocal(out=inverse[key][:], in_=product[:])
+
+    a1 = const.tile([P, PACK], F32)
+    nc.vector.tensor_mul(out=a1[:], in0=inverse["a1"][:], in1=gap[4][:])
+    neg_b3 = const.tile([P, PACK], F32)
+    nc.vector.scalar_tensor_tensor(
+        out=neg_b3[:], in0=inverse["b3"][:], scalar=-1.0, in1=gap[4][:], op0=ALU.mult, op1=ALU.mult
+    )
+    neg_b4 = const.tile([P, PACK], F32)
+    nc.vector.tensor_scalar_mul(out=neg_b4[:], in0=inverse["b4"][:], scalar1=-1.0)
+    return {"knot": knot, "neg_knot": neg_knot, "a0": inverse["a0"], "a1": a1, "neg_b3": neg_b3, "neg_b4": neg_b4}
+
+
+def quantise_coefficients(nc, const, transposed, identity, spline_coeffs):
+    halves = OUTS // P
+    per_pass = FEATURES_PER_PASS * KNOTS
+    natural = const.tile([P, halves, FEATURES * KNOTS], BF16)
+    for h in range(halves):
+        nc.sync.dma_start(
+            out=natural[:, h, :].rearrange("q (i k) -> q i k", k=KNOTS),
+            in_=spline_coeffs[:, P * h : P * h + P, :].rearrange("i q k -> q i k"),
+        )
+    sorted_w = const.tile([P, halves, PASSES, PACK, P], BF16)
+    for h in range(halves):
+        nc.vector.tensor_copy(
+            out=sorted_w[:, h, :, :, :],
+            in_=natural[:, h, :].rearrange("q (g p w) -> q g w p", g=PASSES, w=PACK),
+        )
+    grouped = const.tile([P, PASSES, OUTS, PACK], BF16, align_bytes=64)
+    for g in range(PASSES):
+        flipped = transposed.tile([P, PACK, OUTS], BF16, tag="transposed")
+        for w in range(PACK):
+            for h in range(halves):
+                nc.tensor.transpose(flipped[:, w, P * h : P * h + P], sorted_w[:, h, g, w, :], identity[:])
+        nc.vector.tensor_copy(out=grouped[:, g, :, :], in_=flipped[:].rearrange("p w o -> p o w"))
+    codes = const.tile([P, PASSES, OUTS], U32, align_bytes=64)
+    scales = const.tile([P, PASSES, OUTS], U8, align_bytes=64)
+    nc.vector.quantize_mx(
+        out=codes[:].rearrange("p g o -> p (g o)").bitcast(FP8X4),
+        scales=scales[:].rearrange("p g o -> p (g o)"),
+        in_=grouped[:].rearrange("p g o w -> p (g o w)"),
+    )
+    return codes, scales
+
+
+def tile_kanlayer_t_kernel(tc, x, spline_coeffs, spline_knots, out):
+    nc = tc.nc
+    with ExitStack() as ctx:
+        const = ctx.enter_context(tc.tile_pool(name="const", bufs=1))
+        work = ctx.enter_context(tc.tile_pool(name="work", bufs=2))
+        transposed = ctx.enter_context(tc.psum_pool(name="transposed", bufs=2))
+        sums = ctx.enter_context(tc.psum_pool(name="sums", bufs=4))
+
+        identity = const.tile([P, P], BF16)
+        make_identity(nc, identity[:])
+
+        x_rows = const.tile([P, ROW_TILES, FEATURES], BF16)
+        nc.sync.dma_start(out=x_rows[:], in_=x.rearrange("(m a) i -> m a i", a=ROW_TILES))
+        out_rows = out.rearrange("(m a) o -> m a o", a=ROW_TILES)
+
+        scalars = load_knot_scalars(nc, const, identity, spline_knots)
+        w_codes, w_scales = quantise_coefficients(nc, const, transposed, identity, spline_coeffs)
+
+        for chunk in range(CHUNKS):
+            first = chunk * TILES_PER_CHUNK
+
+            repeated = work.tile([P, TILES_PER_CHUNK * FEATURES, WORDS_PER_FEATURE], BF16)
+            nc.scalar.copy(
+                out=repeated[:],
+                in_=x_rows[:, first : first + TILES_PER_CHUNK, :]
+                .rearrange("m a i -> m (a i)")
+                .unsqueeze(2)
+                .to_broadcast([P, TILES_PER_CHUNK * FEATURES, WORDS_PER_FEATURE]),
+            )
+            blocks = repeated[:].rearrange("m (n f) r -> m n (f r)", f=FEATURES_PER_PASS)
+            x_flipped = transposed.tile([P, COLS], BF16, tag="transposed")
+            for n in range(TILES_PER_CHUNK * PASSES):
+                nc.tensor.transpose(x_flipped[:, P * n : P * n + P], blocks[:, n, :], identity[:])
+            x_cols = work.tile([P, COLS], BF16)
+            nc.scalar.copy(out=x_cols[:], in_=x_flipped[:])
+
+            cube = work.tile([P, CUBES, COLS], F32)
+            for j in range(CUBES):
+                nc.scalar.activation(
+                    out=cube[:, j, :], in_=x_cols[:], func=ACT.Square, bias=scalars["neg_knot"][:, j : j + 1]
+                )
+            for j in range(CUBES):
+                nc.vector.scalar_tensor_tensor(
+                    out=cube[:, j, :],
+                    in0=x_cols[:],
+                    scalar=scalars["knot"][:, j : j + 1],
+                    in1=cube[:, j, :],
+                    op0=ALU.subtract,
+                    op1=ALU.mult,
+                )
+
+            left = work.tile([P, PACK, COLS], F32)
+            right = work.tile([P, PACK, COLS], F32)
+            for w in range(PACK):
+                nc.scalar.activation(
+                    out=left[:, w, :], in_=cube[:, w + 1, :], func=ACT.Relu, scale=scalars["a1"][:, w : w + 1]
+                )
+                nc.scalar.activation(
+                    out=right[:, w, :], in_=cube[:, w + 3, :], func=ACT.Relu, scale=scalars["neg_b3"][:, w : w + 1]
+                )
+            for w in range(PACK):
+                nc.vector.scalar_tensor_tensor(
+                    out=left[:, w, :],
+                    in0=cube[:, w, :],
+                    scalar=scalars["a0"][:, w : w + 1],
+                    in1=left[:, w, :],
+                    op0=ALU.mult,
+                    op1=ALU.subtract,
+                )
+                nc.vector.scalar_tensor_tensor(
+                    out=right[:, w, :],
+                    in0=cube[:, w + 4, :],
+                    scalar=scalars["neg_b4"][:, w : w + 1],
+                    in1=right[:, w, :],
+                    op0=ALU.mult,
+                    op1=ALU.subtract,
+                )
+
+            basis = work.tile([P, COLS, PACK], BF16, align_bytes=64)
+            nc.vector.scalar_tensor_tensor(
+                out=basis[:],
+                in0=left[:].rearrange("p w c -> p c w"),
+                scalar=0.0,
+                in1=right[:].rearrange("p w c -> p c w"),
+                op0=ALU.max,
+                op1=ALU.max,
+            )
+            codes = work.tile([P, COLS], U32, align_bytes=64)
+            scales = work.tile([P, COLS], U8, align_bytes=64)
+            nc.vector.quantize_mx(
+                out=codes[:].bitcast(FP8X4), scales=scales[:], in_=basis[:].rearrange("p c w -> p (c w)")
+            )
+
+            result = work.tile([P, TILES_PER_CHUNK, OUTS], F32)
+            for pair in range(TILES_PER_CHUNK // 2):
+                acc = sums.tile([P, 2, OUTS], F32)
+                for s in range(2):
+                    for g in range(PASSES):
+                        n = (2 * pair + s) * PASSES + g
+                        nc.tensor.matmul_mx(
+                            out=acc[:, s, :],
+                            lhsT=codes[:, P * n : P * n + P].bitcast(FP8X4),
+                            lhsT_scale=scales[:, P * n : P * n + P],
+                            rhs=w_codes[:, g, :].bitcast(FP8X4),
+                            rhs_scale=w_scales[:, g, :],
+                            start=(g == 0),
+                            stop=(g == PASSES - 1),
+                        )
+                nc.scalar.copy(out=result[:, 2 * pair : 2 * pair + 2, :], in_=acc[:])
+            nc.sync.dma_start(out=out_rows[:, first : first + TILES_PER_CHUNK, :], in_=result[:])

@@ -18,89 +18,76 @@ FEATURES = 32
 OUTS = 256
 KNOTS = 32
 DEGREE = 3
+ALL_KNOTS = KNOTS + DEGREE + 1
 PASSES = 2
 FEATURES_PER_PASS = FEATURES // PASSES
 WORDS_PER_FEATURE = KNOTS // PACK
-CUBES = PACK + DEGREE + 1
 ROW_TILES = ROWS // P
-TILES_PER_CHUNK = 4
+TILES_PER_CHUNK = 16
 CHUNKS = ROW_TILES // TILES_PER_CHUNK
-COLS = TILES_PER_CHUNK * PASSES * P
+TILES_PER_GROUP = 4
+GROUP_COLS = TILES_PER_GROUP * PASSES * P
+KNOTS_PER_ROW_TILE = 2
+VECTOR_TAKES_EVERY = 4
 
 FLOPS = 2 * ROWS * FEATURES * KNOTS * OUTS
 
 
-def load_knot_scalars(nc, const, identity, spline_knots):
+def load_knot_scalars(nc, const, spline_knots):
     knots_bf = const.tile([P, KNOTS], BF16)
     nc.sync.dma_start(out=knots_bf[:], in_=spline_knots.partition_broadcast(P))
-    extended = const.tile([P, KNOTS + DEGREE + 1], F32)
-    nc.vector.tensor_copy(out=extended[:, 0:KNOTS], in_=knots_bf[:])
+    knot = const.tile([P, ALL_KNOTS], F32)
+    nc.vector.tensor_copy(out=knot[:, 0:KNOTS], in_=knots_bf[:])
     step = const.tile([P, 1], F32)
-    nc.vector.tensor_sub(out=step[:], in0=extended[:, 1:2], in1=extended[:, 0:1])
+    nc.vector.tensor_sub(out=step[:], in0=knot[:, 1:2], in1=knot[:, 0:1])
     for j in range(DEGREE + 1):
         nc.vector.tensor_scalar(
-            out=extended[:, KNOTS + j : KNOTS + j + 1],
+            out=knot[:, KNOTS + j : KNOTS + j + 1],
             in0=step[:],
             scalar1=float(j + 1),
-            scalar2=extended[:, KNOTS - 1 : KNOTS],
+            scalar2=knot[:, KNOTS - 1 : KNOTS],
             op0=ALU.mult,
             op1=ALU.add,
         )
-
-    is_r = const.tile([P, WORDS_PER_FEATURE], F32)
-    nc.vector.tensor_reduce(
-        out=is_r[:],
-        in_=identity[:].rearrange("p (f r) -> p r f", r=WORDS_PER_FEATURE),
-        axis=mybir.AxisListType.X,
-        op=ALU.add,
-    )
-    windows = const.tile([P, CUBES, WORDS_PER_FEATURE], F32)
-    for half in range(CUBES // PACK):
-        nc.vector.tensor_tensor(
-            out=windows[:, PACK * half : PACK * half + PACK, :],
-            in0=extended[:, PACK * half : PACK * half + KNOTS].rearrange("p (r j) -> p j r", j=PACK),
-            in1=is_r[:].unsqueeze(1).to_broadcast([P, PACK, WORDS_PER_FEATURE]),
-            op=ALU.mult,
-        )
-    knot = const.tile([P, CUBES], F32)
-    nc.vector.tensor_reduce(out=knot[:], in_=windows[:], axis=mybir.AxisListType.X, op=ALU.add)
-    neg_knot = const.tile([P, CUBES], F32)
+    neg_knot = const.tile([P, ALL_KNOTS], F32)
     nc.vector.tensor_scalar_mul(out=neg_knot[:], in0=knot[:], scalar1=-1.0)
 
     gap = {}
     for n in range(1, DEGREE + 2):
-        gap[n] = const.tile([P, CUBES - n], F32, name="gap%d" % n)
-        nc.vector.tensor_sub(out=gap[n][:], in0=knot[:, n:CUBES], in1=knot[:, 0 : CUBES - n])
+        gap[n] = const.tile([P, ALL_KNOTS - n], F32, name="gap%d" % n)
+        nc.vector.tensor_sub(out=gap[n][:], in0=knot[:, n:ALL_KNOTS], in1=knot[:, 0 : ALL_KNOTS - n])
+
+    def from_k(n, shift):
+        return gap[n][:, shift : shift + KNOTS]
 
     factors = {
-        "a0": [gap[1][:, 0:4], gap[2][:, 0:4], gap[3][:, 0:4]],
-        "a1": [gap[1][:, 0:4], gap[1][:, 1:5], gap[2][:, 1:5], gap[3][:, 1:5]],
-        "b4": [gap[3][:, 1:5], gap[2][:, 2:6], gap[1][:, 3:7]],
-        "b3": [gap[1][:, 3:7], gap[1][:, 2:6], gap[2][:, 1:5], gap[3][:, 0:4]],
+        "a0": [from_k(1, 0), from_k(2, 0), from_k(3, 0)],
+        "a1": [from_k(1, 0), from_k(1, 1), from_k(2, 1), from_k(3, 1)],
+        "b4": [from_k(3, 1), from_k(2, 2), from_k(1, 3)],
+        "b3": [from_k(1, 3), from_k(1, 2), from_k(2, 1), from_k(3, 0)],
     }
     inverse = {}
     for key in ("a0", "a1", "b4", "b3"):
-        product = const.tile([P, PACK], F32, name="product_" + key)
+        product = const.tile([P, KNOTS], F32, name="product_" + key)
         nc.vector.tensor_mul(out=product[:], in0=factors[key][0], in1=factors[key][1])
         for factor in factors[key][2:]:
             nc.vector.tensor_mul(out=product[:], in0=product[:], in1=factor)
-        inverse[key] = const.tile([P, PACK], F32, name="inverse_" + key)
+        inverse[key] = const.tile([P, KNOTS], F32, name="inverse_" + key)
         nc.vector.reciprocal(out=inverse[key][:], in_=product[:])
 
-    a1 = const.tile([P, PACK], F32)
+    a1 = const.tile([P, KNOTS], F32)
     nc.vector.tensor_mul(out=a1[:], in0=inverse["a1"][:], in1=gap[4][:])
-    neg_b3 = const.tile([P, PACK], F32)
+    neg_b3 = const.tile([P, KNOTS], F32)
     nc.vector.scalar_tensor_tensor(
         out=neg_b3[:], in0=inverse["b3"][:], scalar=-1.0, in1=gap[4][:], op0=ALU.mult, op1=ALU.mult
     )
-    neg_b4 = const.tile([P, PACK], F32)
+    neg_b4 = const.tile([P, KNOTS], F32)
     nc.vector.tensor_scalar_mul(out=neg_b4[:], in0=inverse["b4"][:], scalar1=-1.0)
     return {"knot": knot, "neg_knot": neg_knot, "a0": inverse["a0"], "a1": a1, "neg_b3": neg_b3, "neg_b4": neg_b4}
 
 
 def quantise_coefficients(nc, const, transposed, identity, spline_coeffs):
     halves = OUTS // P
-    per_pass = FEATURES_PER_PASS * KNOTS
     natural = const.tile([P, halves, FEATURES * KNOTS], BF16)
     for h in range(halves):
         nc.sync.dma_start(
@@ -134,103 +121,100 @@ def tile_kanlayer_t_kernel(tc, x, spline_coeffs, spline_knots, out):
     nc = tc.nc
     with ExitStack() as ctx:
         const = ctx.enter_context(tc.tile_pool(name="const", bufs=1))
+        cube_pool = ctx.enter_context(tc.tile_pool(name="cubes", bufs=8))
+        plane_pool = ctx.enter_context(tc.tile_pool(name="planes", bufs=3))
         work = ctx.enter_context(tc.tile_pool(name="work", bufs=2))
-        transposed = ctx.enter_context(tc.psum_pool(name="transposed", bufs=2))
-        sums = ctx.enter_context(tc.psum_pool(name="sums", bufs=4))
+        transposed = ctx.enter_context(tc.psum_pool(name="transposed", bufs=4))
+        sums = ctx.enter_context(tc.psum_pool(name="sums", bufs=3))
 
         identity = const.tile([P, P], BF16)
         make_identity(nc, identity[:])
 
         x_rows = const.tile([P, ROW_TILES, FEATURES], BF16)
         nc.sync.dma_start(out=x_rows[:], in_=x.rearrange("(m a) i -> m a i", a=ROW_TILES))
+        x_planes = const.tile([P, FEATURES, ROW_TILES], BF16)
+        nc.vector.tensor_copy(out=x_planes[:], in_=x_rows[:].rearrange("m a i -> m i a"))
         out_rows = out.rearrange("(m a) o -> m a o", a=ROW_TILES)
 
-        scalars = load_knot_scalars(nc, const, identity, spline_knots)
+        scalars = load_knot_scalars(nc, const, spline_knots)
         w_codes, w_scales = quantise_coefficients(nc, const, transposed, identity, spline_coeffs)
 
-        for chunk in range(CHUNKS):
+        def column(name, index):
+            return scalars[name][:, index : index + 1]
+
+        def open_chunk(chunk):
             first = chunk * TILES_PER_CHUNK
+            rows = work.tile([P, FEATURES, WORDS_PER_FEATURE, PACK, TILES_PER_CHUNK], BF16, name="rows")
+            return {"first": first, "x": x_planes[:, :, first : first + TILES_PER_CHUNK], "rows": rows, "cube": {}}
 
-            repeated = work.tile([P, TILES_PER_CHUNK * FEATURES, WORDS_PER_FEATURE], BF16)
-            nc.scalar.copy(
-                out=repeated[:],
-                in_=x_rows[:, first : first + TILES_PER_CHUNK, :]
-                .rearrange("m a i -> m (a i)")
-                .unsqueeze(2)
-                .to_broadcast([P, TILES_PER_CHUNK * FEATURES, WORDS_PER_FEATURE]),
-            )
-            blocks = repeated[:].rearrange("m (n f) r -> m n (f r)", f=FEATURES_PER_PASS)
-            x_flipped = transposed.tile([P, COLS], BF16, tag="transposed")
-            for n in range(TILES_PER_CHUNK * PASSES):
-                nc.tensor.transpose(x_flipped[:, P * n : P * n + P], blocks[:, n, :], identity[:])
-            x_cols = work.tile([P, COLS], BF16)
-            nc.scalar.copy(out=x_cols[:], in_=x_flipped[:])
-
-            cube = work.tile([P, CUBES, COLS], F32)
-            for j in range(CUBES):
-                nc.scalar.activation(
-                    out=cube[:, j, :], in_=x_cols[:], func=ACT.Square, bias=scalars["neg_knot"][:, j : j + 1]
-                )
-            for j in range(CUBES):
-                nc.vector.scalar_tensor_tensor(
-                    out=cube[:, j, :],
-                    in0=x_cols[:],
-                    scalar=scalars["knot"][:, j : j + 1],
-                    in1=cube[:, j, :],
-                    op0=ALU.subtract,
-                    op1=ALU.mult,
-                )
-
-            left = work.tile([P, PACK, COLS], F32)
-            right = work.tile([P, PACK, COLS], F32)
-            for w in range(PACK):
-                nc.scalar.activation(
-                    out=left[:, w, :], in_=cube[:, w + 1, :], func=ACT.Relu, scale=scalars["a1"][:, w : w + 1]
-                )
-                nc.scalar.activation(
-                    out=right[:, w, :], in_=cube[:, w + 3, :], func=ACT.Relu, scale=scalars["neg_b3"][:, w : w + 1]
-                )
-            for w in range(PACK):
-                nc.vector.scalar_tensor_tensor(
-                    out=left[:, w, :],
-                    in0=cube[:, w, :],
-                    scalar=scalars["a0"][:, w : w + 1],
-                    in1=left[:, w, :],
-                    op0=ALU.mult,
-                    op1=ALU.subtract,
-                )
-                nc.vector.scalar_tensor_tensor(
-                    out=right[:, w, :],
-                    in0=cube[:, w + 4, :],
-                    scalar=scalars["neg_b4"][:, w : w + 1],
-                    in1=right[:, w, :],
-                    op0=ALU.mult,
-                    op1=ALU.subtract,
-                )
-
-            basis = work.tile([P, COLS, PACK], BF16, align_bytes=64)
+        def add_knot(state, j):
+            cube = state["cube"]
+            cube[j] = cube_pool.tile([P, FEATURES, TILES_PER_CHUNK], F32, name="cube", tag="cube")
+            nc.scalar.activation(out=cube[j][:], in_=state["x"], func=ACT.Square, bias=column("neg_knot", j))
             nc.vector.scalar_tensor_tensor(
-                out=basis[:],
-                in0=left[:].rearrange("p w c -> p c w"),
-                scalar=0.0,
-                in1=right[:].rearrange("p w c -> p c w"),
-                op0=ALU.max,
-                op1=ALU.max,
+                out=cube[j][:], in0=state["x"], scalar=column("knot", j), in1=cube[j][:],
+                op0=ALU.subtract, op1=ALU.mult,
             )
-            codes = work.tile([P, COLS], U32, align_bytes=64)
-            scales = work.tile([P, COLS], U8, align_bytes=64)
-            nc.vector.quantize_mx(
-                out=codes[:].bitcast(FP8X4), scales=scales[:], in_=basis[:].rearrange("p c w -> p (c w)")
+            k = j - DEGREE - 1
+            if k < 0:
+                return
+            inner_left = plane_pool.tile([P, FEATURES, TILES_PER_CHUNK], F32, name="inner_left")
+            inner_right = plane_pool.tile([P, FEATURES, TILES_PER_CHUNK], F32, name="inner_right")
+            if k % VECTOR_TAKES_EVERY == 0:
+                nc.vector.tensor_scalar(
+                    out=inner_left[:], in0=cube[k + 1][:], scalar1=column("a1", k), scalar2=0.0,
+                    op0=ALU.mult, op1=ALU.max,
+                )
+            else:
+                nc.scalar.activation(out=inner_left[:], in_=cube[k + 1][:], func=ACT.Relu, scale=column("a1", k))
+            nc.scalar.activation(out=inner_right[:], in_=cube[k + 3][:], func=ACT.Relu, scale=column("neg_b3", k))
+            left = plane_pool.tile([P, FEATURES, TILES_PER_CHUNK], BF16, name="left")
+            right = plane_pool.tile([P, FEATURES, TILES_PER_CHUNK], BF16, name="right")
+            nc.vector.scalar_tensor_tensor(
+                out=left[:], in0=cube[k][:], scalar=column("a0", k), in1=inner_left[:],
+                op0=ALU.mult, op1=ALU.subtract,
+            )
+            nc.vector.scalar_tensor_tensor(
+                out=right[:], in0=cube[k + 4][:], scalar=column("neg_b4", k), in1=inner_right[:],
+                op0=ALU.mult, op1=ALU.subtract,
+            )
+            nc.vector.tensor_tensor(
+                out=state["rows"][:, :, k // PACK, k % PACK, :], in0=left[:], in1=right[:], op=ALU.max
             )
 
-            result = work.tile([P, TILES_PER_CHUNK, OUTS], F32)
-            for pair in range(TILES_PER_CHUNK // 2):
-                acc = sums.tile([P, 2, OUTS], F32)
-                for s in range(2):
+        def finish_row_tile(state, a):
+            s = a % TILES_PER_GROUP
+            if s == 0:
+                state["basis"] = work.tile([P, TILES_PER_GROUP, PASSES, P, PACK], BF16, align_bytes=64, name="basis")
+            basis = state["basis"]
+            flipped = transposed.tile([P, PASSES, PACK, P], BF16, tag="transposed", name="flipped")
+            for g in range(PASSES):
+                for w in range(PACK):
+                    nc.tensor.transpose(
+                        flipped[:, g, w, :],
+                        state["rows"][:, FEATURES_PER_PASS * g : FEATURES_PER_PASS * (g + 1), :, w, a].rearrange(
+                            "m f r -> m (f r)"
+                        ),
+                        identity[:],
+                    )
+            nc.scalar.activation(
+                out=basis[:, s, :, :, :], in_=flipped[:].rearrange("p g w m -> p g m w"), func=ACT.Relu
+            )
+            if s < TILES_PER_GROUP - 1:
+                return
+            codes = work.tile([P, GROUP_COLS], U32, align_bytes=64, name="codes")
+            scales = work.tile([P, GROUP_COLS], U8, align_bytes=64, name="scales")
+            nc.vector.quantize_mx(
+                out=codes[:].bitcast(FP8X4), scales=scales[:], in_=basis[:].rearrange("p s g m w -> p (s g m w)")
+            )
+            result = work.tile([P, TILES_PER_GROUP, OUTS], F32, name="result")
+            for pair in range(TILES_PER_GROUP // 2):
+                acc = sums.tile([P, 2, OUTS], F32, name="acc")
+                for half in range(2):
                     for g in range(PASSES):
-                        n = (2 * pair + s) * PASSES + g
+                        n = (2 * pair + half) * PASSES + g
                         nc.tensor.matmul_mx(
-                            out=acc[:, s, :],
+                            out=acc[:, half, :],
                             lhsT=codes[:, P * n : P * n + P].bitcast(FP8X4),
                             lhsT_scale=scales[:, P * n : P * n + P],
                             rhs=w_codes[:, g, :].bitcast(FP8X4),
@@ -239,4 +223,15 @@ def tile_kanlayer_t_kernel(tc, x, spline_coeffs, spline_knots, out):
                             stop=(g == PASSES - 1),
                         )
                 nc.scalar.copy(out=result[:, 2 * pair : 2 * pair + 2, :], in_=acc[:])
-            nc.sync.dma_start(out=out_rows[:, first : first + TILES_PER_CHUNK, :], in_=result[:])
+            tile0 = state["first"] + a - s
+            nc.sync.dma_start(out=out_rows[:, tile0 : tile0 + TILES_PER_GROUP, :], in_=result[:])
+
+        finished = None
+        for step in range(CHUNKS + 1):
+            current = open_chunk(step) if step < CHUNKS else None
+            for j in range(ALL_KNOTS):
+                if current is not None:
+                    add_knot(current, j)
+                if finished is not None and j % KNOTS_PER_ROW_TILE == 0 and j // KNOTS_PER_ROW_TILE < TILES_PER_CHUNK:
+                    finish_row_tile(finished, j // KNOTS_PER_ROW_TILE)
+            finished = current

@@ -145,7 +145,16 @@ def tile_kanlayer_t_kernel(tc, x, spline_coeffs, spline_knots, out):
         def open_chunk(chunk):
             first = chunk * TILES_PER_CHUNK
             rows = work.tile([P, FEATURES, WORDS_PER_FEATURE, PACK, TILES_PER_CHUNK], BF16, name="rows")
-            return {"first": first, "x": x_planes[:, :, first : first + TILES_PER_CHUNK], "rows": rows, "cube": {}}
+            return {"first": first, "x": x_planes[:, :, first : first + TILES_PER_CHUNK], "rows": rows, "cube": {}, "sides": None}
+
+        def pick_larger(state):
+            if state["sides"] is None:
+                return
+            k, left, right = state["sides"]
+            nc.vector.tensor_tensor(
+                out=state["rows"][:, :, k // PACK, k % PACK, :], in0=left[:], in1=right[:], op=ALU.max
+            )
+            state["sides"] = None
 
         def add_knot(state, j):
             cube = state["cube"]
@@ -155,6 +164,7 @@ def tile_kanlayer_t_kernel(tc, x, spline_coeffs, spline_knots, out):
                 out=cube[j][:], in0=state["x"], scalar=column("knot", j), in1=cube[j][:],
                 op0=ALU.subtract, op1=ALU.mult,
             )
+            pick_larger(state)
             k = j - DEGREE - 1
             if k < 0:
                 return
@@ -178,9 +188,7 @@ def tile_kanlayer_t_kernel(tc, x, spline_coeffs, spline_knots, out):
                 out=right[:], in0=cube[k + 4][:], scalar=column("neg_b4", k), in1=inner_right[:],
                 op0=ALU.mult, op1=ALU.subtract,
             )
-            nc.vector.tensor_tensor(
-                out=state["rows"][:, :, k // PACK, k % PACK, :], in0=left[:], in1=right[:], op=ALU.max
-            )
+            state["sides"] = (k, left, right)
 
         def finish_row_tile(state, a):
             s = a % TILES_PER_GROUP
@@ -234,4 +242,6 @@ def tile_kanlayer_t_kernel(tc, x, spline_coeffs, spline_knots, out):
                     add_knot(current, j)
                 if finished is not None and j % KNOTS_PER_ROW_TILE == 0 and j // KNOTS_PER_ROW_TILE < TILES_PER_CHUNK:
                     finish_row_tile(finished, j // KNOTS_PER_ROW_TILE)
+            if current is not None:
+                pick_larger(current)
             finished = current

@@ -23,12 +23,11 @@ PASSES = 2
 FEATURES_PER_PASS = FEATURES // PASSES
 WORDS_PER_FEATURE = KNOTS // PACK
 ROW_TILES = ROWS // P
-TILES_PER_CHUNK = 16
-CHUNKS = ROW_TILES // TILES_PER_CHUNK
+CHUNK_TILES = (24, 24, 16)
+PREPARE_AT = 12
+VECTOR_INNER = (0, 15, 27)
 TILES_PER_GROUP = 4
 GROUP_COLS = TILES_PER_GROUP * PASSES * P
-KNOTS_PER_ROW_TILE = 2
-VECTOR_TAKES_EVERY = 4
 
 FLOPS = 2 * ROWS * FEATURES * KNOTS * OUTS
 
@@ -86,7 +85,7 @@ def load_knot_scalars(nc, const, spline_knots):
     return {"knot": knot, "neg_knot": neg_knot, "a0": inverse["a0"], "a1": a1, "neg_b3": neg_b3, "neg_b4": neg_b4}
 
 
-def quantise_coefficients(nc, const, transposed, identity, spline_coeffs):
+def load_coefficients(nc, const, spline_coeffs):
     halves = OUTS // P
     natural = const.tile([P, halves, FEATURES * KNOTS], BF16)
     for h in range(halves):
@@ -94,25 +93,30 @@ def quantise_coefficients(nc, const, transposed, identity, spline_coeffs):
             out=natural[:, h, :].rearrange("q (i k) -> q i k", k=KNOTS),
             in_=spline_coeffs[:, P * h : P * h + P, :].rearrange("i q k -> q i k"),
         )
-    sorted_w = const.tile([P, halves, PASSES, PACK, P], BF16)
-    for h in range(halves):
-        nc.vector.tensor_copy(
-            out=sorted_w[:, h, :, :, :],
-            in_=natural[:, h, :].rearrange("q (g p w) -> q g w p", g=PASSES, w=PACK),
-        )
     grouped = const.tile([P, PASSES, OUTS, PACK], BF16, align_bytes=64)
-    for g in range(PASSES):
-        flipped = transposed.tile([P, PACK, OUTS], BF16, tag="transposed")
-        for w in range(PACK):
-            for h in range(halves):
-                nc.tensor.transpose(flipped[:, w, P * h : P * h + P], sorted_w[:, h, g, w, :], identity[:])
-        nc.vector.tensor_copy(out=grouped[:, g, :, :], in_=flipped[:].rearrange("p w o -> p o w"))
+    return {"natural": natural, "grouped": grouped}
+
+
+def turn_coefficients(nc, transposed, identity, coefficients, g):
+    halves = OUTS // P
+    flipped = transposed.tile([P, PACK, OUTS], BF16, tag="transposed", name="flipped_w")
+    for w in range(PACK):
+        for h in range(halves):
+            nc.tensor.transpose(
+                flipped[:, w, P * h : P * h + P],
+                coefficients["natural"][:, h, :].rearrange("q (g p w) -> q g w p", g=PASSES, w=PACK)[:, g, w, :],
+                identity[:],
+            )
+    nc.scalar.copy(out=coefficients["grouped"][:, g, :, :], in_=flipped[:].rearrange("p w o -> p o w"))
+
+
+def quantise_coefficients(nc, const, coefficients):
     codes = const.tile([P, PASSES, OUTS], U32, align_bytes=64)
     scales = const.tile([P, PASSES, OUTS], U8, align_bytes=64)
     nc.vector.quantize_mx(
         out=codes[:].rearrange("p g o -> p (g o)").bitcast(FP8X4),
         scales=scales[:].rearrange("p g o -> p (g o)"),
-        in_=grouped[:].rearrange("p g o w -> p (g o w)"),
+        in_=coefficients["grouped"][:].rearrange("p g o w -> p (g o w)"),
     )
     return codes, scales
 
@@ -130,22 +134,32 @@ def tile_kanlayer_t_kernel(tc, x, spline_coeffs, spline_knots, out):
         identity = const.tile([P, P], BF16)
         make_identity(nc, identity[:])
 
-        x_rows = const.tile([P, ROW_TILES, FEATURES], BF16)
-        nc.sync.dma_start(out=x_rows[:], in_=x.rearrange("(m a) i -> m a i", a=ROW_TILES))
-        x_planes = const.tile([P, FEATURES, ROW_TILES], BF16)
-        nc.vector.tensor_copy(out=x_planes[:], in_=x_rows[:].rearrange("m a i -> m i a"))
-        out_rows = out.rearrange("(m a) o -> m a o", a=ROW_TILES)
-
         scalars = load_knot_scalars(nc, const, spline_knots)
-        w_codes, w_scales = quantise_coefficients(nc, const, transposed, identity, spline_coeffs)
+        x_by_rows = x.rearrange("(m a) i -> m a i", a=ROW_TILES)
+        x_rows = []
+        x_planes = []
+        for chunk in range(len(CHUNK_TILES)):
+            first = sum(CHUNK_TILES[:chunk])
+            tiles = CHUNK_TILES[chunk]
+            x_rows.append(const.tile([P, tiles, FEATURES], BF16, name="x_rows%d" % chunk))
+            nc.sync.dma_start(out=x_rows[chunk][:], in_=x_by_rows[:, first : first + tiles, :])
+            x_planes.append(const.tile([P, FEATURES, tiles], BF16, name="x_planes%d" % chunk))
+        nc.vector.tensor_copy(out=x_planes[0][:], in_=x_rows[0][:].rearrange("m a i -> m i a"))
+        out_rows = out.rearrange("(m a) o -> m a o", a=ROW_TILES)
+        coefficients = load_coefficients(nc, const, spline_coeffs)
+        weights = {}
 
         def column(name, index):
             return scalars[name][:, index : index + 1]
 
         def open_chunk(chunk):
-            first = chunk * TILES_PER_CHUNK
-            rows = work.tile([P, FEATURES, WORDS_PER_FEATURE, PACK, TILES_PER_CHUNK], BF16, name="rows")
-            return {"first": first, "x": x_planes[:, :, first : first + TILES_PER_CHUNK], "rows": rows, "cube": {}, "sides": None}
+            first = sum(CHUNK_TILES[:chunk])
+            tiles = CHUNK_TILES[chunk]
+            rows = work.tile([P, FEATURES, WORDS_PER_FEATURE, PACK, tiles], BF16, name="rows")
+            return {
+                "first": first, "tiles": tiles, "x": x_planes[chunk][:], "rows": rows, "cube": {},
+                "sides": None, "vector_inner": VECTOR_INNER[chunk],
+            }
 
         def pick_larger(state):
             if state["sides"] is None:
@@ -158,7 +172,7 @@ def tile_kanlayer_t_kernel(tc, x, spline_coeffs, spline_knots, out):
 
         def add_knot(state, j):
             cube = state["cube"]
-            cube[j] = cube_pool.tile([P, FEATURES, TILES_PER_CHUNK], F32, name="cube", tag="cube")
+            cube[j] = cube_pool.tile([P, FEATURES, state["tiles"]], F32, name="cube", tag="cube")
             nc.scalar.activation(out=cube[j][:], in_=state["x"], func=ACT.Square, bias=column("neg_knot", j))
             nc.vector.scalar_tensor_tensor(
                 out=cube[j][:], in0=state["x"], scalar=column("knot", j), in1=cube[j][:],
@@ -168,9 +182,9 @@ def tile_kanlayer_t_kernel(tc, x, spline_coeffs, spline_knots, out):
             k = j - DEGREE - 1
             if k < 0:
                 return
-            inner_left = plane_pool.tile([P, FEATURES, TILES_PER_CHUNK], F32, name="inner_left")
-            inner_right = plane_pool.tile([P, FEATURES, TILES_PER_CHUNK], F32, name="inner_right")
-            if k % VECTOR_TAKES_EVERY == 0:
+            inner_left = plane_pool.tile([P, FEATURES, state["tiles"]], F32, name="inner_left")
+            inner_right = plane_pool.tile([P, FEATURES, state["tiles"]], F32, name="inner_right")
+            if (k + 1) * state["vector_inner"] // KNOTS > k * state["vector_inner"] // KNOTS:
                 nc.vector.tensor_scalar(
                     out=inner_left[:], in0=cube[k + 1][:], scalar1=column("a1", k), scalar2=0.0,
                     op0=ALU.mult, op1=ALU.max,
@@ -178,8 +192,8 @@ def tile_kanlayer_t_kernel(tc, x, spline_coeffs, spline_knots, out):
             else:
                 nc.scalar.activation(out=inner_left[:], in_=cube[k + 1][:], func=ACT.Relu, scale=column("a1", k))
             nc.scalar.activation(out=inner_right[:], in_=cube[k + 3][:], func=ACT.Relu, scale=column("neg_b3", k))
-            left = plane_pool.tile([P, FEATURES, TILES_PER_CHUNK], BF16, name="left")
-            right = plane_pool.tile([P, FEATURES, TILES_PER_CHUNK], BF16, name="right")
+            left = plane_pool.tile([P, FEATURES, state["tiles"]], BF16, name="left")
+            right = plane_pool.tile([P, FEATURES, state["tiles"]], BF16, name="right")
             nc.vector.scalar_tensor_tensor(
                 out=left[:], in0=cube[k][:], scalar=column("a0", k), in1=inner_left[:],
                 op0=ALU.mult, op1=ALU.subtract,
@@ -190,7 +204,7 @@ def tile_kanlayer_t_kernel(tc, x, spline_coeffs, spline_knots, out):
             )
             state["sides"] = (k, left, right)
 
-        def finish_row_tile(state, a):
+        def finish_row_tile(state, a, planes_done):
             s = a % TILES_PER_GROUP
             if s == 0:
                 state["basis"] = work.tile([P, TILES_PER_GROUP, PASSES, P, PACK], BF16, align_bytes=64, name="basis")
@@ -205,9 +219,14 @@ def tile_kanlayer_t_kernel(tc, x, spline_coeffs, spline_knots, out):
                         ),
                         identity[:],
                     )
-            nc.scalar.activation(
-                out=basis[:, s, :, :, :], in_=flipped[:].rearrange("p g w m -> p g m w"), func=ACT.Relu
-            )
+            if planes_done and a % 2 == 1:
+                nc.vector.tensor_scalar_max(
+                    out=basis[:, s, :, :, :], in0=flipped[:].rearrange("p g w m -> p g m w"), scalar1=0.0
+                )
+            else:
+                nc.scalar.activation(
+                    out=basis[:, s, :, :, :], in_=flipped[:].rearrange("p g w m -> p g m w"), func=ACT.Relu
+                )
             if s < TILES_PER_GROUP - 1:
                 return
             codes = work.tile([P, GROUP_COLS], U32, align_bytes=64, name="codes")
@@ -225,23 +244,35 @@ def tile_kanlayer_t_kernel(tc, x, spline_coeffs, spline_knots, out):
                             out=acc[:, half, :],
                             lhsT=codes[:, P * n : P * n + P].bitcast(FP8X4),
                             lhsT_scale=scales[:, P * n : P * n + P],
-                            rhs=w_codes[:, g, :].bitcast(FP8X4),
-                            rhs_scale=w_scales[:, g, :],
+                            rhs=weights["codes"][:, g, :].bitcast(FP8X4),
+                            rhs_scale=weights["scales"][:, g, :],
                             start=(g == 0),
                             stop=(g == PASSES - 1),
                         )
-                nc.scalar.copy(out=result[:, 2 * pair : 2 * pair + 2, :], in_=acc[:])
+                if planes_done and pair % 2 == 1:
+                    nc.vector.tensor_copy(out=result[:, 2 * pair : 2 * pair + 2, :], in_=acc[:])
+                else:
+                    nc.scalar.copy(out=result[:, 2 * pair : 2 * pair + 2, :], in_=acc[:])
             tile0 = state["first"] + a - s
             nc.sync.dma_start(out=out_rows[:, tile0 : tile0 + TILES_PER_GROUP, :], in_=result[:])
 
         finished = None
-        for step in range(CHUNKS + 1):
-            current = open_chunk(step) if step < CHUNKS else None
+        for step in range(len(CHUNK_TILES) + 1):
+            current = open_chunk(step) if step < len(CHUNK_TILES) else None
+            done = 0
             for j in range(ALL_KNOTS):
                 if current is not None:
                     add_knot(current, j)
-                if finished is not None and j % KNOTS_PER_ROW_TILE == 0 and j // KNOTS_PER_ROW_TILE < TILES_PER_CHUNK:
-                    finish_row_tile(finished, j // KNOTS_PER_ROW_TILE)
+                if j == PREPARE_AT and step + 1 < len(CHUNK_TILES):
+                    nc.scalar.copy(out=x_planes[step + 1][:], in_=x_rows[step + 1][:].rearrange("m a i -> m i a"))
+                if step == 0 and j in (PREPARE_AT + 4, PREPARE_AT + 8):
+                    turn_coefficients(nc, transposed, identity, coefficients, (j - PREPARE_AT) // 4 - 1)
+                if step == 0 and j == PREPARE_AT + 12:
+                    weights["codes"], weights["scales"] = quantise_coefficients(nc, const, coefficients)
+                if finished is not None:
+                    while done * ALL_KNOTS < (j + 1) * finished["tiles"]:
+                        finish_row_tile(finished, done, current is None)
+                        done += 1
             if current is not None:
                 pick_larger(current)
             finished = current

@@ -25,7 +25,7 @@ WORDS_PER_FEATURE = KNOTS // PACK
 ROW_TILES = ROWS // P
 CHUNK_TILES = (24, 24, 16)
 PREPARE_AT = 12
-VECTOR_INNER = (0, 15, 27)
+VECTOR_INNER = (0, 8, 20)
 TILES_PER_GROUP = 4
 GROUP_COLS = TILES_PER_GROUP * PASSES * P
 
@@ -125,8 +125,8 @@ def tile_kanlayer_t_kernel(tc, x, spline_coeffs, spline_knots, out):
     nc = tc.nc
     with ExitStack() as ctx:
         const = ctx.enter_context(tc.tile_pool(name="const", bufs=1))
-        cube_pool = ctx.enter_context(tc.tile_pool(name="cubes", bufs=8))
-        plane_pool = ctx.enter_context(tc.tile_pool(name="planes", bufs=3))
+        cube_pool = ctx.enter_context(tc.tile_pool(name="cubes", bufs=10))
+        plane_pool = ctx.enter_context(tc.tile_pool(name="planes", bufs=4))
         work = ctx.enter_context(tc.tile_pool(name="work", bufs=2))
         transposed = ctx.enter_context(tc.psum_pool(name="transposed", bufs=4))
         sums = ctx.enter_context(tc.psum_pool(name="sums", bufs=3))
@@ -219,7 +219,7 @@ def tile_kanlayer_t_kernel(tc, x, spline_coeffs, spline_knots, out):
                         ),
                         identity[:],
                     )
-            if planes_done and a % 2 == 1:
+            if planes_done and s == 1:
                 nc.vector.tensor_scalar_max(
                     out=basis[:, s, :, :, :], in0=flipped[:].rearrange("p g w m -> p g m w"), scalar1=0.0
                 )
@@ -249,7 +249,7 @@ def tile_kanlayer_t_kernel(tc, x, spline_coeffs, spline_knots, out):
                             start=(g == 0),
                             stop=(g == PASSES - 1),
                         )
-                if planes_done and pair % 2 == 1:
+                if planes_done:
                     nc.vector.tensor_copy(out=result[:, 2 * pair : 2 * pair + 2, :], in_=acc[:])
                 else:
                     nc.scalar.copy(out=result[:, 2 * pair : 2 * pair + 2, :], in_=acc[:])

@@ -133,6 +133,8 @@ def tile_kanlayer_t_kernel(tc, x, spline_coeffs, spline_knots, out):
 
         identity = const.tile([P, P], BF16)
         make_identity(nc, identity[:])
+        identity_f32 = const.tile([P, P], F32)
+        make_identity(nc, identity_f32[:])
 
         scalars = load_knot_scalars(nc, const, spline_knots)
         x_by_rows = x.rearrange("(m a) i -> m a i", a=ROW_TILES)
@@ -204,29 +206,31 @@ def tile_kanlayer_t_kernel(tc, x, spline_coeffs, spline_knots, out):
             )
             state["sides"] = (k, left, right)
 
-        def finish_row_tile(state, a, planes_done):
+        def finish_row_tiles(state, a, planes_done):
             s = a % TILES_PER_GROUP
             if s == 0:
                 state["basis"] = work.tile([P, TILES_PER_GROUP, PASSES, P, PACK], BF16, align_bytes=64, name="basis")
             basis = state["basis"]
-            flipped = transposed.tile([P, PASSES, PACK, P], BF16, tag="transposed", name="flipped")
+            words = state["rows"][:].bitcast(F32)
             for g in range(PASSES):
+                flipped = transposed.tile([P, PACK, P], F32, tag="transposed", name="flipped")
                 for w in range(PACK):
                     nc.tensor.transpose(
-                        flipped[:, g, w, :],
-                        state["rows"][:, FEATURES_PER_PASS * g : FEATURES_PER_PASS * (g + 1), :, w, a].rearrange(
+                        flipped[:, w, :],
+                        words[:, FEATURES_PER_PASS * g : FEATURES_PER_PASS * (g + 1), :, w, a // 2].rearrange(
                             "m f r -> m (f r)"
                         ),
-                        identity[:],
+                        identity_f32[:],
                     )
-            if planes_done and s == 1:
-                nc.vector.tensor_scalar_max(
-                    out=basis[:, s, :, :, :], in0=flipped[:].rearrange("p g w m -> p g m w"), scalar1=0.0
+                halves = flipped[:].rearrange("p w m -> p (w m)").bitcast(BF16).rearrange(
+                    "p (w m e) -> p e m w", w=PACK, e=2
                 )
-            else:
-                nc.scalar.activation(
-                    out=basis[:, s, :, :, :], in_=flipped[:].rearrange("p g w m -> p g m w"), func=ACT.Relu
-                )
+                if planes_done and s == 0 and g == 1:
+                    nc.vector.tensor_scalar_max(out=basis[:, s : s + 2, g, :, :], in0=halves, scalar1=0.0)
+                else:
+                    nc.scalar.activation(out=basis[:, s : s + 2, g, :, :], in_=halves, func=ACT.Relu)
+            s += 1
+            a += 1
             if s < TILES_PER_GROUP - 1:
                 return
             codes = work.tile([P, GROUP_COLS], U32, align_bytes=64, name="codes")
@@ -271,8 +275,8 @@ def tile_kanlayer_t_kernel(tc, x, spline_coeffs, spline_knots, out):
                     weights["codes"], weights["scales"] = quantise_coefficients(nc, const, coefficients)
                 if finished is not None:
                     while done * ALL_KNOTS < (j + 1) * finished["tiles"]:
-                        finish_row_tile(finished, done, current is None)
-                        done += 1
+                        finish_row_tiles(finished, done, current is None)
+                        done += 2
             if current is not None:
                 pick_larger(current)
             finished = current

@@ -206,7 +206,9 @@ def tile_kanlayer_t_kernel(tc, x, spline_coeffs, spline_knots, out):
             )
             state["sides"] = (k, left, right)
 
-        def finish_row_tiles(state, a, planes_done):
+        later = []
+
+        def finish_row_tiles(state, a, planes_done, now):
             s = a % TILES_PER_GROUP
             if s == 0:
                 state["basis"] = work.tile([P, TILES_PER_GROUP, PASSES, P, PACK], BF16, align_bytes=64, name="basis")
@@ -229,44 +231,60 @@ def tile_kanlayer_t_kernel(tc, x, spline_coeffs, spline_knots, out):
                     nc.vector.tensor_scalar_max(out=basis[:, s : s + 2, g, :, :], in0=halves, scalar1=0.0)
                 else:
                     nc.scalar.activation(out=basis[:, s : s + 2, g, :, :], in_=halves, func=ACT.Relu)
-            s += 1
-            a += 1
-            if s < TILES_PER_GROUP - 1:
+            if s + 2 < TILES_PER_GROUP:
                 return
-            codes = work.tile([P, GROUP_COLS], U32, align_bytes=64, name="codes")
-            scales = work.tile([P, GROUP_COLS], U8, align_bytes=64, name="scales")
+            group = {"basis": basis, "tile0": state["first"] + a - s, "planes_done": planes_done}
+            later.append((now + 1, quantise_group, group))
+            later.append((now + 2, multiply_group, group))
+            later.append((now + 3, store_group, group))
+
+        def quantise_group(group):
+            group["codes"] = work.tile([P, GROUP_COLS], U32, align_bytes=64, name="codes")
+            group["scales"] = work.tile([P, GROUP_COLS], U8, align_bytes=64, name="scales")
             nc.vector.quantize_mx(
-                out=codes[:].bitcast(FP8X4), scales=scales[:], in_=basis[:].rearrange("p s g m w -> p (s g m w)")
+                out=group["codes"][:].bitcast(FP8X4), scales=group["scales"][:],
+                in_=group["basis"][:].rearrange("p s g m w -> p (s g m w)"),
             )
-            result = work.tile([P, TILES_PER_GROUP, OUTS], F32, name="result")
+
+        def multiply_group(group):
+            group["acc"] = []
             for pair in range(TILES_PER_GROUP // 2):
                 acc = sums.tile([P, 2, OUTS], F32, name="acc")
+                group["acc"].append(acc)
                 for half in range(2):
                     for g in range(PASSES):
                         n = (2 * pair + half) * PASSES + g
                         nc.tensor.matmul_mx(
                             out=acc[:, half, :],
-                            lhsT=codes[:, P * n : P * n + P].bitcast(FP8X4),
-                            lhsT_scale=scales[:, P * n : P * n + P],
+                            lhsT=group["codes"][:, P * n : P * n + P].bitcast(FP8X4),
+                            lhsT_scale=group["scales"][:, P * n : P * n + P],
                             rhs=weights["codes"][:, g, :].bitcast(FP8X4),
                             rhs_scale=weights["scales"][:, g, :],
                             start=(g == 0),
                             stop=(g == PASSES - 1),
                         )
-                if planes_done:
-                    nc.vector.tensor_copy(out=result[:, 2 * pair : 2 * pair + 2, :], in_=acc[:])
+
+        def store_group(group):
+            result = work.tile([P, TILES_PER_GROUP, OUTS], F32, name="result")
+            for pair in range(TILES_PER_GROUP // 2):
+                if group["planes_done"]:
+                    nc.vector.tensor_copy(out=result[:, 2 * pair : 2 * pair + 2, :], in_=group["acc"][pair][:])
                 else:
-                    nc.scalar.copy(out=result[:, 2 * pair : 2 * pair + 2, :], in_=acc[:])
-            tile0 = state["first"] + a - s
-            nc.sync.dma_start(out=out_rows[:, tile0 : tile0 + TILES_PER_GROUP, :], in_=result[:])
+                    nc.scalar.copy(out=result[:, 2 * pair : 2 * pair + 2, :], in_=group["acc"][pair][:])
+            nc.sync.dma_start(out=out_rows[:, group["tile0"] : group["tile0"] + TILES_PER_GROUP, :], in_=result[:])
+
+        def run_later(now):
+            for entry in later:
+                if entry[0] == now:
+                    entry[1](entry[2])
 
         finished = None
-        for step in range(len(CHUNK_TILES) + 1):
-            current = open_chunk(step) if step < len(CHUNK_TILES) else None
+        now = 0
+        for step in range(len(CHUNK_TILES)):
+            current = open_chunk(step)
             done = 0
             for j in range(ALL_KNOTS):
-                if current is not None:
-                    add_knot(current, j)
+                add_knot(current, j)
                 if j == PREPARE_AT and step + 1 < len(CHUNK_TILES):
                     nc.scalar.copy(out=x_planes[step + 1][:], in_=x_rows[step + 1][:].rearrange("m a i -> m i a"))
                 if step == 0 and j in (PREPARE_AT + 4, PREPARE_AT + 8):
@@ -275,8 +293,15 @@ def tile_kanlayer_t_kernel(tc, x, spline_coeffs, spline_knots, out):
                     weights["codes"], weights["scales"] = quantise_coefficients(nc, const, coefficients)
                 if finished is not None:
                     while done * ALL_KNOTS < (j + 1) * finished["tiles"]:
-                        finish_row_tiles(finished, done, current is None)
+                        finish_row_tiles(finished, done, False, now)
                         done += 2
-            if current is not None:
-                pick_larger(current)
+                run_later(now)
+                now += 1
+            pick_larger(current)
             finished = current
+        for a in range(0, finished["tiles"], 2):
+            finish_row_tiles(finished, a, True, now)
+            run_later(now)
+            now += 1
+        for tick in range(now, now + 3):
+            run_later(tick)

@@ -20,12 +20,13 @@ KNOTS = 32
 DEGREE = 3
 ALL_KNOTS = KNOTS + DEGREE + 1
 PASSES = 2
-FEATURES_PER_PASS = FEATURES // PASSES
-WORDS_PER_FEATURE = KNOTS // PACK
+CLASSES = P // KNOTS
+PAIRS = PACK // 2
+QUADS = PASSES * PAIRS * CLASSES
 ROW_TILES = ROWS // P
 CHUNK_TILES = (24, 24, 16)
 PREPARE_AT = 12
-VECTOR_INNER = (0, 8, 20)
+VECTOR_PARTS = (0, 0, 4)
 TILES_PER_GROUP = 4
 GROUP_COLS = TILES_PER_GROUP * PASSES * P
 
@@ -74,15 +75,24 @@ def load_knot_scalars(nc, const, spline_knots):
         inverse[key] = const.tile([P, KNOTS], F32, name="inverse_" + key)
         nc.vector.reciprocal(out=inverse[key][:], in_=product[:])
 
-    a1 = const.tile([P, KNOTS], F32)
-    nc.vector.tensor_mul(out=a1[:], in0=inverse["a1"][:], in1=gap[4][:])
-    neg_b3 = const.tile([P, KNOTS], F32)
+    up = const.tile([P, KNOTS + 1], F32)
+    nc.vector.tensor_copy(out=up[:, 0:1], in_=inverse["a0"][:, 0:1])
+    nc.vector.tensor_mul(out=up[:, 1 : KNOTS + 1], in0=inverse["a1"][:], in1=gap[4][:])
+    down = const.tile([P, KNOTS + 1], F32)
     nc.vector.scalar_tensor_tensor(
-        out=neg_b3[:], in0=inverse["b3"][:], scalar=-1.0, in1=gap[4][:], op0=ALU.mult, op1=ALU.mult
+        out=down[:, 0:KNOTS], in0=inverse["b3"][:], scalar=-1.0, in1=gap[4][:], op0=ALU.mult, op1=ALU.mult
     )
-    neg_b4 = const.tile([P, KNOTS], F32)
-    nc.vector.tensor_scalar_mul(out=neg_b4[:], in0=inverse["b4"][:], scalar1=-1.0)
-    return {"knot": knot, "neg_knot": neg_knot, "a0": inverse["a0"], "a1": a1, "neg_b3": neg_b3, "neg_b4": neg_b4}
+    nc.vector.tensor_scalar_mul(out=down[:, KNOTS : KNOTS + 1], in0=inverse["b4"][:, KNOTS - 1 : KNOTS], scalar1=-1.0)
+    one_over = const.tile([P, 2, KNOTS], F32)
+    nc.vector.reciprocal(out=one_over[:, 0, :], in_=up[:, 0:KNOTS])
+    nc.vector.reciprocal(out=one_over[:, 1, :], in_=down[:, 1 : KNOTS + 1])
+    first_up = const.tile([P, KNOTS], F32)
+    nc.vector.tensor_mul(out=first_up[:], in0=inverse["a0"][:], in1=one_over[:, 0, :])
+    first_down = const.tile([P, KNOTS], F32)
+    nc.vector.scalar_tensor_tensor(
+        out=first_down[:], in0=inverse["b4"][:], scalar=-1.0, in1=one_over[:, 1, :], op0=ALU.mult, op1=ALU.mult
+    )
+    return {"knot": knot, "neg_knot": neg_knot, "up": up, "down": down, "first_up": first_up, "first_down": first_down}
 
 
 def load_coefficients(nc, const, spline_coeffs):
@@ -100,14 +110,13 @@ def load_coefficients(nc, const, spline_coeffs):
 def turn_coefficients(nc, transposed, identity, coefficients, g):
     halves = OUTS // P
     flipped = transposed.tile([P, PACK, OUTS], BF16, tag="transposed", name="flipped_w")
-    for w in range(PACK):
+    for t in range(PACK):
         for h in range(halves):
+            first = (PACK * g + t) * P
             nc.tensor.transpose(
-                flipped[:, w, P * h : P * h + P],
-                coefficients["natural"][:, h, :].rearrange("q (g p w) -> q g w p", g=PASSES, w=PACK)[:, g, w, :],
-                identity[:],
+                flipped[:, t, P * h : P * h + P], coefficients["natural"][:, h, first : first + P], identity[:]
             )
-    nc.scalar.copy(out=coefficients["grouped"][:, g, :, :], in_=flipped[:].rearrange("p w o -> p o w"))
+    nc.scalar.copy(out=coefficients["grouped"][:, g, :, :], in_=flipped[:].rearrange("p t o -> p o t"))
 
 
 def quantise_coefficients(nc, const, coefficients):
@@ -116,7 +125,7 @@ def quantise_coefficients(nc, const, coefficients):
     nc.vector.quantize_mx(
         out=codes[:].rearrange("p g o -> p (g o)").bitcast(FP8X4),
         scales=scales[:].rearrange("p g o -> p (g o)"),
-        in_=coefficients["grouped"][:].rearrange("p g o w -> p (g o w)"),
+        in_=coefficients["grouped"][:].rearrange("p g o t -> p (g o t)"),
     )
     return codes, scales
 
@@ -125,8 +134,10 @@ def tile_kanlayer_t_kernel(tc, x, spline_coeffs, spline_knots, out):
     nc = tc.nc
     with ExitStack() as ctx:
         const = ctx.enter_context(tc.tile_pool(name="const", bufs=1))
-        cube_pool = ctx.enter_context(tc.tile_pool(name="cubes", bufs=10))
-        plane_pool = ctx.enter_context(tc.tile_pool(name="planes", bufs=4))
+        cube_pool = ctx.enter_context(tc.tile_pool(name="cubes", bufs=5))
+        part_pool = ctx.enter_context(tc.tile_pool(name="parts", bufs=4))
+        left_pool = ctx.enter_context(tc.tile_pool(name="lefts", bufs=7))
+        right_pool = ctx.enter_context(tc.tile_pool(name="rights", bufs=3))
         work = ctx.enter_context(tc.tile_pool(name="work", bufs=2))
         transposed = ctx.enter_context(tc.psum_pool(name="transposed", bufs=4))
         sums = ctx.enter_context(tc.psum_pool(name="sums", bufs=3))
@@ -145,8 +156,18 @@ def tile_kanlayer_t_kernel(tc, x, spline_coeffs, spline_knots, out):
             tiles = CHUNK_TILES[chunk]
             x_rows.append(const.tile([P, tiles, FEATURES], BF16, name="x_rows%d" % chunk))
             nc.sync.dma_start(out=x_rows[chunk][:], in_=x_by_rows[:, first : first + tiles, :])
-            x_planes.append(const.tile([P, FEATURES, tiles], BF16, name="x_planes%d" % chunk))
-        nc.vector.tensor_copy(out=x_planes[0][:], in_=x_rows[0][:].rearrange("m a i -> m i a"))
+            x_planes.append(const.tile([P, QUADS, tiles, 2], BF16, name="x_planes%d" % chunk))
+
+        def lay_out_x(engine_copy, chunk):
+            for gu in range(PASSES * PAIRS):
+                engine_copy(
+                    out=x_planes[chunk][:, CLASSES * gu : CLASSES * (gu + 1), :, :],
+                    in_=x_rows[chunk][:, :, 2 * CLASSES * gu : 2 * CLASSES * (gu + 1)].rearrange(
+                        "m a (e c) -> m c a e", e=2
+                    ),
+                )
+
+        lay_out_x(nc.vector.tensor_copy, 0)
         out_rows = out.rearrange("(m a) o -> m a o", a=ROW_TILES)
         coefficients = load_coefficients(nc, const, spline_coeffs)
         weights = {}
@@ -155,12 +176,13 @@ def tile_kanlayer_t_kernel(tc, x, spline_coeffs, spline_knots, out):
             return scalars[name][:, index : index + 1]
 
         def open_chunk(chunk):
-            first = sum(CHUNK_TILES[:chunk])
             tiles = CHUNK_TILES[chunk]
-            rows = work.tile([P, FEATURES, WORDS_PER_FEATURE, PACK, tiles], BF16, name="rows")
+            rows = work.tile([P, QUADS, KNOTS, 2 * tiles], BF16, name="rows")
             return {
-                "first": first, "tiles": tiles, "x": x_planes[chunk][:], "rows": rows, "cube": {},
-                "sides": None, "vector_inner": VECTOR_INNER[chunk],
+                "first": sum(CHUNK_TILES[:chunk]), "tiles": tiles, "cols": FEATURES * tiles,
+                "x": x_planes[chunk][:].rearrange("m q a e -> m (q a e)"), "rows": rows,
+                "cube": {}, "positive": {}, "negative": {}, "left": {}, "sides": None,
+                "vector_parts": VECTOR_PARTS[chunk],
             }
 
         def pick_larger(state):
@@ -168,69 +190,79 @@ def tile_kanlayer_t_kernel(tc, x, spline_coeffs, spline_knots, out):
                 return
             k, left, right = state["sides"]
             nc.vector.tensor_tensor(
-                out=state["rows"][:, :, k // PACK, k % PACK, :], in0=left[:], in1=right[:], op=ALU.max
+                out=state["rows"][:, :, k, :],
+                in0=left[:].rearrange("m (q n) -> m q n", q=QUADS),
+                in1=right[:].rearrange("m (q n) -> m q n", q=QUADS),
+                op=ALU.max,
             )
             state["sides"] = None
 
         def add_knot(state, j):
             cube = state["cube"]
-            cube[j] = cube_pool.tile([P, FEATURES, state["tiles"]], F32, name="cube", tag="cube")
-            nc.scalar.activation(out=cube[j][:], in_=state["x"], func=ACT.Square, bias=column("neg_knot", j))
-            nc.vector.scalar_tensor_tensor(
-                out=cube[j][:], in0=state["x"], scalar=column("knot", j), in1=cube[j][:],
-                op0=ALU.subtract, op1=ALU.mult,
-            )
-            pick_larger(state)
-            k = j - DEGREE - 1
-            if k < 0:
-                return
-            inner_left = plane_pool.tile([P, FEATURES, state["tiles"]], F32, name="inner_left")
-            inner_right = plane_pool.tile([P, FEATURES, state["tiles"]], F32, name="inner_right")
-            if (k + 1) * state["vector_inner"] // KNOTS > k * state["vector_inner"] // KNOTS:
-                nc.vector.tensor_scalar(
-                    out=inner_left[:], in0=cube[k + 1][:], scalar1=column("a1", k), scalar2=0.0,
-                    op0=ALU.mult, op1=ALU.max,
+            cols = state["cols"]
+            if j < ALL_KNOTS:
+                cube[j] = cube_pool.tile([P, cols], F32, name="cube")
+                nc.scalar.activation(out=cube[j][:], in_=state["x"], func=ACT.Square, bias=column("neg_knot", j))
+                nc.vector.scalar_tensor_tensor(
+                    out=cube[j][:], in0=state["x"], scalar=column("knot", j), in1=cube[j][:],
+                    op0=ALU.subtract, op1=ALU.mult,
                 )
-            else:
-                nc.scalar.activation(out=inner_left[:], in_=cube[k + 1][:], func=ACT.Relu, scale=column("a1", k))
-            nc.scalar.activation(out=inner_right[:], in_=cube[k + 3][:], func=ACT.Relu, scale=column("neg_b3", k))
-            left = plane_pool.tile([P, FEATURES, state["tiles"]], BF16, name="left")
-            right = plane_pool.tile([P, FEATURES, state["tiles"]], BF16, name="right")
-            nc.vector.scalar_tensor_tensor(
-                out=left[:], in0=cube[k][:], scalar=column("a0", k), in1=inner_left[:],
-                op0=ALU.mult, op1=ALU.subtract,
-            )
-            nc.vector.scalar_tensor_tensor(
-                out=right[:], in0=cube[k + 4][:], scalar=column("neg_b4", k), in1=inner_right[:],
-                op0=ALU.mult, op1=ALU.subtract,
-            )
-            state["sides"] = (k, left, right)
+            pick_larger(state)
+            n = j - 1
+            if 0 <= n <= KNOTS:
+                state["positive"][n] = part_pool.tile([P, cols], F32, name="positive")
+                if (n + 1) * state["vector_parts"] // (KNOTS + 1) > n * state["vector_parts"] // (KNOTS + 1):
+                    nc.vector.tensor_scalar(
+                        out=state["positive"][n][:], in0=cube[n][:], scalar1=column("up", n), scalar2=0.0,
+                        op0=ALU.mult, op1=ALU.max,
+                    )
+                else:
+                    nc.scalar.activation(out=state["positive"][n][:], in_=cube[n][:], func=ACT.Relu, scale=column("up", n))
+            if DEGREE <= n < ALL_KNOTS:
+                state["negative"][n] = part_pool.tile([P, cols], F32, name="negative")
+                nc.scalar.activation(
+                    out=state["negative"][n][:], in_=cube[n][:], func=ACT.Relu, scale=column("down", n - DEGREE)
+                )
+            k = j - 2
+            if 0 <= k < KNOTS:
+                state["left"][k] = left_pool.tile([P, cols], BF16, name="left")
+                nc.vector.scalar_tensor_tensor(
+                    out=state["left"][k][:], in0=state["positive"][k][:], scalar=column("first_up", k),
+                    in1=state["positive"][k + 1][:], op0=ALU.mult, op1=ALU.subtract,
+                )
+            k = j - DEGREE - 2
+            if 0 <= k < KNOTS:
+                right = right_pool.tile([P, cols], BF16, name="right")
+                nc.vector.scalar_tensor_tensor(
+                    out=right[:], in0=state["negative"][k + DEGREE + 1][:], scalar=column("first_down", k),
+                    in1=state["negative"][k + DEGREE][:], op0=ALU.mult, op1=ALU.subtract,
+                )
+                state["sides"] = (k, state["left"][k], right)
 
         later = []
 
         def finish_row_tiles(state, a, planes_done, now):
             s = a % TILES_PER_GROUP
             if s == 0:
-                state["basis"] = work.tile([P, TILES_PER_GROUP, PASSES, P, PACK], BF16, align_bytes=64, name="basis")
+                state["basis"] = work.tile([P, TILES_PER_GROUP, PASSES * P * PACK], BF16, align_bytes=64, name="basis")
             basis = state["basis"]
             words = state["rows"][:].bitcast(F32)
-            for g in range(PASSES):
-                flipped = transposed.tile([P, PACK, P], F32, tag="transposed", name="flipped")
-                for w in range(PACK):
-                    nc.tensor.transpose(
-                        flipped[:, w, :],
-                        words[:, FEATURES_PER_PASS * g : FEATURES_PER_PASS * (g + 1), :, w, a // 2].rearrange(
-                            "m f r -> m (f r)"
-                        ),
-                        identity_f32[:],
-                    )
-                halves = flipped[:].rearrange("p w m -> p (w m)").bitcast(BF16).rearrange(
-                    "p (w m e) -> p e m w", w=PACK, e=2
+            for tile in range(a, a + 2):
+                flipped = transposed.tile([P, PASSES, PAIRS, P], F32, tag="transposed", name="flipped")
+                for g in range(PASSES):
+                    for u in range(PAIRS):
+                        gu = PAIRS * g + u
+                        nc.tensor.transpose(
+                            flipped[:, g, u, :],
+                            words[:, CLASSES * gu : CLASSES * (gu + 1), :, tile].rearrange("m c k -> m (c k)"),
+                            identity_f32[:],
+                        )
+                nc.scalar.copy(
+                    out=basis[:, tile % TILES_PER_GROUP, :].bitcast(F32).rearrange(
+                        "p (g m u) -> p g m u", g=PASSES, u=PAIRS
+                    ),
+                    in_=flipped[:].rearrange("p g u m -> p g m u"),
                 )
-                if planes_done and s == 0 and g == 1:
-                    nc.vector.tensor_scalar_max(out=basis[:, s : s + 2, g, :, :], in0=halves, scalar1=0.0)
-                else:
-                    nc.scalar.activation(out=basis[:, s : s + 2, g, :, :], in_=halves, func=ACT.Relu)
             if s + 2 < TILES_PER_GROUP:
                 return
             group = {"basis": basis, "tile0": state["first"] + a - s, "planes_done": planes_done}
@@ -243,7 +275,7 @@ def tile_kanlayer_t_kernel(tc, x, spline_coeffs, spline_knots, out):
             group["scales"] = work.tile([P, GROUP_COLS], U8, align_bytes=64, name="scales")
             nc.vector.quantize_mx(
                 out=group["codes"][:].bitcast(FP8X4), scales=group["scales"][:],
-                in_=group["basis"][:].rearrange("p s g m w -> p (s g m w)"),
+                in_=group["basis"][:].rearrange("p s n -> p (s n)"),
             )
 
         def multiply_group(group):
@@ -278,21 +310,22 @@ def tile_kanlayer_t_kernel(tc, x, spline_coeffs, spline_knots, out):
                 if entry[0] == now:
                     entry[1](entry[2])
 
+        ticks = ALL_KNOTS + 1
         finished = None
         now = 0
         for step in range(len(CHUNK_TILES)):
             current = open_chunk(step)
             done = 0
-            for j in range(ALL_KNOTS):
+            for j in range(ticks):
                 add_knot(current, j)
                 if j == PREPARE_AT and step + 1 < len(CHUNK_TILES):
-                    nc.scalar.copy(out=x_planes[step + 1][:], in_=x_rows[step + 1][:].rearrange("m a i -> m i a"))
+                    lay_out_x(nc.scalar.copy, step + 1)
                 if step == 0 and j in (PREPARE_AT + 4, PREPARE_AT + 8):
                     turn_coefficients(nc, transposed, identity, coefficients, (j - PREPARE_AT) // 4 - 1)
                 if step == 0 and j == PREPARE_AT + 12:
                     weights["codes"], weights["scales"] = quantise_coefficients(nc, const, coefficients)
                 if finished is not None:
-                    while done * ALL_KNOTS < (j + 1) * finished["tiles"]:
+                    while done * ticks < (j + 1) * finished["tiles"]:
                         finish_row_tiles(finished, done, False, now)
                         done += 2
                 run_later(now)

@@ -25,8 +25,9 @@ PAIRS = PACK // 2
 QUADS = PASSES * PAIRS * CLASSES
 ROW_TILES = ROWS // P
 CHUNK_TILES = (24, 24, 16)
+TURNED_TILES = (12, 12, 0)
 PREPARE_AT = 12
-VECTOR_PARTS = (0, 0, 4)
+VECTOR_PARTS = (2, 16, 6)
 TILES_PER_GROUP = 4
 GROUP_COLS = TILES_PER_GROUP * PASSES * P
 
@@ -67,11 +68,13 @@ def load_knot_scalars(nc, const, spline_knots):
         "b3": [from_k(1, 3), from_k(1, 2), from_k(2, 1), from_k(3, 0)],
     }
     inverse = {}
+    products = {}
     for key in ("a0", "a1", "b4", "b3"):
         product = const.tile([P, KNOTS], F32, name="product_" + key)
         nc.vector.tensor_mul(out=product[:], in0=factors[key][0], in1=factors[key][1])
         for factor in factors[key][2:]:
             nc.vector.tensor_mul(out=product[:], in0=product[:], in1=factor)
+        products[key] = product
         inverse[key] = const.tile([P, KNOTS], F32, name="inverse_" + key)
         nc.vector.reciprocal(out=inverse[key][:], in_=product[:])
 
@@ -92,7 +95,18 @@ def load_knot_scalars(nc, const, spline_knots):
     nc.vector.scalar_tensor_tensor(
         out=first_down[:], in0=inverse["b4"][:], scalar=-1.0, in1=one_over[:, 1, :], op0=ALU.mult, op1=ALU.mult
     )
-    return {"knot": knot, "neg_knot": neg_knot, "up": up, "down": down, "first_up": first_up, "first_down": first_down}
+    neg_alpha = const.tile([P, KNOTS], F32)
+    nc.vector.scalar_tensor_tensor(
+        out=neg_alpha[:], in0=up[:, 1 : KNOTS + 1], scalar=-1.0, in1=products["a0"][:], op0=ALU.mult, op1=ALU.mult
+    )
+    neg_beta = const.tile([P, KNOTS], F32)
+    nc.vector.tensor_mul(out=neg_beta[:], in0=down[:, 0:KNOTS], in1=products["b4"][:])
+    neg_b4 = const.tile([P, KNOTS], F32)
+    nc.vector.tensor_scalar_mul(out=neg_b4[:], in0=inverse["b4"][:], scalar1=-1.0)
+    return {
+        "knot": knot, "neg_knot": neg_knot, "up": up, "down": down, "first_up": first_up, "first_down": first_down,
+        "neg_alpha": neg_alpha, "neg_beta": neg_beta, "a0": inverse["a0"], "neg_b4": neg_b4,
+    }
 
 
 def load_coefficients(nc, const, spline_coeffs):
@@ -139,8 +153,11 @@ def tile_kanlayer_t_kernel(tc, x, spline_coeffs, spline_knots, out):
         left_pool = ctx.enter_context(tc.tile_pool(name="lefts", bufs=7))
         right_pool = ctx.enter_context(tc.tile_pool(name="rights", bufs=3))
         work = ctx.enter_context(tc.tile_pool(name="work", bufs=2))
-        transposed = ctx.enter_context(tc.psum_pool(name="transposed", bufs=4))
-        sums = ctx.enter_context(tc.psum_pool(name="sums", bufs=3))
+        turned_pool = ctx.enter_context(tc.tile_pool(name="turned", bufs=3))
+        turned_left_pool = ctx.enter_context(tc.tile_pool(name="turned_lefts", bufs=7))
+        transposed = ctx.enter_context(tc.psum_pool(name="transposed", bufs=2))
+        sides = ctx.enter_context(tc.psum_pool(name="sides", bufs=2))
+        sums = ctx.enter_context(tc.psum_pool(name="sums", bufs=2))
 
         identity = const.tile([P, P], BF16)
         make_identity(nc, identity[:])
@@ -156,16 +173,36 @@ def tile_kanlayer_t_kernel(tc, x, spline_coeffs, spline_knots, out):
             tiles = CHUNK_TILES[chunk]
             x_rows.append(const.tile([P, tiles, FEATURES], BF16, name="x_rows%d" % chunk))
             nc.sync.dma_start(out=x_rows[chunk][:], in_=x_by_rows[:, first : first + tiles, :])
-            x_planes.append(const.tile([P, QUADS, tiles, 2], BF16, name="x_planes%d" % chunk))
+            x_planes.append(const.tile([P, FEATURES * tiles], BF16, name="x_planes%d" % chunk))
 
         def lay_out_x(engine_copy, chunk):
+            turned = TURNED_TILES[chunk]
+            straight = CHUNK_TILES[chunk] - turned
+            to_turn = const.tile([P, QUADS, turned, 2], BF16, name="to_turn%d" % chunk) if turned > 0 else None
             for gu in range(PASSES * PAIRS):
+                features = slice(2 * CLASSES * gu, 2 * CLASSES * (gu + 1))
+                quads = slice(CLASSES * gu, CLASSES * (gu + 1))
                 engine_copy(
-                    out=x_planes[chunk][:, CLASSES * gu : CLASSES * (gu + 1), :, :],
-                    in_=x_rows[chunk][:, :, 2 * CLASSES * gu : 2 * CLASSES * (gu + 1)].rearrange(
-                        "m a (e c) -> m c a e", e=2
-                    ),
+                    out=x_planes[chunk][:, 0 : FEATURES * straight].rearrange("m (q a e) -> m q a e", q=QUADS, e=2)[
+                        :, quads, :, :
+                    ],
+                    in_=x_rows[chunk][:, 0:straight, features].rearrange("m a (e c) -> m c a e", e=2),
                 )
+                if turned > 0:
+                    engine_copy(
+                        out=to_turn[:, quads, :, :],
+                        in_=x_rows[chunk][:, straight : straight + turned, features].rearrange("m a (e c) -> m c a e", e=2),
+                    )
+            if turned > 0:
+                blocks = FEATURES * turned // P
+                flipped_x = transposed.tile([P, blocks * P], BF16, tag="transposed", name="flipped_x")
+                for n in range(blocks):
+                    nc.tensor.transpose(
+                        flipped_x[:, P * n : P * n + P],
+                        to_turn[:].rearrange("m q a e -> m (q a e)")[:, P * n : P * n + P],
+                        identity[:],
+                    )
+                engine_copy(out=x_planes[chunk][:, FEATURES * straight : FEATURES * (straight + turned)], in_=flipped_x[:])
 
         lay_out_x(nc.vector.tensor_copy, 0)
         out_rows = out.rearrange("(m a) o -> m a o", a=ROW_TILES)
@@ -180,8 +217,10 @@ def tile_kanlayer_t_kernel(tc, x, spline_coeffs, spline_knots, out):
             rows = work.tile([P, QUADS, KNOTS, 2 * tiles], BF16, name="rows")
             return {
                 "first": sum(CHUNK_TILES[:chunk]), "tiles": tiles, "cols": FEATURES * tiles,
-                "x": x_planes[chunk][:].rearrange("m q a e -> m (q a e)"), "rows": rows,
+                "straight": FEATURES * (tiles - TURNED_TILES[chunk]),
+                "x": x_planes[chunk][:], "rows": rows,
                 "cube": {}, "positive": {}, "negative": {}, "left": {}, "sides": None,
+                "turned_inner": {}, "turned_left": {},
                 "vector_parts": VECTOR_PARTS[chunk],
             }
 
@@ -190,7 +229,7 @@ def tile_kanlayer_t_kernel(tc, x, spline_coeffs, spline_knots, out):
                 return
             k, left, right = state["sides"]
             nc.vector.tensor_tensor(
-                out=state["rows"][:, :, k, :],
+                out=state["rows"][:, :, k, 0 : state["straight"] // QUADS],
                 in0=left[:].rearrange("m (q n) -> m q n", q=QUADS),
                 in1=right[:].rearrange("m (q n) -> m q n", q=QUADS),
                 op=ALU.max,
@@ -200,6 +239,7 @@ def tile_kanlayer_t_kernel(tc, x, spline_coeffs, spline_knots, out):
         def add_knot(state, j):
             cube = state["cube"]
             cols = state["cols"]
+            straight = state["straight"]
             if j < ALL_KNOTS:
                 cube[j] = cube_pool.tile([P, cols], F32, name="cube")
                 nc.scalar.activation(out=cube[j][:], in_=state["x"], func=ACT.Square, bias=column("neg_knot", j))
@@ -210,34 +250,87 @@ def tile_kanlayer_t_kernel(tc, x, spline_coeffs, spline_knots, out):
             pick_larger(state)
             n = j - 1
             if 0 <= n <= KNOTS:
-                state["positive"][n] = part_pool.tile([P, cols], F32, name="positive")
+                state["positive"][n] = part_pool.tile([P, straight], F32, name="positive")
                 if (n + 1) * state["vector_parts"] // (KNOTS + 1) > n * state["vector_parts"] // (KNOTS + 1):
                     nc.vector.tensor_scalar(
-                        out=state["positive"][n][:], in0=cube[n][:], scalar1=column("up", n), scalar2=0.0,
+                        out=state["positive"][n][:], in0=cube[n][:, 0:straight], scalar1=column("up", n), scalar2=0.0,
                         op0=ALU.mult, op1=ALU.max,
                     )
                 else:
-                    nc.scalar.activation(out=state["positive"][n][:], in_=cube[n][:], func=ACT.Relu, scale=column("up", n))
+                    nc.scalar.activation(
+                        out=state["positive"][n][:], in_=cube[n][:, 0:straight], func=ACT.Relu, scale=column("up", n)
+                    )
             if DEGREE <= n < ALL_KNOTS:
-                state["negative"][n] = part_pool.tile([P, cols], F32, name="negative")
+                state["negative"][n] = part_pool.tile([P, straight], F32, name="negative")
                 nc.scalar.activation(
-                    out=state["negative"][n][:], in_=cube[n][:], func=ACT.Relu, scale=column("down", n - DEGREE)
+                    out=state["negative"][n][:], in_=cube[n][:, 0:straight], func=ACT.Relu, scale=column("down", n - DEGREE)
                 )
             k = j - 2
             if 0 <= k < KNOTS:
-                state["left"][k] = left_pool.tile([P, cols], BF16, name="left")
+                state["left"][k] = left_pool.tile([P, straight], BF16, name="left")
                 nc.vector.scalar_tensor_tensor(
                     out=state["left"][k][:], in0=state["positive"][k][:], scalar=column("first_up", k),
                     in1=state["positive"][k + 1][:], op0=ALU.mult, op1=ALU.subtract,
                 )
             k = j - DEGREE - 2
             if 0 <= k < KNOTS:
-                right = right_pool.tile([P, cols], BF16, name="right")
+                right = right_pool.tile([P, straight], BF16, name="right")
                 nc.vector.scalar_tensor_tensor(
                     out=right[:], in0=state["negative"][k + DEGREE + 1][:], scalar=column("first_down", k),
                     in1=state["negative"][k + DEGREE][:], op0=ALU.mult, op1=ALU.subtract,
                 )
                 state["sides"] = (k, state["left"][k], right)
+            if straight < cols:
+                add_turned(state, n)
+
+        def turn_and_add(bank, first_plane, second_plane, width):
+            for n in range(width // P):
+                block = slice(P * n, P * n + P)
+                nc.tensor.matmul(
+                    bank[:, block], lhsT=first_plane[:, block], rhs=identity_f32[:], start=True, stop=False,
+                    is_transpose=True,
+                )
+                nc.tensor.matmul(
+                    bank[:, block], lhsT=second_plane[:, block], rhs=identity_f32[:], start=False, stop=True,
+                    is_transpose=True,
+                )
+
+        def add_turned(state, n):
+            cube = state["cube"]
+            straight = state["straight"]
+            width = state["cols"] - straight
+            run = width // QUADS
+            k = n - DEGREE - 1
+            if 0 <= k < KNOTS:
+                right_sum = sides.tile([P, 4 * P], F32, name="right_sum")
+                turn_and_add(right_sum, cube[n][:, straight : straight + width], state["turned_inner"][k], width)
+                nc.vector.scalar_tensor_tensor(
+                    out=state["rows"][:, :, k, straight // QUADS : straight // QUADS + run],
+                    in0=right_sum[:, 0:width].rearrange("m (q n) -> m q n", q=QUADS),
+                    scalar=column("neg_b4", k),
+                    in1=state["turned_left"][k][:].rearrange("m (q n) -> m q n", q=QUADS),
+                    op0=ALU.mult, op1=ALU.max,
+                )
+            k = n - DEGREE
+            if 0 <= k < KNOTS:
+                state["turned_inner"][k] = turned_pool.tile([P, width], F32, name="turned_inner_right")
+                nc.scalar.activation(
+                    out=state["turned_inner"][k][:], in_=cube[n][:, straight : straight + width], func=ACT.Relu,
+                    scale=column("neg_beta", k),
+                )
+            k = n - 1
+            if 0 <= k < KNOTS:
+                inner_left = turned_pool.tile([P, width], F32, name="turned_inner_left")
+                nc.vector.tensor_scalar(
+                    out=inner_left[:], in0=cube[n][:, straight : straight + width], scalar1=column("neg_alpha", k),
+                    scalar2=0.0, op0=ALU.mult, op1=ALU.min,
+                )
+                left_sum = sides.tile([P, 4 * P], F32, name="left_sum")
+                turn_and_add(left_sum, cube[k][:, straight : straight + width], inner_left, width)
+                state["turned_left"][k] = turned_left_pool.tile([P, width], BF16, name="turned_left")
+                nc.scalar.activation(
+                    out=state["turned_left"][k][:], in_=left_sum[:, 0:width], func=ACT.Relu, scale=column("a0", k)
+                )
 
         later = []
 

@@ -24,10 +24,10 @@ CLASSES = P // KNOTS
 PAIRS = PACK // 2
 QUADS = PASSES * PAIRS * CLASSES
 ROW_TILES = ROWS // P
-CHUNK_TILES = (24, 24, 16)
-TURNED_TILES = (12, 12, 0)
+CHUNK_TILES = (28, 24, 12)
+TURNED_TILES = (16, 8, 0)
 PREPARE_AT = 12
-VECTOR_PARTS = (2, 16, 6)
+VECTOR_PARTS = (4, 12, 14)
 TILES_PER_GROUP = 4
 GROUP_COLS = TILES_PER_GROUP * PASSES * P
 

@@ -5,6 +5,7 @@ from concourse.masks import make_identity
 
 F32 = mybir.dt.float32
 BF16 = mybir.dt.bfloat16
+I32 = mybir.dt.int32
 U32 = mybir.dt.uint32
 U8 = mybir.dt.uint8
 FP8X4 = mybir.dt.float8_e4m3fn_x4
@@ -18,416 +19,532 @@ FEATURES = 32
 OUTS = 256
 KNOTS = 32
 DEGREE = 3
-ALL_KNOTS = KNOTS + DEGREE + 1
 PASSES = 2
 CLASSES = P // KNOTS
 PAIRS = PACK // 2
 QUADS = PASSES * PAIRS * CLASSES
 ROW_TILES = ROWS // P
-CHUNK_TILES = (28, 24, 12)
-TURNED_TILES = (16, 8, 0)
-PREPARE_AT = 12
-VECTOR_PARTS = (4, 12, 14)
 TILES_PER_GROUP = 4
 GROUP_COLS = TILES_PER_GROUP * PASSES * P
+
+STEPS = 34
+STEP_ROWS = STEPS + 1
+TRIPLE = 3
+X_ROW = TRIPLE * STEP_ROWS
+GROUPS = 5
+BLOCKS = 2 * GROUPS + 1
+GEO = 6
+LOOK = 1 + TRIPLE * GEO
+LAST = 1 + GEO
+LOOK_SLOTS = GROUPS + 1
+Q_PAD = LOOK_SLOTS * TRIPLE
+CELL_BITS = 6
+
+CHUNK_TILES = (4, 12, 16, 16, 12, 4)
+SUB_TILES = 4
+STEP_BUFS = 3
+MAX_TILES = max(CHUNK_TILES)
+QUARTER = 16
+PARK_TILES = 4
 
 FLOPS = 2 * ROWS * FEATURES * KNOTS * OUTS
 
 
-def load_knot_scalars(nc, const, spline_knots):
-    knots_bf = const.tile([P, KNOTS], BF16)
+def load_knots(nc, pool, spline_knots):
+    knots_bf = pool.tile([P, KNOTS], BF16)
     nc.sync.dma_start(out=knots_bf[:], in_=spline_knots.partition_broadcast(P))
-    knot = const.tile([P, ALL_KNOTS], F32)
-    nc.vector.tensor_copy(out=knot[:, 0:KNOTS], in_=knots_bf[:])
-    step = const.tile([P, 1], F32)
-    nc.vector.tensor_sub(out=step[:], in0=knot[:, 1:2], in1=knot[:, 0:1])
-    for j in range(DEGREE + 1):
+    knot = pool.tile([P, KNOTS + 8], F32)
+    nc.vector.tensor_copy(out=knot[:, 2 : 2 + KNOTS], in_=knots_bf[:])
+    for i in range(2):
+        nc.vector.tensor_copy(out=knot[:, i : i + 1], in_=knots_bf[:, 0:1])
+    step = pool.tile([P, 1], F32)
+    nc.vector.tensor_sub(out=step[:], in0=knot[:, 3:4], in1=knot[:, 2:3])
+    for n in range(1, 7):
+        at = 2 + KNOTS - 1 + n
         nc.vector.tensor_scalar(
-            out=knot[:, KNOTS + j : KNOTS + j + 1],
-            in0=step[:],
-            scalar1=float(j + 1),
-            scalar2=knot[:, KNOTS - 1 : KNOTS],
-            op0=ALU.mult,
-            op1=ALU.add,
+            out=knot[:, at : at + 1], in0=step[:], scalar1=float(n), scalar2=knot[:, 1 + KNOTS : 2 + KNOTS],
+            op0=ALU.mult, op1=ALU.add,
         )
-    neg_knot = const.tile([P, ALL_KNOTS], F32)
-    nc.vector.tensor_scalar_mul(out=neg_knot[:], in0=knot[:], scalar1=-1.0)
-
-    gap = {}
-    for n in range(1, DEGREE + 2):
-        gap[n] = const.tile([P, ALL_KNOTS - n], F32, name="gap%d" % n)
-        nc.vector.tensor_sub(out=gap[n][:], in0=knot[:, n:ALL_KNOTS], in1=knot[:, 0 : ALL_KNOTS - n])
-
-    def from_k(n, shift):
-        return gap[n][:, shift : shift + KNOTS]
-
-    factors = {
-        "a0": [from_k(1, 0), from_k(2, 0), from_k(3, 0)],
-        "a1": [from_k(1, 0), from_k(1, 1), from_k(2, 1), from_k(3, 1)],
-        "b4": [from_k(3, 1), from_k(2, 2), from_k(1, 3)],
-        "b3": [from_k(1, 3), from_k(1, 2), from_k(2, 1), from_k(3, 0)],
-    }
-    inverse = {}
-    products = {}
-    for key in ("a0", "a1", "b4", "b3"):
-        product = const.tile([P, KNOTS], F32, name="product_" + key)
-        nc.vector.tensor_mul(out=product[:], in0=factors[key][0], in1=factors[key][1])
-        for factor in factors[key][2:]:
-            nc.vector.tensor_mul(out=product[:], in0=product[:], in1=factor)
-        products[key] = product
-        inverse[key] = const.tile([P, KNOTS], F32, name="inverse_" + key)
-        nc.vector.reciprocal(out=inverse[key][:], in_=product[:])
-
-    up = const.tile([P, KNOTS + 1], F32)
-    nc.vector.tensor_copy(out=up[:, 0:1], in_=inverse["a0"][:, 0:1])
-    nc.vector.tensor_mul(out=up[:, 1 : KNOTS + 1], in0=inverse["a1"][:], in1=gap[4][:])
-    down = const.tile([P, KNOTS + 1], F32)
-    nc.vector.scalar_tensor_tensor(
-        out=down[:, 0:KNOTS], in0=inverse["b3"][:], scalar=-1.0, in1=gap[4][:], op0=ALU.mult, op1=ALU.mult
-    )
-    nc.vector.tensor_scalar_mul(out=down[:, KNOTS : KNOTS + 1], in0=inverse["b4"][:, KNOTS - 1 : KNOTS], scalar1=-1.0)
-    one_over = const.tile([P, 2, KNOTS], F32)
-    nc.vector.reciprocal(out=one_over[:, 0, :], in_=up[:, 0:KNOTS])
-    nc.vector.reciprocal(out=one_over[:, 1, :], in_=down[:, 1 : KNOTS + 1])
-    first_up = const.tile([P, KNOTS], F32)
-    nc.vector.tensor_mul(out=first_up[:], in0=inverse["a0"][:], in1=one_over[:, 0, :])
-    first_down = const.tile([P, KNOTS], F32)
-    nc.vector.scalar_tensor_tensor(
-        out=first_down[:], in0=inverse["b4"][:], scalar=-1.0, in1=one_over[:, 1, :], op0=ALU.mult, op1=ALU.mult
-    )
-    neg_alpha = const.tile([P, KNOTS], F32)
-    nc.vector.scalar_tensor_tensor(
-        out=neg_alpha[:], in0=up[:, 1 : KNOTS + 1], scalar=-1.0, in1=products["a0"][:], op0=ALU.mult, op1=ALU.mult
-    )
-    neg_beta = const.tile([P, KNOTS], F32)
-    nc.vector.tensor_mul(out=neg_beta[:], in0=down[:, 0:KNOTS], in1=products["b4"][:])
-    neg_b4 = const.tile([P, KNOTS], F32)
-    nc.vector.tensor_scalar_mul(out=neg_b4[:], in0=inverse["b4"][:], scalar1=-1.0)
-    return {
-        "knot": knot, "neg_knot": neg_knot, "up": up, "down": down, "first_up": first_up, "first_down": first_down,
-        "neg_alpha": neg_alpha, "neg_beta": neg_beta, "a0": inverse["a0"], "neg_b4": neg_b4,
-    }
+    gap = pool.tile([P, KNOTS + 7], F32)
+    nc.vector.tensor_sub(out=gap[:], in0=knot[:, 1 : KNOTS + 8], in1=knot[:, 0 : KNOTS + 7])
+    return knot, gap
 
 
-def load_coefficients(nc, const, spline_coeffs):
+def build_table(nc, const, pool, psum, identity_f32, knot, gap):
+    threshold_col = LOOK + 1
+    wide = pool.tile([P, LOOK + 2, P], F32)
+    nc.vector.memset(wide[:], 0.0)
+
+    def steps(first):
+        return gap[:, first : first + STEPS]
+
+    def row(n):
+        return wide[:, 1 + n, 0:STEPS]
+
+    for n, first, sign in ((0, 2, -1.0), (1, 3, 1.0), (2, 1, -1.0), (3, 4, 1.0)):
+        nc.vector.tensor_scalar_mul(out=row(n), in0=steps(first), scalar1=sign)
+    nc.vector.tensor_sub(out=row(4), in0=steps(5), in1=steps(2))
+    nc.vector.tensor_sub(out=row(5), in0=steps(3), in1=steps(0))
+
+    def start(n):
+        return wide[:, 1 + n, STEPS : STEPS + 1]
+
+    for n, at, sign in ((0, 2, -1.0), (1, 3, 1.0), (2, 1, -1.0), (3, 4, 1.0)):
+        nc.vector.tensor_scalar_mul(out=start(n), in0=knot[:, at : at + 1], scalar1=sign)
+    nc.vector.tensor_sub(out=start(4), in0=knot[:, 5:6], in1=knot[:, 2:3])
+    nc.vector.tensor_sub(out=start(5), in0=knot[:, 3:4], in1=knot[:, 0:1])
+    for c in range(1, TRIPLE):
+        nc.vector.tensor_copy(
+            out=wide[:, 1 + GEO * c : 1 + GEO * (c + 1), STEP_ROWS * c : STEP_ROWS * (c + 1)],
+            in_=wide[:, 1 : 1 + GEO, 0:STEP_ROWS],
+        )
+    for c in range(TRIPLE):
+        for n, slope in ((0, 1.0), (1, -1.0), (2, 1.0), (3, -1.0)):
+            nc.vector.memset(wide[:, 1 + GEO * c + n, X_ROW + c : X_ROW + c + 1], slope)
+        nc.vector.memset(wide[:, 0, STEP_ROWS * c : STEP_ROWS * (c + 1)], float(2 ** (CELL_BITS * c)))
+        nc.vector.tensor_copy(
+            out=wide[:, threshold_col, STEP_ROWS * c : STEP_ROWS * c + STEPS], in_=knot[:, 3 : 3 + STEPS]
+        )
+        nc.vector.memset(wide[:, threshold_col, STEP_ROWS * c + STEPS : STEP_ROWS * (c + 1)], -(2.0**100))
+    nc.vector.memset(wide[:, LOOK, STEP_ROWS : STEP_ROWS * 2], 1.0)
+
+    table = const.tile([P, LOOK + LAST], BF16)
+    threshold = const.tile([P, 1], F32)
+    for first in range(0, LOOK + 2, 4):
+        count = min(4, LOOK + 2 - first)
+        flipped = psum.tile([P, 4, P], F32, tag="transposed", name="flipped_table")
+        for b in range(count):
+            nc.tensor.transpose(flipped[:, b, :], wide[:, first + b, :], identity_f32[:])
+        last = min(first + count, threshold_col)
+        if last > first:
+            nc.vector.tensor_copy(out=table[:, first:last], in_=flipped[:, 0 : last - first, 0])
+        if first + count > threshold_col:
+            nc.vector.tensor_copy(out=threshold[:], in_=flipped[:, threshold_col - first, 0:1])
+    nc.vector.tensor_copy(out=table[:, LOOK + 1 : LOOK + LAST], in_=table[:, 1 + GEO : 1 + 2 * GEO])
+    return table, threshold
+
+
+def park_x(nc, pool, psum, identity, knot, x, parked):
+    x_rows = pool.tile([P, ROW_TILES, FEATURES], BF16)
+    nc.sync.dma_start(out=x_rows[:], in_=x.rearrange("(m a) i -> m a i", a=ROW_TILES))
+    clamped = pool.tile([P, ROW_TILES, FEATURES], BF16)
+    turned = pool.tile([P, ROW_TILES // 4, P], BF16)
+    for quarter in range(ROW_TILES // QUARTER):
+        tiles = slice(QUARTER * quarter, QUARTER * (quarter + 1))
+        by_e = x_rows[:, tiles, :].rearrange("m a (u e c) -> m e a u c", e=2, c=CLASSES)
+        for e in range(2):
+            first = TRIPLE * GROUPS * e
+            nc.vector.tensor_scalar(
+                out=clamped[:, tiles, first : first + QUADS].rearrange("m a (u c) -> m a u c", c=CLASSES),
+                in0=by_e[:, e], scalar1=knot[:, 2:3], scalar2=knot[:, 38:39], op0=ALU.max, op1=ALU.min,
+            )
+        nc.vector.tensor_scalar(
+            out=clamped[:, tiles, FEATURES - 2 : FEATURES], in0=x_rows[:, tiles, FEATURES - 5 : FEATURES : 4],
+            scalar1=knot[:, 2:3], scalar2=knot[:, 38:39], op0=ALU.max, op1=ALU.min,
+        )
+        flipped = psum.tile([P, 4, P], BF16, tag="transposed", name="flipped_x")
+        for n in range(4):
+            first = QUARTER * quarter + 4 * n
+            nc.tensor.transpose(
+                flipped[:, n, :], clamped[:, first : first + 4, :].rearrange("m a i -> m (a i)"), identity[:]
+            )
+        nc.scalar.copy(out=turned[:, 4 * quarter : 4 * quarter + 4, :], in_=flipped[:])
+        words = turned[:].bitcast(F32)
+        queue = nc.sync if quarter == 0 else nc.gpsimd
+        for b in range(4):
+            queue.dma_start(
+                out=parked[:, quarter, :].rearrange("r (n b w) -> r n b w", n=4, b=4)[:, :, b, :],
+                in_=words[FEATURES * b : FEATURES * (b + 1), 4 * quarter : 4 * quarter + 4, :],
+            )
+
+
+def prepare_coefficients(nc, const, pool, psum, identity, spline_coeffs):
     halves = OUTS // P
-    natural = const.tile([P, halves, FEATURES * KNOTS], BF16)
+    natural = pool.tile([P, halves, FEATURES * KNOTS], BF16)
     for h in range(halves):
         nc.sync.dma_start(
             out=natural[:, h, :].rearrange("q (i k) -> q i k", k=KNOTS),
             in_=spline_coeffs[:, P * h : P * h + P, :].rearrange("i q k -> q i k"),
         )
-    grouped = const.tile([P, PASSES, OUTS, PACK], BF16, align_bytes=64)
-    return {"natural": natural, "grouped": grouped}
-
-
-def turn_coefficients(nc, transposed, identity, coefficients, g):
-    halves = OUTS // P
-    flipped = transposed.tile([P, PACK, OUTS], BF16, tag="transposed", name="flipped_w")
-    for t in range(PACK):
-        for h in range(halves):
-            first = (PACK * g + t) * P
-            nc.tensor.transpose(
-                flipped[:, t, P * h : P * h + P], coefficients["natural"][:, h, first : first + P], identity[:]
-            )
-    nc.scalar.copy(out=coefficients["grouped"][:, g, :, :], in_=flipped[:].rearrange("p t o -> p o t"))
-
-
-def quantise_coefficients(nc, const, coefficients):
+    grouped = pool.tile([P, PASSES, OUTS, PACK], BF16, align_bytes=64)
+    for g in range(PASSES):
+        flipped = psum.tile([P, PACK, OUTS], BF16, tag="transposed", name="flipped_w")
+        for t in range(PACK):
+            for h in range(halves):
+                first = (PACK * g + t) * P
+                nc.tensor.transpose(flipped[:, t, P * h : P * h + P], natural[:, h, first : first + P], identity[:])
+        nc.scalar.copy(out=grouped[:, g, :, :], in_=flipped[:].rearrange("p t o -> p o t"))
     codes = const.tile([P, PASSES, OUTS], U32, align_bytes=64)
     scales = const.tile([P, PASSES, OUTS], U8, align_bytes=64)
     nc.vector.quantize_mx(
         out=codes[:].rearrange("p g o -> p (g o)").bitcast(FP8X4),
         scales=scales[:].rearrange("p g o -> p (g o)"),
-        in_=coefficients["grouped"][:].rearrange("p g o t -> p (g o t)"),
+        in_=grouped[:].rearrange("p g o t -> p (g o t)"),
     )
     return codes, scales
+
+
+def interleave(*lists):
+    entries = []
+    for which, items in enumerate(lists):
+        for n, item in enumerate(items):
+            entries.append(((n + 0.5) / len(items), which, n, item))
+    return [entry[3] for entry in sorted(entries, key=lambda entry: entry[:3])]
 
 
 def tile_kanlayer_t_kernel(tc, x, spline_coeffs, spline_knots, out):
     nc = tc.nc
     with ExitStack() as ctx:
         const = ctx.enter_context(tc.tile_pool(name="const", bufs=1))
-        cube_pool = ctx.enter_context(tc.tile_pool(name="cubes", bufs=5))
-        part_pool = ctx.enter_context(tc.tile_pool(name="parts", bufs=4))
-        left_pool = ctx.enter_context(tc.tile_pool(name="lefts", bufs=7))
-        right_pool = ctx.enter_context(tc.tile_pool(name="rights", bufs=3))
-        work = ctx.enter_context(tc.tile_pool(name="work", bufs=2))
-        turned_pool = ctx.enter_context(tc.tile_pool(name="turned", bufs=3))
-        turned_left_pool = ctx.enter_context(tc.tile_pool(name="turned_lefts", bufs=7))
+        planes = ctx.enter_context(tc.tile_pool(name="planes", bufs=1))
+        keys = ctx.enter_context(tc.tile_pool(name="keys", bufs=1))
+        carried = ctx.enter_context(tc.tile_pool(name="carried", bufs=2))
         transposed = ctx.enter_context(tc.psum_pool(name="transposed", bufs=2))
-        sides = ctx.enter_context(tc.psum_pool(name="sides", bufs=2))
+        lookups = ctx.enter_context(tc.psum_pool(name="lookups", bufs=1))
         sums = ctx.enter_context(tc.psum_pool(name="sums", bufs=2))
 
         identity = const.tile([P, P], BF16)
         make_identity(nc, identity[:])
         identity_f32 = const.tile([P, P], F32)
         make_identity(nc, identity_f32[:])
+        x_steps = []
+        for n in range(STEP_BUFS):
+            x_steps.append(const.tile([P, BLOCKS, SUB_TILES * P], BF16, name="x_steps%d" % n))
+            nc.gpsimd.memset(x_steps[n][:].bitcast(U32), 0)
+        raws = [const.tile([P, LOOK * LOOK_SLOTS * 2 * MAX_TILES], F32, name="raw%d" % n) for n in range(2)]
+        ones = const.tile([P, P], F32)
+        nc.gpsimd.memset(ones[:], 1.0)
+        banks = []
+        for n in range(2):
+            banks.append(lookups.tile([P, 4 * P], F32, name="bank%d" % n))
+            for b in range(4):
+                nc.tensor.transpose(banks[n][:, P * b : P * (b + 1)], ones[:], identity_f32[:])
 
-        scalars = load_knot_scalars(nc, const, spline_knots)
-        x_by_rows = x.rearrange("(m a) i -> m a i", a=ROW_TILES)
-        x_rows = []
-        x_planes = []
-        for chunk in range(len(CHUNK_TILES)):
-            first = sum(CHUNK_TILES[:chunk])
-            tiles = CHUNK_TILES[chunk]
-            x_rows.append(const.tile([P, tiles, FEATURES], BF16, name="x_rows%d" % chunk))
-            nc.sync.dma_start(out=x_rows[chunk][:], in_=x_by_rows[:, first : first + tiles, :])
-            x_planes.append(const.tile([P, FEATURES * tiles], BF16, name="x_planes%d" % chunk))
-
-        def lay_out_x(engine_copy, chunk):
-            turned = TURNED_TILES[chunk]
-            straight = CHUNK_TILES[chunk] - turned
-            to_turn = const.tile([P, QUADS, turned, 2], BF16, name="to_turn%d" % chunk) if turned > 0 else None
-            for gu in range(PASSES * PAIRS):
-                features = slice(2 * CLASSES * gu, 2 * CLASSES * (gu + 1))
-                quads = slice(CLASSES * gu, CLASSES * (gu + 1))
-                engine_copy(
-                    out=x_planes[chunk][:, 0 : FEATURES * straight].rearrange("m (q a e) -> m q a e", q=QUADS, e=2)[
-                        :, quads, :, :
-                    ],
-                    in_=x_rows[chunk][:, 0:straight, features].rearrange("m a (e c) -> m c a e", e=2),
-                )
-                if turned > 0:
-                    engine_copy(
-                        out=to_turn[:, quads, :, :],
-                        in_=x_rows[chunk][:, straight : straight + turned, features].rearrange("m a (e c) -> m c a e", e=2),
-                    )
-            if turned > 0:
-                blocks = FEATURES * turned // P
-                flipped_x = transposed.tile([P, blocks * P], BF16, tag="transposed", name="flipped_x")
-                for n in range(blocks):
-                    nc.tensor.transpose(
-                        flipped_x[:, P * n : P * n + P],
-                        to_turn[:].rearrange("m q a e -> m (q a e)")[:, P * n : P * n + P],
-                        identity[:],
-                    )
-                engine_copy(out=x_planes[chunk][:, FEATURES * straight : FEATURES * (straight + turned)], in_=flipped_x[:])
-
-        lay_out_x(nc.vector.tensor_copy, 0)
         out_rows = out.rearrange("(m a) o -> m a o", a=ROW_TILES)
-        coefficients = load_coefficients(nc, const, spline_coeffs)
-        weights = {}
+        parked = out_rows[:, ROW_TILES - PARK_TILES : ROW_TILES, :].rearrange("(r h) a o -> r h (a o)", h=ROW_TILES // QUARTER)
 
-        def column(name, index):
-            return scalars[name][:, index : index + 1]
+        with tc.tile_pool(name="setup", bufs=1) as setup:
+            knot, gap = load_knots(nc, setup, spline_knots)
+            park_x(nc, setup, transposed, identity, knot, x, parked)
+            table, threshold = build_table(nc, const, setup, transposed, identity_f32, knot, gap)
+            w_codes, w_scales = prepare_coefficients(nc, const, setup, transposed, identity, spline_coeffs)
 
-        def open_chunk(chunk):
-            tiles = CHUNK_TILES[chunk]
-            rows = work.tile([P, QUADS, KNOTS, 2 * tiles], BF16, name="rows")
-            return {
-                "first": sum(CHUNK_TILES[:chunk]), "tiles": tiles, "cols": FEATURES * tiles,
-                "straight": FEATURES * (tiles - TURNED_TILES[chunk]),
-                "x": x_planes[chunk][:], "rows": rows,
-                "cube": {}, "positive": {}, "negative": {}, "left": {}, "sides": None,
-                "turned_inner": {}, "turned_left": {},
-                "vector_parts": VECTOR_PARTS[chunk],
-            }
+        rows_pool = ctx.enter_context(tc.tile_pool(name="rows", bufs=2))
+        work = ctx.enter_context(tc.tile_pool(name="work", bufs=2))
 
-        def pick_larger(state):
-            if state["sides"] is None:
-                return
-            k, left, right = state["sides"]
-            nc.vector.tensor_tensor(
-                out=state["rows"][:, :, k, 0 : state["straight"] // QUADS],
-                in0=left[:].rearrange("m (q n) -> m q n", q=QUADS),
-                in1=right[:].rearrange("m (q n) -> m q n", q=QUADS),
-                op=ALU.max,
-            )
-            state["sides"] = None
-
-        def add_knot(state, j):
-            cube = state["cube"]
-            cols = state["cols"]
-            straight = state["straight"]
-            if j < ALL_KNOTS:
-                cube[j] = cube_pool.tile([P, cols], F32, name="cube")
-                nc.scalar.activation(out=cube[j][:], in_=state["x"], func=ACT.Square, bias=column("neg_knot", j))
-                nc.vector.scalar_tensor_tensor(
-                    out=cube[j][:], in0=state["x"], scalar=column("knot", j), in1=cube[j][:],
-                    op0=ALU.subtract, op1=ALU.mult,
+        def load(number):
+            steps = x_steps[number % STEP_BUFS]
+            tile0 = SUB_TILES * number
+            words = slice((tile0 % QUARTER) * P // 2, (tile0 % QUARTER + SUB_TILES) * P // 2)
+            source = parked[:, tile0 // QUARTER, words]
+            target = steps[:].bitcast(F32)
+            for c in range(TRIPLE):
+                blocks = BLOCKS if c < 2 else BLOCKS - 1
+                nc.sync.dma_start(
+                    out=target[STEP_ROWS * c : STEP_ROWS * (c + 1), 0:blocks, :],
+                    in_=source[c : c + 3 * blocks - 2 : 3, :].partition_broadcast(STEP_ROWS),
                 )
-            pick_larger(state)
-            n = j - 1
-            if 0 <= n <= KNOTS:
-                state["positive"][n] = part_pool.tile([P, straight], F32, name="positive")
-                if (n + 1) * state["vector_parts"] // (KNOTS + 1) > n * state["vector_parts"] // (KNOTS + 1):
+            nc.sync.dma_start(
+                out=target[X_ROW : X_ROW + TRIPLE, 0 : BLOCKS - 1, :],
+                in_=source[0 : 3 * (BLOCKS - 1), :].rearrange("(g c) w -> c g w", c=TRIPLE),
+            )
+            nc.sync.dma_start(out=target[X_ROW : X_ROW + 2, BLOCKS - 1, :], in_=source[FEATURES - 2 : FEATURES, :])
+
+        def look_up(state):
+            actions = []
+            size = LOOK * LOOK_SLOTS * 2 * state["tiles"]
+            raw = raws[state["index"] % 2][:, 0:size].rearrange("m (w g s) -> m w g s", w=LOOK, g=LOOK_SLOTS)
+            state["raw"] = raw
+            for first in range(0, state["tiles"], SUB_TILES):
+                number = (state["first"] + first) // SUB_TILES
+                steps = x_steps[number % STEP_BUFS]
+
+                def compare(steps=steps):
                     nc.vector.tensor_scalar(
-                        out=state["positive"][n][:], in0=cube[n][:, 0:straight], scalar1=column("up", n), scalar2=0.0,
-                        op0=ALU.mult, op1=ALU.max,
+                        out=steps[0:X_ROW, :, :], in0=steps[0:X_ROW, :, :], scalar1=threshold[0:X_ROW, :], scalar2=None,
+                        op0=ALU.is_ge,
                     )
-                else:
-                    nc.scalar.activation(
-                        out=state["positive"][n][:], in_=cube[n][:, 0:straight], func=ACT.Relu, scale=column("up", n)
-                    )
-            if DEGREE <= n < ALL_KNOTS:
-                state["negative"][n] = part_pool.tile([P, straight], F32, name="negative")
-                nc.scalar.activation(
-                    out=state["negative"][n][:], in_=cube[n][:, 0:straight], func=ACT.Relu, scale=column("down", n - DEGREE)
-                )
-            k = j - 2
-            if 0 <= k < KNOTS:
-                state["left"][k] = left_pool.tile([P, straight], BF16, name="left")
-                nc.vector.scalar_tensor_tensor(
-                    out=state["left"][k][:], in0=state["positive"][k][:], scalar=column("first_up", k),
-                    in1=state["positive"][k + 1][:], op0=ALU.mult, op1=ALU.subtract,
-                )
-            k = j - DEGREE - 2
-            if 0 <= k < KNOTS:
-                right = right_pool.tile([P, straight], BF16, name="right")
-                nc.vector.scalar_tensor_tensor(
-                    out=right[:], in0=state["negative"][k + DEGREE + 1][:], scalar=column("first_down", k),
-                    in1=state["negative"][k + DEGREE][:], op0=ALU.mult, op1=ALU.subtract,
-                )
-                state["sides"] = (k, state["left"][k], right)
-            if straight < cols:
-                add_turned(state, n)
 
-        def turn_and_add(bank, first_plane, second_plane, width):
-            for n in range(width // P):
-                block = slice(P * n, P * n + P)
-                nc.tensor.matmul(
-                    bank[:, block], lhsT=first_plane[:, block], rhs=identity_f32[:], start=True, stop=False,
-                    is_transpose=True,
-                )
-                nc.tensor.matmul(
-                    bank[:, block], lhsT=second_plane[:, block], rhs=identity_f32[:], start=False, stop=True,
-                    is_transpose=True,
-                )
+                actions.append(compare)
+                for pair in range(0, SUB_TILES, 2):
 
-        def add_turned(state, n):
-            cube = state["cube"]
-            straight = state["straight"]
-            width = state["cols"] - straight
-            run = width // QUADS
-            k = n - DEGREE - 1
-            if 0 <= k < KNOTS:
-                right_sum = sides.tile([P, 4 * P], F32, name="right_sum")
-                turn_and_add(right_sum, cube[n][:, straight : straight + width], state["turned_inner"][k], width)
-                nc.vector.scalar_tensor_tensor(
-                    out=state["rows"][:, :, k, straight // QUADS : straight // QUADS + run],
-                    in0=right_sum[:, 0:width].rearrange("m (q n) -> m q n", q=QUADS),
-                    scalar=column("neg_b4", k),
-                    in1=state["turned_left"][k][:].rearrange("m (q n) -> m q n", q=QUADS),
-                    op0=ALU.mult, op1=ALU.max,
-                )
-            k = n - DEGREE
-            if 0 <= k < KNOTS:
-                state["turned_inner"][k] = turned_pool.tile([P, width], F32, name="turned_inner_right")
-                nc.scalar.activation(
-                    out=state["turned_inner"][k][:], in_=cube[n][:, straight : straight + width], func=ACT.Relu,
-                    scale=column("neg_beta", k),
-                )
-            k = n - 1
-            if 0 <= k < KNOTS:
-                inner_left = turned_pool.tile([P, width], F32, name="turned_inner_left")
-                nc.vector.tensor_scalar(
-                    out=inner_left[:], in0=cube[n][:, straight : straight + width], scalar1=column("neg_alpha", k),
-                    scalar2=0.0, op0=ALU.mult, op1=ALU.min,
-                )
-                left_sum = sides.tile([P, 4 * P], F32, name="left_sum")
-                turn_and_add(left_sum, cube[k][:, straight : straight + width], inner_left, width)
-                state["turned_left"][k] = turned_left_pool.tile([P, width], BF16, name="turned_left")
-                nc.scalar.activation(
-                    out=state["turned_left"][k][:], in_=left_sum[:, 0:width], func=ACT.Relu, scale=column("a0", k)
-                )
-
-        later = []
-
-        def finish_row_tiles(state, a, planes_done, now):
-            s = a % TILES_PER_GROUP
-            if s == 0:
-                state["basis"] = work.tile([P, TILES_PER_GROUP, PASSES * P * PACK], BF16, align_bytes=64, name="basis")
-            basis = state["basis"]
-            words = state["rows"][:].bitcast(F32)
-            for tile in range(a, a + 2):
-                flipped = transposed.tile([P, PASSES, PAIRS, P], F32, tag="transposed", name="flipped")
-                for g in range(PASSES):
-                    for u in range(PAIRS):
-                        gu = PAIRS * g + u
-                        nc.tensor.transpose(
-                            flipped[:, g, u, :],
-                            words[:, CLASSES * gu : CLASSES * (gu + 1), :, tile].rearrange("m c k -> m (c k)"),
-                            identity_f32[:],
+                    def multiply(first=first, steps=steps, pair=pair):
+                        bank = banks[(first + pair) // 2 % 2]
+                        slots = bank[:, 0 : LOOK * LOOK_SLOTS * 4].rearrange("m (w g a e) -> m w g a e", w=LOOK, g=LOOK_SLOTS, a=2)
+                        for half in range(2):
+                            columns = slice(P * (pair + half), P * (pair + half + 1))
+                            for e in range(2):
+                                for g in range(GROUPS):
+                                    nc.tensor.matmul(
+                                        slots[:, :, g, half, e], lhsT=steps[:, GROUPS * e + g, columns],
+                                        rhs=table[:, 0:LOOK], start=True, stop=True,
+                                    )
+                                nc.tensor.matmul(
+                                    slots[:, 0:LAST, GROUPS, half, e], lhsT=steps[:, BLOCKS - 1, columns],
+                                    rhs=table[:, LOOK * e : LOOK * e + LAST], start=True, stop=True,
+                                )
+                        at = 2 * (first + pair)
+                        nc.scalar.copy(
+                            out=raw[:, :, :, at : at + 4],
+                            in_=bank[:, 0 : LOOK * LOOK_SLOTS * 4].rearrange("m (w g s) -> m w g s", w=LOOK, g=LOOK_SLOTS),
                         )
-                nc.scalar.copy(
-                    out=basis[:, tile % TILES_PER_GROUP, :].bitcast(F32).rearrange(
-                        "p (g m u) -> p g m u", g=PASSES, u=PAIRS
-                    ),
-                    in_=flipped[:].rearrange("p g u m -> p g m u"),
+
+                    actions.append(multiply)
+                if SUB_TILES * (number + STEP_BUFS) < ROW_TILES:
+                    actions.append(lambda number=number: load(number + STEP_BUFS))
+            return actions
+
+        def work_out(state):
+            slots = 2 * state["tiles"]
+            raw = state["raw"]
+
+            def column(n):
+                return raw[:, 1 + n : 1 + n + 2 * GEO + 1 : GEO, :, 0:slots]
+
+            def plane(name):
+                return planes.tile([P, TRIPLE, LOOK_SLOTS, slots], F32, name=name)
+
+            def every(tile):
+                return tile[:, :, :, 0:slots]
+
+            def used(tile):
+                return tile[:, :, :, 0:slots]
+
+            def by_quad(tile):
+                return tile[:, :, :, 0:slots].rearrange("m c g s -> m g c s")
+
+            def quads(tile):
+                return tile[:, :, 0:slots].rearrange("m (g c) s -> m g c s", c=TRIPLE)
+
+            vec = nc.vector
+            t = {}
+
+            def sums_of_distances():
+                for name in ("length", "double", "lower", "upper", "third", "first"):
+                    t[name] = plane(name)
+                vec.tensor_add(out=every(t["length"]), in0=column(0), in1=column(1))
+                vec.tensor_add(out=every(t["lower"]), in0=column(2), in1=column(1))
+                vec.tensor_add(out=every(t["upper"]), in0=column(0), in1=column(3))
+                vec.tensor_add(out=every(t["double"]), in0=column(2), in1=column(3))
+                nc.scalar.activation(out=every(t["third"]), in_=column(4), func=ACT.Abs_reciprocal_sqrt)
+                nc.scalar.activation(out=every(t["first"]), in_=column(5), func=ACT.Abs_reciprocal_sqrt)
+
+            def cells():
+                cell = keys.tile([P, LOOK_SLOTS, slots], I32, name="cell")
+                vec.tensor_copy(out=cell[:, :, 0:slots], in_=raw[:, 0, :, 0:slots])
+                own = keys.tile([P, TRIPLE, LOOK_SLOTS, slots], I32, name="own")
+                state["slot_index3"] = carried.tile([P, Q_PAD, slots], BF16, name="slot_index3")
+                for c in range(TRIPLE):
+                    vec.tensor_scalar(
+                        out=own[:, c, :, 0:slots], in0=cell[:, :, 0:slots], scalar1=CELL_BITS * c, scalar2=2**CELL_BITS - 1,
+                        op0=ALU.logical_shift_right, op1=ALU.bitwise_and,
+                    )
+                for name, shift, mask in (("bit0", 0, 1), ("bit1", 1, 1), ("four", 2, 15)):
+                    part = keys.tile([P, TRIPLE, LOOK_SLOTS, slots], I32, name="part_" + name)
+                    vec.tensor_scalar(
+                        out=used(part), in0=used(own), scalar1=shift, scalar2=mask,
+                        op0=ALU.logical_shift_right, op1=ALU.bitwise_and,
+                    )
+                    if name == "four":
+                        t[name] = state["slot_index3"]
+                    else:
+                        t[name] = keys.tile([P, Q_PAD, slots], BF16, name=name)
+                    nc.scalar.activation(out=quads(t[name]), in_=by_quad(part[:].bitcast(U32)), func=ACT.Copy)
+
+            def products():
+                vec.tensor_mul(out=used(t["upper"]), in0=used(t["length"]), in1=used(t["upper"]))
+                vec.tensor_mul(out=used(t["lower"]), in0=used(t["length"]), in1=used(t["lower"]))
+                for name in ("third", "first"):
+                    nc.scalar.activation(out=used(t[name]), in_=used(t[name]), func=ACT.Square)
+                for name in ("upper", "lower", "double"):
+                    nc.scalar.activation(out=used(t[name]), in_=used(t[name]), func=ACT.Abs_reciprocal_sqrt)
+                nc.scalar.activation(out=used(t["double"]), in_=used(t["double"]), func=ACT.Square)
+
+            def ratios():
+                vec.tensor_mul(out=every(t["third"]), in0=column(0), in1=every(t["third"]))
+                vec.scalar_tensor_tensor(
+                    out=every(t["first"]), in0=column(1), scalar=0.0, in1=every(t["first"]), op0=ALU.max, op1=ALU.mult
                 )
-            if s + 2 < TILES_PER_GROUP:
-                return
-            group = {"basis": basis, "tile0": state["first"] + a - s, "planes_done": planes_done}
-            later.append((now + 1, quantise_group, group))
-            later.append((now + 2, multiply_group, group))
-            later.append((now + 3, store_group, group))
+                vec.tensor_mul(out=every(t["upper"]), in0=column(0), in1=every(t["upper"]))
+                vec.tensor_mul(out=every(t["lower"]), in0=column(1), in1=every(t["lower"]))
+                vec.tensor_mul(out=every(t["double"]), in0=column(2), in1=every(t["double"]))
+                for name in ("upper", "lower"):
+                    nc.scalar.activation(out=used(t[name]), in_=used(t[name]), func=ACT.Square)
 
-        def quantise_group(group):
-            group["codes"] = work.tile([P, GROUP_COLS], U32, align_bytes=64, name="codes")
-            group["scales"] = work.tile([P, GROUP_COLS], U8, align_bytes=64, name="scales")
-            nc.vector.quantize_mx(
-                out=group["codes"][:].bitcast(FP8X4), scales=group["scales"][:],
-                in_=group["basis"][:].rearrange("p s n -> p (s n)"),
-            )
+            def values():
+                four = keys.tile([P, 4, Q_PAD, slots], BF16, name="values")
+                t["values"] = four
+                upper, lower, double, third, first, length = (
+                    used(t[name]) for name in ("upper", "lower", "double", "third", "first", "length")
+                )
+                vec.tensor_mul(out=third, in0=upper, in1=third)
+                vec.tensor_mul(out=first, in0=lower, in1=first)
+                vec.tensor_add(out=length, in0=upper, in1=lower)
+                vec.scalar_tensor_tensor(out=length, in0=length, scalar=1.0, in1=double, op0=ALU.subtract, op1=ALU.mult)
+                vec.tensor_sub(out=upper, in0=upper, in1=length)
+                vec.tensor_sub(out=quads(four[:, 2]), in0=by_quad(t["upper"]), in1=by_quad(t["third"]))
+                vec.tensor_add(out=length, in0=upper, in1=first)
+                nc.scalar.activation(out=quads(four[:, 3]), in_=by_quad(t["third"]), func=ACT.Copy)
+                nc.scalar.activation(out=quads(four[:, 0]), in_=by_quad(t["first"]), func=ACT.Copy)
+                nc.scalar.activation(
+                    out=quads(four[:, 1]), in_=by_quad(t["length"]), func=ACT.Copy, scale=-1.0, bias=1.0
+                )
 
-        def multiply_group(group):
-            group["acc"] = []
-            for pair in range(TILES_PER_GROUP // 2):
-                acc = sums.tile([P, 2, OUTS], F32, name="acc")
-                group["acc"].append(acc)
+            def slot_indices():
+                def bits(name):
+                    return t[name][:, 0:QUADS, 0:slots]
+
+                index = carried.tile([P, 3, QUADS, slots], BF16, name="index")
+                state["slot_index"] = index
+                either = keys.tile([P, QUADS, slots], BF16, name="either")
+                both = keys.tile([P, QUADS, slots], BF16, name="both")
+                vec.tensor_max(out=either[:, :, 0:slots], in0=bits("bit0"), in1=bits("bit1"))
+                vec.tensor_mul(out=both[:, :, 0:slots], in0=bits("bit0"), in1=bits("bit1"))
+                vec.tensor_add(out=index[:, 1, :, 0:slots], in0=bits("four"), in1=bits("bit1"))
+                vec.tensor_add(out=index[:, 0, :, 0:slots], in0=bits("four"), in1=either[:, :, 0:slots])
+                vec.tensor_add(out=index[:, 2, :, 0:slots], in0=bits("four"), in1=both[:, :, 0:slots])
+
+            def rotate(source, bit, by, target):
+                shape = [P, 4, QUADS, slots]
+                flag = t[bit][:, 0:QUADS, 0:slots].unsqueeze(1).to_broadcast(shape)
+                moved = keys.tile([P, 4, QUADS, slots], BF16, name="moved")
+                kept = source
+                whole = source[:, :, 0:QUADS, 0:slots]
+                vec.tensor_mul(out=moved[:, :, :, 0:slots], in0=whole, in1=flag)
+                vec.tensor_sub(out=whole, in0=whole, in1=moved[:, :, :, 0:slots])
+                vec.tensor_add(
+                    out=target[:, by:4, :, 0:slots], in0=kept[:, by:4, 0:QUADS, 0:slots], in1=moved[:, 0 : 4 - by, :, 0:slots]
+                )
+                vec.tensor_add(
+                    out=target[:, 0:by, :, 0:slots], in0=kept[:, 0:by, 0:QUADS, 0:slots], in1=moved[:, 4 - by : 4, :, 0:slots]
+                )
+
+            def first_turn():
+                t["half_turned"] = keys.tile([P, 4, QUADS, slots], BF16, name="half_turned")
+                rotate(t["values"], "bit0", 1, t["half_turned"])
+
+            def second_turn():
+                state["slot_value"] = carried.tile([P, 4, QUADS, slots], BF16, name="slot_value")
+                rotate(t["half_turned"], "bit1", 2, state["slot_value"])
+
+            return [sums_of_distances, cells, products, slot_indices, ratios, values, first_turn, second_turn]
+
+        def spread(state):
+            slots = 2 * state["tiles"]
+            state["rows"] = rows_pool.tile([P, QUADS, KNOTS, slots], BF16, name="rows")
+            rows = state["rows"]
+            actions = []
+            for s in range(4):
                 for half in range(2):
-                    for g in range(PASSES):
-                        n = (2 * pair + half) * PASSES + g
-                        nc.tensor.matmul_mx(
-                            out=acc[:, half, :],
-                            lhsT=group["codes"][:, P * n : P * n + P].bitcast(FP8X4),
-                            lhsT_scale=group["scales"][:, P * n : P * n + P],
-                            rhs=weights["codes"][:, g, :].bitcast(FP8X4),
-                            rhs_scale=weights["scales"][:, g, :],
-                            start=(g == 0),
-                            stop=(g == PASSES - 1),
+
+                    def mark(s=s, half=half):
+                        for n in range(4 * half, 4 * half + 4):
+                            index = state["slot_index3"][:, 0:QUADS] if s == 3 else state["slot_index"][:, s]
+                            nc.vector.tensor_scalar(
+                                out=rows[:, :, 4 * n + s, 0:slots], in0=index[:, :, 0:slots], scalar1=float(n + 1),
+                                scalar2=None, op0=ALU.is_equal,
+                            )
+
+                    def fill(s=s, half=half):
+                        target = rows[:, :, :, 0:slots].rearrange("m q (n s) x -> m s n q x", s=4)[:, s, 4 * half : 4 * half + 4]
+                        value = state["slot_value"][:, s, :, 0:slots].unsqueeze(1).to_broadcast([P, 4, QUADS, slots])
+                        nc.vector.tensor_mul(out=target, in0=target, in1=value)
+
+                    actions.append(mark)
+                    actions.append(fill)
+            return actions
+
+        def finish(state, alone):
+            words = state["rows"][:].bitcast(F32)
+            actions = []
+            pending = []
+            for group in range(0, state["tiles"], TILES_PER_GROUP):
+                store = {}
+
+                def turn(pair, group=group, store=store):
+                    if pair == 0:
+                        store["basis"] = work.tile(
+                            [P, TILES_PER_GROUP, PASSES * P * PACK], BF16, align_bytes=64, name="basis"
+                        )
+                    for n in range(2 * pair, 2 * pair + 2):
+                        flipped = transposed.tile([P, PASSES, PAIRS, P], F32, tag="transposed", name="flipped")
+                        for g in range(PASSES):
+                            for u in range(PAIRS):
+                                gu = PAIRS * g + u
+                                nc.tensor.transpose(
+                                    flipped[:, g, u, :],
+                                    words[:, CLASSES * gu : CLASSES * (gu + 1), :, group + n].rearrange("m c k -> m (c k)"),
+                                    identity_f32[:],
+                                )
+                        nc.scalar.copy(
+                            out=store["basis"][:, n, :].bitcast(F32).rearrange("p (g m u) -> p g m u", g=PASSES, u=PAIRS),
+                            in_=flipped[:].rearrange("p g u m -> p g m u"),
                         )
 
-        def store_group(group):
-            result = work.tile([P, TILES_PER_GROUP, OUTS], F32, name="result")
-            for pair in range(TILES_PER_GROUP // 2):
-                if group["planes_done"]:
-                    nc.vector.tensor_copy(out=result[:, 2 * pair : 2 * pair + 2, :], in_=group["acc"][pair][:])
-                else:
-                    nc.scalar.copy(out=result[:, 2 * pair : 2 * pair + 2, :], in_=group["acc"][pair][:])
-            nc.sync.dma_start(out=out_rows[:, group["tile0"] : group["tile0"] + TILES_PER_GROUP, :], in_=result[:])
+                def quantise(store=store):
+                    store["codes"] = work.tile([P, GROUP_COLS], U32, align_bytes=64, name="codes")
+                    store["scales"] = work.tile([P, GROUP_COLS], U8, align_bytes=64, name="scales")
+                    nc.vector.quantize_mx(
+                        out=store["codes"][:].bitcast(FP8X4), scales=store["scales"][:],
+                        in_=store["basis"][:].rearrange("p s n -> p (s n)"),
+                    )
 
-        def run_later(now):
-            for entry in later:
-                if entry[0] == now:
-                    entry[1](entry[2])
+                def multiply(store=store):
+                    store["acc"] = []
+                    for pair in range(TILES_PER_GROUP // 2):
+                        acc = sums.tile([P, 2, OUTS], F32, name="acc")
+                        store["acc"].append(acc)
+                        for half in range(2):
+                            for g in range(PASSES):
+                                n = (2 * pair + half) * PASSES + g
+                                nc.tensor.matmul_mx(
+                                    out=acc[:, half, :],
+                                    lhsT=store["codes"][:, P * n : P * n + P].bitcast(FP8X4),
+                                    lhsT_scale=store["scales"][:, P * n : P * n + P],
+                                    rhs=w_codes[:, g, :].bitcast(FP8X4),
+                                    rhs_scale=w_scales[:, g, :],
+                                    start=(g == 0),
+                                    stop=(g == PASSES - 1),
+                                )
 
-        ticks = ALL_KNOTS + 1
-        finished = None
-        now = 0
-        for step in range(len(CHUNK_TILES)):
-            current = open_chunk(step)
-            done = 0
-            for j in range(ticks):
-                add_knot(current, j)
-                if j == PREPARE_AT and step + 1 < len(CHUNK_TILES):
-                    lay_out_x(nc.scalar.copy, step + 1)
-                if step == 0 and j in (PREPARE_AT + 4, PREPARE_AT + 8):
-                    turn_coefficients(nc, transposed, identity, coefficients, (j - PREPARE_AT) // 4 - 1)
-                if step == 0 and j == PREPARE_AT + 12:
-                    weights["codes"], weights["scales"] = quantise_coefficients(nc, const, coefficients)
-                if finished is not None:
-                    while done * ticks < (j + 1) * finished["tiles"]:
-                        finish_row_tiles(finished, done, False, now)
-                        done += 2
-                run_later(now)
-                now += 1
-            pick_larger(current)
-            finished = current
-        for a in range(0, finished["tiles"], 2):
-            finish_row_tiles(finished, a, True, now)
-            run_later(now)
-            now += 1
-        for tick in range(now, now + 3):
-            run_later(tick)
+                def send(group=group, store=store):
+                    result = work.tile([P, TILES_PER_GROUP, OUTS], F32, name="result")
+                    for pair in range(TILES_PER_GROUP // 2):
+                        if alone and pair == 1:
+                            nc.vector.tensor_copy(out=result[:, 2 * pair : 2 * pair + 2, :], in_=store["acc"][pair][:])
+                        else:
+                            nc.scalar.copy(out=result[:, 2 * pair : 2 * pair + 2, :], in_=store["acc"][pair][:])
+                    tile0 = state["first"] + group
+                    nc.sync.dma_start(out=out_rows[:, tile0 : tile0 + TILES_PER_GROUP, :], in_=result[:])
+
+                actions.append(lambda turn=turn: turn(0))
+                if pending:
+                    actions.append(pending.pop(0))
+                actions.append(lambda turn=turn: turn(1))
+                if pending:
+                    actions.append(pending.pop(0))
+                if pending:
+                    actions.append(pending.pop(0))
+                pending.extend([quantise, multiply, send])
+            return actions + pending
+
+        states = []
+        for n, tiles in enumerate(CHUNK_TILES):
+            states.append({"index": n, "first": sum(CHUNK_TILES[:n]), "tiles": tiles})
+
+        for number in range(STEP_BUFS):
+            load(number)
+        for action in look_up(states[0]) + work_out(states[0]) + look_up(states[1]):
+            action()
+        for n, state in enumerate(states):
+            side = [spread(state)]
+            if n + 1 < len(states):
+                side.append(work_out(states[n + 1]))
+            if n + 2 < len(states):
+                side.append(look_up(states[n + 2]))
+            if n > 0:
+                side.append(finish(states[n - 1], False))
+            for action in interleave(*side):
+                action()
+        for action in finish(states[-1], True):
+            action()

@@ -27,25 +27,27 @@ ROW_TILES = ROWS // P
 TILES_PER_GROUP = 4
 GROUP_COLS = TILES_PER_GROUP * PASSES * P
 
-STEPS = 34
-STEP_ROWS = STEPS + 1
+STEPS = 35
+LOW_STEPS = range(2, 6)
+STEP_ROWS = STEPS + len(LOW_STEPS)
 TRIPLE = 3
-X_ROW = TRIPLE * STEP_ROWS
+ONE_ROW = TRIPLE * STEP_ROWS
+X_ROW = ONE_ROW + 1
 GROUPS = 5
 BLOCKS = 2 * GROUPS + 1
 GEO = 6
 LOOK = 1 + TRIPLE * GEO
 LAST = 1 + GEO
 LOOK_SLOTS = GROUPS + 1
-Q_PAD = LOOK_SLOTS * TRIPLE
-CELL_BITS = 6
+CODE_BITS = 7
+FAR = 2.0**100
 
 CHUNK_TILES = (4, 12, 16, 16, 12, 4)
 SUB_TILES = 4
-STEP_BUFS = 3
-MAX_TILES = max(CHUNK_TILES)
+STEP_BUFS = 4
 QUARTER = 16
-PARK_TILES = 4
+PARK_HALF = 32
+PARK_TILES = 8
 
 FLOPS = 2 * ROWS * FEATURES * KNOTS * OUTS
 
@@ -53,60 +55,61 @@ FLOPS = 2 * ROWS * FEATURES * KNOTS * OUTS
 def load_knots(nc, pool, spline_knots):
     knots_bf = pool.tile([P, KNOTS], BF16)
     nc.sync.dma_start(out=knots_bf[:], in_=spline_knots.partition_broadcast(P))
-    knot = pool.tile([P, KNOTS + 8], F32)
+    knot = pool.tile([P, KNOTS + 9], F32)
     nc.vector.tensor_copy(out=knot[:, 2 : 2 + KNOTS], in_=knots_bf[:])
     for i in range(2):
         nc.vector.tensor_copy(out=knot[:, i : i + 1], in_=knots_bf[:, 0:1])
     step = pool.tile([P, 1], F32)
     nc.vector.tensor_sub(out=step[:], in0=knot[:, 3:4], in1=knot[:, 2:3])
-    for n in range(1, 7):
+    for n in range(1, 8):
         at = 2 + KNOTS - 1 + n
         nc.vector.tensor_scalar(
             out=knot[:, at : at + 1], in0=step[:], scalar1=float(n), scalar2=knot[:, 1 + KNOTS : 2 + KNOTS],
             op0=ALU.mult, op1=ALU.add,
         )
-    gap = pool.tile([P, KNOTS + 7], F32)
-    nc.vector.tensor_sub(out=gap[:], in0=knot[:, 1 : KNOTS + 8], in1=knot[:, 0 : KNOTS + 7])
-    return knot, gap
+    return knot
 
 
-def build_table(nc, const, pool, psum, identity_f32, knot, gap):
-    threshold_col = LOOK + 1
+def build_table(nc, const, pool, psum, identity_f32, knot):
+    level_col = LOOK + 1
     wide = pool.tile([P, LOOK + 2, P], F32)
     nc.vector.memset(wide[:], 0.0)
-
-    def steps(first):
-        return gap[:, first : first + STEPS]
-
-    def row(n):
-        return wide[:, 1 + n, 0:STEPS]
-
-    for n, first, sign in ((0, 2, -1.0), (1, 3, 1.0), (2, 1, -1.0), (3, 4, 1.0)):
-        nc.vector.tensor_scalar_mul(out=row(n), in0=steps(first), scalar1=sign)
-    nc.vector.tensor_sub(out=row(4), in0=steps(5), in1=steps(2))
-    nc.vector.tensor_sub(out=row(5), in0=steps(3), in1=steps(0))
-
-    def start(n):
-        return wide[:, 1 + n, STEPS : STEPS + 1]
-
-    for n, at, sign in ((0, 2, -1.0), (1, 3, 1.0), (2, 1, -1.0), (3, 4, 1.0)):
-        nc.vector.tensor_scalar_mul(out=start(n), in0=knot[:, at : at + 1], scalar1=sign)
-    nc.vector.tensor_sub(out=start(4), in0=knot[:, 5:6], in1=knot[:, 2:3])
-    nc.vector.tensor_sub(out=start(5), in0=knot[:, 3:4], in1=knot[:, 0:1])
-    for c in range(1, TRIPLE):
-        nc.vector.tensor_copy(
-            out=wide[:, 1 + GEO * c : 1 + GEO * (c + 1), STEP_ROWS * c : STEP_ROWS * (c + 1)],
-            in_=wide[:, 1 : 1 + GEO, 0:STEP_ROWS],
-        )
+    span = pool.tile([P, KNOTS + 6], F32)
+    nc.vector.tensor_sub(out=span[:], in0=knot[:, 3 : KNOTS + 9], in1=knot[:, 0 : KNOTS + 6])
+    cell = pool.tile([P, GEO, STEPS + 1], F32)
+    half = (STEPS + 1) // 2
+    for n, offsets in enumerate(((0, 1), (1, 0), (-1, 2), (2, -1))):
+        for odd in range(2):
+            first = 2 + odd + offsets[odd]
+            nc.vector.tensor_scalar_mul(
+                out=cell[:, n, odd : STEPS + 1 : 2], in0=knot[:, first : first + 2 * half - 1 : 2], scalar1=-1.0
+            )
+    for n, offsets in ((4, (0, -2)), (5, (-2, 0))):
+        for odd in range(2):
+            first = 2 + odd + offsets[odd]
+            nc.vector.tensor_copy(out=cell[:, n, odd : STEPS + 1 : 2], in_=span[:, first : first + 2 * half - 1 : 2])
+    changes = wide[:, 1 : 1 + GEO, 0:STEPS]
+    nc.vector.tensor_sub(out=changes, in0=cell[:, :, 1 : STEPS + 1], in1=cell[:, :, 0:STEPS])
+    low_rows = slice(LOW_STEPS[0] - 1, LOW_STEPS[-1])
+    rounded = pool.tile([P, GEO, len(LOW_STEPS)], BF16)
+    nc.vector.tensor_copy(out=rounded[:], in_=changes[:, :, low_rows])
+    nc.vector.tensor_sub(out=wide[:, 1 : 1 + GEO, STEPS:STEP_ROWS], in0=changes[:, :, low_rows], in1=rounded[:])
+    level = wide[:, level_col, 0:STEP_ROWS]
+    nc.vector.tensor_copy(out=level[:, 0:STEPS], in_=knot[:, 3 : 3 + STEPS])
+    nc.vector.tensor_copy(out=level[:, STEPS:STEP_ROWS], in_=knot[:, 2 + LOW_STEPS[0] : 3 + LOW_STEPS[-1]])
+    nc.vector.memset(wide[:, level_col, ONE_ROW : ONE_ROW + 1], -FAR)
     for c in range(TRIPLE):
-        for n, slope in ((0, 1.0), (1, -1.0), (2, 1.0), (3, -1.0)):
-            nc.vector.memset(wide[:, 1 + GEO * c + n, X_ROW + c : X_ROW + c + 1], slope)
-        nc.vector.memset(wide[:, 0, STEP_ROWS * c : STEP_ROWS * (c + 1)], float(2 ** (CELL_BITS * c)))
-        nc.vector.tensor_copy(
-            out=wide[:, threshold_col, STEP_ROWS * c : STEP_ROWS * c + STEPS], in_=knot[:, 3 : 3 + STEPS]
-        )
-        nc.vector.memset(wide[:, threshold_col, STEP_ROWS * c + STEPS : STEP_ROWS * (c + 1)], -(2.0**100))
-    nc.vector.memset(wide[:, LOOK, STEP_ROWS : STEP_ROWS * 2], 1.0)
+        rows = slice(STEP_ROWS * c, STEP_ROWS * (c + 1))
+        mine = slice(1 + GEO * c, 1 + GEO * (c + 1))
+        if c > 0:
+            nc.vector.tensor_copy(out=wide[:, mine, rows], in_=wide[:, 1 : 1 + GEO, 0:STEP_ROWS])
+            nc.vector.tensor_copy(out=wide[:, level_col, rows], in_=level)
+        nc.vector.tensor_copy(out=wide[:, mine, ONE_ROW : ONE_ROW + 1], in_=cell[:, :, 0:1])
+        nc.vector.memset(wide[:, 1 + GEO * c : 1 + GEO * c + 4, X_ROW + c : X_ROW + c + 1], 1.0)
+        for col, unit in ((0, 2.0 ** (CODE_BITS * c)), (LOOK, float(c == 1))):
+            for n, change in enumerate((1.0, 2.0, 4.0, 1.0)):
+                if unit > 0:
+                    nc.vector.memset(wide[:, col, STEP_ROWS * c + n : STEP_ROWS * c + STEPS : 4], change * unit)
 
     table = const.tile([P, LOOK + LAST], BF16)
     threshold = const.tile([P, 1], F32)
@@ -115,73 +118,49 @@ def build_table(nc, const, pool, psum, identity_f32, knot, gap):
         flipped = psum.tile([P, 4, P], F32, tag="transposed", name="flipped_table")
         for b in range(count):
             nc.tensor.transpose(flipped[:, b, :], wide[:, first + b, :], identity_f32[:])
-        last = min(first + count, threshold_col)
-        if last > first:
-            nc.vector.tensor_copy(out=table[:, first:last], in_=flipped[:, 0 : last - first, 0])
-        if first + count > threshold_col:
-            nc.vector.tensor_copy(out=threshold[:], in_=flipped[:, threshold_col - first, 0:1])
+        in_table = min(count, level_col - first)
+        if in_table > 0:
+            nc.vector.tensor_copy(out=table[:, first : first + in_table], in_=flipped[:, 0:in_table, 0])
+        if count > in_table:
+            nc.vector.tensor_copy(out=threshold[:], in_=flipped[:, count - 1 : count, 0])
     nc.vector.tensor_copy(out=table[:, LOOK + 1 : LOOK + LAST], in_=table[:, 1 + GEO : 1 + 2 * GEO])
     return table, threshold
 
 
-def park_x(nc, pool, psum, identity, knot, x, parked):
-    x_rows = pool.tile([P, ROW_TILES, FEATURES], BF16)
-    nc.sync.dma_start(out=x_rows[:], in_=x.rearrange("(m a) i -> m a i", a=ROW_TILES))
-    clamped = pool.tile([P, ROW_TILES, FEATURES], BF16)
-    turned = pool.tile([P, ROW_TILES // 4, P], BF16)
-    for quarter in range(ROW_TILES // QUARTER):
-        tiles = slice(QUARTER * quarter, QUARTER * (quarter + 1))
-        by_e = x_rows[:, tiles, :].rearrange("m a (u e c) -> m e a u c", e=2, c=CLASSES)
+def park_x(nc, pool, psum, identity, knot, x_rows, parked, quarter):
+    tiles = slice(QUARTER * quarter, QUARTER * (quarter + 1))
+    clamped = pool.tile([P, QUARTER, FEATURES], BF16, name="clamped%d" % quarter)
+
+    engine = nc.vector if quarter == 0 else nc.gpsimd
+
+    def clamp(out_columns, in_columns):
+        engine.tensor_scalar(
+            out=clamped[:, :, out_columns], in0=x_rows[:, tiles, in_columns],
+            scalar1=knot[:, 38:39], scalar2=knot[:, 2:3], op0=ALU.min, op1=ALU.max,
+        )
+
+    cuts = sorted(set(list(range(0, QUADS - 1, CLASSES)) + list(range(0, QUADS, GROUPS))))
+    for q0, q1 in zip(cuts[:-1], cuts[1:]):
+        g, c = q0 % GROUPS, 2 - q0 // GROUPS
         for e in range(2):
-            first = TRIPLE * GROUPS * e
-            nc.vector.tensor_scalar(
-                out=clamped[:, tiles, first : first + QUADS].rearrange("m a (u c) -> m a u c", c=CLASSES),
-                in0=by_e[:, e], scalar1=knot[:, 2:3], scalar2=knot[:, 38:39], op0=ALU.max, op1=ALU.min,
-            )
-        nc.vector.tensor_scalar(
-            out=clamped[:, tiles, FEATURES - 2 : FEATURES], in0=x_rows[:, tiles, FEATURES - 5 : FEATURES : 4],
-            scalar1=knot[:, 2:3], scalar2=knot[:, 38:39], op0=ALU.max, op1=ALU.min,
-        )
-        flipped = psum.tile([P, 4, P], BF16, tag="transposed", name="flipped_x")
-        for n in range(4):
-            first = QUARTER * quarter + 4 * n
-            nc.tensor.transpose(
-                flipped[:, n, :], clamped[:, first : first + 4, :].rearrange("m a i -> m (a i)"), identity[:]
-            )
-        nc.scalar.copy(out=turned[:, 4 * quarter : 4 * quarter + 4, :], in_=flipped[:])
-        words = turned[:].bitcast(F32)
-        queue = nc.sync if quarter == 0 else nc.gpsimd
-        for b in range(4):
-            queue.dma_start(
-                out=parked[:, quarter, :].rearrange("r (n b w) -> r n b w", n=4, b=4)[:, :, b, :],
-                in_=words[FEATURES * b : FEATURES * (b + 1), 4 * quarter : 4 * quarter + 4, :],
-            )
-
-
-def prepare_coefficients(nc, const, pool, psum, identity, spline_coeffs):
-    halves = OUTS // P
-    natural = pool.tile([P, halves, FEATURES * KNOTS], BF16)
-    for h in range(halves):
-        nc.sync.dma_start(
-            out=natural[:, h, :].rearrange("q (i k) -> q i k", k=KNOTS),
-            in_=spline_coeffs[:, P * h : P * h + P, :].rearrange("i q k -> q i k"),
-        )
-    grouped = pool.tile([P, PASSES, OUTS, PACK], BF16, align_bytes=64)
-    for g in range(PASSES):
-        flipped = psum.tile([P, PACK, OUTS], BF16, tag="transposed", name="flipped_w")
-        for t in range(PACK):
-            for h in range(halves):
-                first = (PACK * g + t) * P
-                nc.tensor.transpose(flipped[:, t, P * h : P * h + P], natural[:, h, first : first + P], identity[:])
-        nc.scalar.copy(out=grouped[:, g, :, :], in_=flipped[:].rearrange("p t o -> p o t"))
-    codes = const.tile([P, PASSES, OUTS], U32, align_bytes=64)
-    scales = const.tile([P, PASSES, OUTS], U8, align_bytes=64)
-    nc.vector.quantize_mx(
-        out=codes[:].rearrange("p g o -> p (g o)").bitcast(FP8X4),
-        scales=scales[:].rearrange("p g o -> p (g o)"),
-        in_=grouped[:].rearrange("p g o t -> p (g o t)"),
-    )
-    return codes, scales
+            r = 3 * (GROUPS * e + g) + c
+            i = 8 * (q0 // CLASSES) + 4 * e + q0 % CLASSES
+            count = q1 - q0
+            clamp(slice(r, r + 3 * count - 2, 3), slice(i, i + count))
+    clamp(slice(FEATURES - 2, FEATURES), slice(FEATURES - 5, FEATURES, 4))
+    flipped = psum.tile([P, 4, P], BF16, tag="transposed", name="flipped_x")
+    for n in range(4):
+        nc.tensor.transpose(flipped[:, n, :], clamped[:, 4 * n : 4 * n + 4, :].rearrange("m a i -> m (a i)"), identity[:])
+    turned = pool.tile([P, 4, P], BF16, name="turned%d" % quarter)
+    nc.scalar.copy(out=turned[:], in_=flipped[:])
+    words = turned[:].bitcast(F32)
+    queue = nc.sync if quarter == 0 else nc.gpsimd
+    size = QUARTER * P // 2
+    at = quarter % 2 * size
+    place = parked[:, quarter // 2, at : at + size].rearrange("r (n b w) -> r n b w", n=4, b=4)
+    for b in range(4):
+        queue.dma_start(out=place[0:FEATURES, :, b, :], in_=words[FEATURES * b : FEATURES * (b + 1)])
+    queue.dma_start(out=place[FEATURES].rearrange("n b w -> b n w"), in_=words[FEATURES - 1 : P : FEATURES])
 
 
 def interleave(*lists):
@@ -199,291 +178,365 @@ def tile_kanlayer_t_kernel(tc, x, spline_coeffs, spline_knots, out):
         planes = ctx.enter_context(tc.tile_pool(name="planes", bufs=1))
         keys = ctx.enter_context(tc.tile_pool(name="keys", bufs=1))
         carried = ctx.enter_context(tc.tile_pool(name="carried", bufs=2))
-        transposed = ctx.enter_context(tc.psum_pool(name="transposed", bufs=2))
-        lookups = ctx.enter_context(tc.psum_pool(name="lookups", bufs=1))
+        rows_pool = ctx.enter_context(tc.tile_pool(name="rows", bufs=2))
+        transposed = ctx.enter_context(tc.psum_pool(name="transposed", bufs=4))
+        lookups = ctx.enter_context(tc.psum_pool(name="lookups", bufs=2))
         sums = ctx.enter_context(tc.psum_pool(name="sums", bufs=2))
 
         identity = const.tile([P, P], BF16)
         make_identity(nc, identity[:])
         identity_f32 = const.tile([P, P], F32)
         make_identity(nc, identity_f32[:])
-        x_steps = []
-        for n in range(STEP_BUFS):
-            x_steps.append(const.tile([P, BLOCKS, SUB_TILES * P], BF16, name="x_steps%d" % n))
-            nc.gpsimd.memset(x_steps[n][:].bitcast(U32), 0)
-        raws = [const.tile([P, LOOK * LOOK_SLOTS * 2 * MAX_TILES], F32, name="raw%d" % n) for n in range(2)]
-        ones = const.tile([P, P], F32)
-        nc.gpsimd.memset(ones[:], 1.0)
-        banks = []
-        for n in range(2):
-            banks.append(lookups.tile([P, 4 * P], F32, name="bank%d" % n))
-            for b in range(4):
-                nc.tensor.transpose(banks[n][:, P * b : P * (b + 1)], ones[:], identity_f32[:])
+        x_steps = [const.tile([P, BLOCKS, SUB_TILES * P], BF16, name="x_steps%d" % n) for n in range(STEP_BUFS)]
+        w_codes = const.tile([P, PASSES, OUTS], U32, align_bytes=64)
+        w_scales = const.tile([P, PASSES, OUTS], U8, align_bytes=64)
 
         out_rows = out.rearrange("(m a) o -> m a o", a=ROW_TILES)
-        parked = out_rows[:, ROW_TILES - PARK_TILES : ROW_TILES, :].rearrange("(r h) a o -> r h (a o)", h=ROW_TILES // QUARTER)
+        parked = out_rows[:, ROW_TILES - PARK_TILES : ROW_TILES, :].rearrange("(r h) a o -> r h (a o)", h=ROW_TILES // PARK_HALF)
 
-        with tc.tile_pool(name="setup", bufs=1) as setup:
-            knot, gap = load_knots(nc, setup, spline_knots)
-            park_x(nc, setup, transposed, identity, knot, x, parked)
-            table, threshold = build_table(nc, const, setup, transposed, identity_f32, knot, gap)
-            w_codes, w_scales = prepare_coefficients(nc, const, setup, transposed, identity, spline_coeffs)
+        pools = {}
 
-        rows_pool = ctx.enter_context(tc.tile_pool(name="rows", bufs=2))
-        work = ctx.enter_context(tc.tile_pool(name="work", bufs=2))
+        def prepare_coefficients(setup):
+            halves = OUTS // P
+            natural = setup.tile([P, halves, FEATURES * KNOTS], BF16)
+            grouped = setup.tile([P, PASSES, OUTS, PACK], BF16, align_bytes=64)
+            flips = {}
 
-        def load(number):
-            steps = x_steps[number % STEP_BUFS]
-            tile0 = SUB_TILES * number
-            words = slice((tile0 % QUARTER) * P // 2, (tile0 % QUARTER + SUB_TILES) * P // 2)
-            source = parked[:, tile0 // QUARTER, words]
-            target = steps[:].bitcast(F32)
-            for c in range(TRIPLE):
-                blocks = BLOCKS if c < 2 else BLOCKS - 1
-                nc.sync.dma_start(
-                    out=target[STEP_ROWS * c : STEP_ROWS * (c + 1), 0:blocks, :],
-                    in_=source[c : c + 3 * blocks - 2 : 3, :].partition_broadcast(STEP_ROWS),
-                )
-            nc.sync.dma_start(
-                out=target[X_ROW : X_ROW + TRIPLE, 0 : BLOCKS - 1, :],
-                in_=source[0 : 3 * (BLOCKS - 1), :].rearrange("(g c) w -> c g w", c=TRIPLE),
-            )
-            nc.sync.dma_start(out=target[X_ROW : X_ROW + 2, BLOCKS - 1, :], in_=source[FEATURES - 2 : FEATURES, :])
-
-        def look_up(state):
-            actions = []
-            size = LOOK * LOOK_SLOTS * 2 * state["tiles"]
-            raw = raws[state["index"] % 2][:, 0:size].rearrange("m (w g s) -> m w g s", w=LOOK, g=LOOK_SLOTS)
-            state["raw"] = raw
-            for first in range(0, state["tiles"], SUB_TILES):
-                number = (state["first"] + first) // SUB_TILES
-                steps = x_steps[number % STEP_BUFS]
-
-                def compare(steps=steps):
-                    nc.vector.tensor_scalar(
-                        out=steps[0:X_ROW, :, :], in0=steps[0:X_ROW, :, :], scalar1=threshold[0:X_ROW, :], scalar2=None,
-                        op0=ALU.is_ge,
+            def fetch():
+                for h in range(halves):
+                    nc.gpsimd.dma_start(
+                        out=natural[:, h, :].rearrange("q (i k) -> q i k", k=KNOTS),
+                        in_=spline_coeffs[:, P * h : P * h + P, :].rearrange("i q k -> q i k"),
                     )
 
-                actions.append(compare)
-                for pair in range(0, SUB_TILES, 2):
-
-                    def multiply(first=first, steps=steps, pair=pair):
-                        bank = banks[(first + pair) // 2 % 2]
-                        slots = bank[:, 0 : LOOK * LOOK_SLOTS * 4].rearrange("m (w g a e) -> m w g a e", w=LOOK, g=LOOK_SLOTS, a=2)
-                        for half in range(2):
-                            columns = slice(P * (pair + half), P * (pair + half + 1))
-                            for e in range(2):
-                                for g in range(GROUPS):
-                                    nc.tensor.matmul(
-                                        slots[:, :, g, half, e], lhsT=steps[:, GROUPS * e + g, columns],
-                                        rhs=table[:, 0:LOOK], start=True, stop=True,
-                                    )
-                                nc.tensor.matmul(
-                                    slots[:, 0:LAST, GROUPS, half, e], lhsT=steps[:, BLOCKS - 1, columns],
-                                    rhs=table[:, LOOK * e : LOOK * e + LAST], start=True, stop=True,
-                                )
-                        at = 2 * (first + pair)
-                        nc.scalar.copy(
-                            out=raw[:, :, :, at : at + 4],
-                            in_=bank[:, 0 : LOOK * LOOK_SLOTS * 4].rearrange("m (w g s) -> m w g s", w=LOOK, g=LOOK_SLOTS),
+            def turn(g):
+                flips[g] = transposed.tile([P, PACK, OUTS], BF16, tag="transposed", name="flipped_w")
+                for t in range(PACK):
+                    for h in range(halves):
+                        first = (PACK * g + t) * P
+                        nc.tensor.transpose(
+                            flips[g][:, t, P * h : P * h + P], natural[:, h, first : first + P], identity[:]
                         )
 
-                    actions.append(multiply)
+            def group(g):
+                nc.scalar.copy(out=grouped[:, g, :, :], in_=flips[g][:].rearrange("p t o -> p o t"))
+
+            def quantise():
+                nc.vector.quantize_mx(
+                    out=w_codes[:].rearrange("p g o -> p (g o)").bitcast(FP8X4),
+                    scales=w_scales[:].rearrange("p g o -> p (g o)"),
+                    in_=grouped[:].rearrange("p g o t -> p (g o t)"),
+                )
+
+            return fetch, [lambda: turn(0), lambda: turn(1), lambda: group(0), lambda: group(1), quantise]
+
+        def load(number):
+            tile0 = SUB_TILES * number
+            words = slice((tile0 % PARK_HALF) * P // 2, (tile0 % PARK_HALF + SUB_TILES) * P // 2)
+            source = parked[0 : TRIPLE * BLOCKS, tile0 // PARK_HALF, words].rearrange("(g c) w -> c g w", c=TRIPLE)
+            target = x_steps[number % STEP_BUFS][:].bitcast(F32)
+            for c in range(TRIPLE):
+                nc.sync.dma_start(
+                    out=target[STEP_ROWS * c : STEP_ROWS * (c + 1), :, :], in_=source[c].partition_broadcast(STEP_ROWS)
+                )
+            for c, first, last in ((0, ONE_ROW, X_ROW + 1), (1, X_ROW + 1, X_ROW + 2), (2, X_ROW + 2, P)):
+                nc.sync.dma_start(out=target[first:last, :, :], in_=source[c].partition_broadcast(last - first))
+
+        def look_up(state):
+            slots = 2 * state["tiles"]
+            actions = []
+            banks = {}
+
+            def start():
+                state["cell"] = carried.tile([P, LOOK_SLOTS, slots], U32, name="cell")
+                state["geo"] = carried.tile([P, GEO, QUADS, slots], F32, name="geo")
+
+            def compare(number):
+                steps = x_steps[number % STEP_BUFS]
+                mine = steps[0:X_ROW, :, :]
+                nc.vector.tensor_scalar(
+                    out=mine, in0=mine, scalar1=threshold[0:X_ROW, :], scalar2=None, op0=ALU.is_ge
+                )
+
+            def multiply(pair, number):
+                steps = x_steps[number % STEP_BUFS]
+                bank = lookups.tile([P, LOOK, LOOK_SLOTS, 2, 2], F32, name="bank")
+                banks[pair] = bank
+                for half in range(2):
+                    tile = pair + half - SUB_TILES * number + state["first"]
+                    columns = slice(P * tile, P * (tile + 1))
+                    for e in range(2):
+                        for g in range(GROUPS):
+                            nc.tensor.matmul(
+                                bank[:, :, g, half, e], lhsT=steps[:, GROUPS * e + g, columns],
+                                rhs=table[:, 0:LOOK], start=True, stop=True,
+                            )
+                        nc.tensor.matmul(
+                            bank[:, 0:LAST, GROUPS, half, e], lhsT=steps[:, BLOCKS - 1, columns],
+                            rhs=table[:, LOOK * e : LOOK * e + LAST], start=True, stop=True,
+                        )
+
+            def evacuate(pair):
+                bank = banks[pair][:].rearrange("m w g a e -> m w g (a e)")
+                at = slice(2 * pair, 2 * pair + 4)
+                nc.scalar.activation(out=state["cell"][:, :, at], in_=bank[:, 0], func=ACT.Copy)
+                for c in range(TRIPLE):
+                    count = LOOK_SLOTS if c == 0 else GROUPS
+                    q0 = GROUPS * (2 - c)
+                    nc.scalar.activation(
+                        out=state["geo"][:, :, q0 : q0 + count, at],
+                        in_=bank[:, 1 + GEO * c : 1 + GEO * (c + 1), 0:count, :], func=ACT.Abs,
+                    )
+
+            actions.append(start)
+            for first in range(0, state["tiles"], SUB_TILES):
+                number = (state["first"] + first) // SUB_TILES
+                actions.append(lambda number=number: compare(number))
+                for pair in range(first, first + SUB_TILES, 2):
+                    actions.append(lambda pair=pair, number=number: multiply(pair, number))
+                for pair in range(first, first + SUB_TILES, 2):
+                    actions.append(lambda pair=pair: evacuate(pair))
                 if SUB_TILES * (number + STEP_BUFS) < ROW_TILES:
                     actions.append(lambda number=number: load(number + STEP_BUFS))
             return actions
 
         def work_out(state):
             slots = 2 * state["tiles"]
-            raw = state["raw"]
-
-            def column(n):
-                return raw[:, 1 + n : 1 + n + 2 * GEO + 1 : GEO, :, 0:slots]
-
-            def plane(name):
-                return planes.tile([P, TRIPLE, LOOK_SLOTS, slots], F32, name=name)
-
-            def every(tile):
-                return tile[:, :, :, 0:slots]
-
-            def used(tile):
-                return tile[:, :, :, 0:slots]
-
-            def by_quad(tile):
-                return tile[:, :, :, 0:slots].rearrange("m c g s -> m g c s")
-
-            def quads(tile):
-                return tile[:, :, 0:slots].rearrange("m (g c) s -> m g c s", c=TRIPLE)
-
+            lanes = QUADS * slots
             vec = nc.vector
+            act = nc.scalar.activation
             t = {}
 
-            def sums_of_distances():
-                for name in ("length", "double", "lower", "upper", "third", "first"):
-                    t[name] = plane(name)
-                vec.tensor_add(out=every(t["length"]), in0=column(0), in1=column(1))
-                vec.tensor_add(out=every(t["lower"]), in0=column(2), in1=column(1))
-                vec.tensor_add(out=every(t["upper"]), in0=column(0), in1=column(3))
-                vec.tensor_add(out=every(t["double"]), in0=column(2), in1=column(3))
-                nc.scalar.activation(out=every(t["third"]), in_=column(4), func=ACT.Abs_reciprocal_sqrt)
-                nc.scalar.activation(out=every(t["first"]), in_=column(5), func=ACT.Abs_reciprocal_sqrt)
+            def by_n():
+                return state["geo"][:].rearrange("m n q s -> m n (q s)")
 
-            def cells():
-                cell = keys.tile([P, LOOK_SLOTS, slots], I32, name="cell")
-                vec.tensor_copy(out=cell[:, :, 0:slots], in_=raw[:, 0, :, 0:slots])
-                own = keys.tile([P, TRIPLE, LOOK_SLOTS, slots], I32, name="own")
-                state["slot_index3"] = carried.tile([P, Q_PAD, slots], BF16, name="slot_index3")
-                for c in range(TRIPLE):
-                    vec.tensor_scalar(
-                        out=own[:, c, :, 0:slots], in0=cell[:, :, 0:slots], scalar1=CELL_BITS * c, scalar2=2**CELL_BITS - 1,
-                        op0=ALU.logical_shift_right, op1=ALU.bitwise_and,
-                    )
-                for name, shift, mask in (("bit0", 0, 1), ("bit1", 1, 1), ("four", 2, 15)):
-                    part = keys.tile([P, TRIPLE, LOOK_SLOTS, slots], I32, name="part_" + name)
-                    vec.tensor_scalar(
-                        out=used(part), in0=used(own), scalar1=shift, scalar2=mask,
-                        op0=ALU.logical_shift_right, op1=ALU.bitwise_and,
-                    )
-                    if name == "four":
-                        t[name] = state["slot_index3"]
-                    else:
-                        t[name] = keys.tile([P, Q_PAD, slots], BF16, name=name)
-                    nc.scalar.activation(out=quads(t[name]), in_=by_quad(part[:].bitcast(U32)), func=ACT.Copy)
+            def twice(one):
+                return one.unsqueeze(1).to_broadcast([P, 2, lanes])
 
-            def products():
-                vec.tensor_mul(out=used(t["upper"]), in0=used(t["length"]), in1=used(t["upper"]))
-                vec.tensor_mul(out=used(t["lower"]), in0=used(t["length"]), in1=used(t["lower"]))
-                for name in ("third", "first"):
-                    nc.scalar.activation(out=used(t[name]), in_=used(t[name]), func=ACT.Square)
-                for name in ("upper", "lower", "double"):
-                    nc.scalar.activation(out=used(t[name]), in_=used(t[name]), func=ACT.Abs_reciprocal_sqrt)
-                nc.scalar.activation(out=used(t["double"]), in_=used(t["double"]), func=ACT.Square)
+            def left_sums():
+                t["left"] = planes.tile([P, 2, lanes], F32, name="left")
+                vec.tensor_add(out=t["left"][:], in0=by_n()[:, 0:3:2], in1=twice(by_n()[:, 1]))
 
-            def ratios():
-                vec.tensor_mul(out=every(t["third"]), in0=column(0), in1=every(t["third"]))
+            def right_sums():
+                t["right"] = planes.tile([P, 3, lanes], F32, name="right")
+                vec.tensor_add(out=t["right"][:, 0:2], in0=by_n()[:, 0:3:2], in1=twice(by_n()[:, 3]))
+
+            def outer_roots():
+                t["outer"] = planes.tile([P, 2, lanes], F32, name="outer")
+                act(out=t["outer"][:], in_=by_n()[:, 4:6], func=ACT.Abs_reciprocal_sqrt)
+
+            def outer_squares():
+                act(out=t["outer"][:], in_=t["outer"][:], func=ACT.Square)
+
+            def upper_product():
+                vec.tensor_mul(out=t["right"][:, 0], in0=t["left"][:, 0], in1=t["right"][:, 0])
+
+            def lower_product():
+                vec.tensor_mul(out=t["right"][:, 2], in0=t["left"][:, 0], in1=t["left"][:, 1])
+
+            def right_roots():
+                act(out=t["right"][:], in_=t["right"][:], func=ACT.Abs_reciprocal_sqrt)
+
+            def middle_square():
+                act(out=t["right"][:, 1], in_=t["right"][:, 1], func=ACT.Square)
+
+            def outer_ratios():
+                vec.tensor_mul(out=t["outer"][:], in0=by_n()[:, 0:2], in1=t["outer"][:])
+
+            def inner_ratios():
+                vec.tensor_mul(out=t["right"][:, 0:2], in0=by_n()[:, 0:3:2], in1=t["right"][:, 0:2])
+
+            def low_ratio():
+                vec.tensor_mul(out=t["right"][:, 2], in0=by_n()[:, 1], in1=t["right"][:, 2])
+
+            def quadratics():
+                act(out=t["right"][:, 0:3:2], in_=t["right"][:, 0:3:2], func=ACT.Square)
+
+            def cubics():
+                vec.tensor_mul(out=t["outer"][:], in0=t["right"][:, 0:3:2], in1=t["outer"][:])
+
+            def cubics_out():
+                t["values"] = keys.tile([P, 4, lanes], BF16, name="values")
+                act(out=t["values"][:, 0:3:2], in_=t["outer"][:], func=ACT.Copy)
+
+            def both_quadratics():
+                vec.tensor_add(out=t["left"][:, 0], in0=t["right"][:, 0], in1=t["right"][:, 2])
+
+            def middle():
                 vec.scalar_tensor_tensor(
-                    out=every(t["first"]), in0=column(1), scalar=0.0, in1=every(t["first"]), op0=ALU.max, op1=ALU.mult
-                )
-                vec.tensor_mul(out=every(t["upper"]), in0=column(0), in1=every(t["upper"]))
-                vec.tensor_mul(out=every(t["lower"]), in0=column(1), in1=every(t["lower"]))
-                vec.tensor_mul(out=every(t["double"]), in0=column(2), in1=every(t["double"]))
-                for name in ("upper", "lower"):
-                    nc.scalar.activation(out=used(t[name]), in_=used(t[name]), func=ACT.Square)
-
-            def values():
-                four = keys.tile([P, 4, Q_PAD, slots], BF16, name="values")
-                t["values"] = four
-                upper, lower, double, third, first, length = (
-                    used(t[name]) for name in ("upper", "lower", "double", "third", "first", "length")
-                )
-                vec.tensor_mul(out=third, in0=upper, in1=third)
-                vec.tensor_mul(out=first, in0=lower, in1=first)
-                vec.tensor_add(out=length, in0=upper, in1=lower)
-                vec.scalar_tensor_tensor(out=length, in0=length, scalar=1.0, in1=double, op0=ALU.subtract, op1=ALU.mult)
-                vec.tensor_sub(out=upper, in0=upper, in1=length)
-                vec.tensor_sub(out=quads(four[:, 2]), in0=by_quad(t["upper"]), in1=by_quad(t["third"]))
-                vec.tensor_add(out=length, in0=upper, in1=first)
-                nc.scalar.activation(out=quads(four[:, 3]), in_=by_quad(t["third"]), func=ACT.Copy)
-                nc.scalar.activation(out=quads(four[:, 0]), in_=by_quad(t["first"]), func=ACT.Copy)
-                nc.scalar.activation(
-                    out=quads(four[:, 1]), in_=by_quad(t["length"]), func=ACT.Copy, scale=-1.0, bias=1.0
+                    out=t["left"][:, 0], in0=t["left"][:, 0], scalar=1.0, in1=t["right"][:, 1],
+                    op0=ALU.subtract, op1=ALU.mult,
                 )
 
-            def slot_indices():
-                def bits(name):
-                    return t[name][:, 0:QUADS, 0:slots]
+            def upper_sum():
+                vec.tensor_sub(out=t["right"][:, 0], in0=t["right"][:, 0], in1=t["left"][:, 0])
 
-                index = carried.tile([P, 3, QUADS, slots], BF16, name="index")
-                state["slot_index"] = index
-                either = keys.tile([P, QUADS, slots], BF16, name="either")
-                both = keys.tile([P, QUADS, slots], BF16, name="both")
-                vec.tensor_max(out=either[:, :, 0:slots], in0=bits("bit0"), in1=bits("bit1"))
-                vec.tensor_mul(out=both[:, :, 0:slots], in0=bits("bit0"), in1=bits("bit1"))
-                vec.tensor_add(out=index[:, 1, :, 0:slots], in0=bits("four"), in1=bits("bit1"))
-                vec.tensor_add(out=index[:, 0, :, 0:slots], in0=bits("four"), in1=either[:, :, 0:slots])
-                vec.tensor_add(out=index[:, 2, :, 0:slots], in0=bits("four"), in1=both[:, :, 0:slots])
+            def other_sum():
+                vec.tensor_add(out=t["left"][:, 1], in0=t["right"][:, 0], in1=t["outer"][:, 1])
 
-            def rotate(source, bit, by, target):
-                shape = [P, 4, QUADS, slots]
-                flag = t[bit][:, 0:QUADS, 0:slots].unsqueeze(1).to_broadcast(shape)
-                moved = keys.tile([P, 4, QUADS, slots], BF16, name="moved")
-                kept = source
-                whole = source[:, :, 0:QUADS, 0:slots]
-                vec.tensor_mul(out=moved[:, :, :, 0:slots], in0=whole, in1=flag)
-                vec.tensor_sub(out=whole, in0=whole, in1=moved[:, :, :, 0:slots])
+            def third_value():
+                vec.tensor_sub(out=t["values"][:, 3], in0=t["right"][:, 0], in1=t["outer"][:, 0])
+
+            def second_value():
+                act(out=t["values"][:, 1], in_=t["left"][:, 1], func=ACT.Copy, scale=-1.0, bias=1.0)
+
+            def own_cell(c):
+                if c == 0:
+                    t["own"] = keys.tile([P, QUADS, slots], I32, name="own")
+                count = LOOK_SLOTS if c == 0 else GROUPS
+                q0 = GROUPS * (2 - c)
+                vec.tensor_scalar(
+                    out=t["own"][:, q0 : q0 + count], in0=state["cell"][:, 0:count].bitcast(I32),
+                    scalar1=CODE_BITS * c, scalar2=2**CODE_BITS - 1, op0=ALU.logical_shift_right, op1=ALU.bitwise_and,
+                )
+
+            def part(at, shift, mask):
+                if at == 0:
+                    t["parts"] = keys.tile([P, 4, lanes], I32, name="parts")
+                vec.tensor_scalar(
+                    out=t["parts"][:, at], in0=t["own"][:].rearrange("m q s -> m (q s)"), scalar1=shift, scalar2=mask,
+                    op0=ALU.logical_shift_right, op1=ALU.bitwise_and,
+                )
+
+            def parts_out():
+                t["bits"] = keys.tile([P, 5, lanes], BF16, name="bits")
+                act(out=t["bits"][:, 1:5], in_=t["parts"][:].bitcast(U32), func=ACT.Copy)
+
+            def slot0_index():
+                t["index"] = carried.tile([P, 4, lanes], BF16, name="index")
+                act(out=t["index"][:, 0], in_=t["parts"][:, 3].bitcast(U32), func=ACT.Copy, bias=1.0)
+
+            def swap_flag():
+                vec.tensor_sub(out=t["bits"][:, 0], in0=t["bits"][:, 1], in1=t["bits"][:, 3])
+
+            def slot_index():
                 vec.tensor_add(
-                    out=target[:, by:4, :, 0:slots], in0=kept[:, by:4, 0:QUADS, 0:slots], in1=moved[:, 0 : 4 - by, :, 0:slots]
+                    out=t["index"][:, 1:4], in0=t["bits"][:, 1:4],
+                    in1=t["bits"][:, 4].unsqueeze(1).to_broadcast([P, 3, lanes]),
                 )
+
+            def pairs(tile):
+                return tile.rearrange("m (p h) n -> m p h n", h=2)
+
+            def take():
+                t["moved"] = keys.tile([P, 4, lanes], BF16, name="moved")
+                flags = t["bits"][:, 0:3:2].unsqueeze(2).to_broadcast([P, 2, 2, lanes])
+                vec.tensor_mul(out=pairs(t["moved"][:]), in0=pairs(t["values"][:]), in1=flags)
+
+            def keep():
+                vec.tensor_sub(out=t["values"][:], in0=t["values"][:], in1=t["moved"][:])
+
+            def join(h):
+                if h == 0:
+                    t["slot_values"] = carried.tile([P, 4, lanes], BF16, name="slot_values")
                 vec.tensor_add(
-                    out=target[:, 0:by, :, 0:slots], in0=kept[:, 0:by, 0:QUADS, 0:slots], in1=moved[:, 4 - by : 4, :, 0:slots]
+                    out=t["slot_values"][:, 2 * h : 2 * h + 2], in0=pairs(t["values"][:])[:, :, h],
+                    in1=pairs(t["moved"][:])[:, :, 1 - h],
                 )
 
-            def first_turn():
-                t["half_turned"] = keys.tile([P, 4, QUADS, slots], BF16, name="half_turned")
-                rotate(t["values"], "bit0", 1, t["half_turned"])
+            def hand_over():
+                state["values"] = t["slot_values"]
+                state["index"] = t["index"]
 
-            def second_turn():
-                state["slot_value"] = carried.tile([P, 4, QUADS, slots], BF16, name="slot_value")
-                rotate(t["half_turned"], "bit1", 2, state["slot_value"])
-
-            return [sums_of_distances, cells, products, slot_indices, ratios, values, first_turn, second_turn]
+            return [
+                left_sums,
+                outer_roots,
+                right_sums,
+                lambda: own_cell(0),
+                outer_squares,
+                upper_product,
+                lambda: own_cell(1),
+                lower_product,
+                lambda: own_cell(2),
+                right_roots,
+                lambda: part(0, 0, 1),
+                lambda: part(1, 1, 1),
+                outer_ratios,
+                lambda: part(2, 2, 1),
+                lambda: part(3, 3, 15),
+                middle_square,
+                parts_out,
+                inner_ratios,
+                low_ratio,
+                slot0_index,
+                quadratics,
+                swap_flag,
+                slot_index,
+                cubics,
+                both_quadratics,
+                cubics_out,
+                middle,
+                upper_sum,
+                other_sum,
+                third_value,
+                second_value,
+                take,
+                keep,
+                lambda: join(0),
+                lambda: join(1),
+                hand_over,
+            ]
 
         def spread(state):
             slots = 2 * state["tiles"]
-            state["rows"] = rows_pool.tile([P, QUADS, KNOTS, slots], BF16, name="rows")
-            rows = state["rows"]
-            actions = []
-            for s in range(4):
-                for half in range(2):
 
-                    def mark(s=s, half=half):
-                        for n in range(4 * half, 4 * half + 4):
-                            index = state["slot_index3"][:, 0:QUADS] if s == 3 else state["slot_index"][:, s]
-                            nc.vector.tensor_scalar(
-                                out=rows[:, :, 4 * n + s, 0:slots], in0=index[:, :, 0:slots], scalar1=float(n + 1),
-                                scalar2=None, op0=ALU.is_equal,
-                            )
+            def by_quad(tile):
+                return tile[:].rearrange("m s (q x) -> m s q x", x=slots)
 
-                    def fill(s=s, half=half):
-                        target = rows[:, :, :, 0:slots].rearrange("m q (n s) x -> m s n q x", s=4)[:, s, 4 * half : 4 * half + 4]
-                        value = state["slot_value"][:, s, :, 0:slots].unsqueeze(1).to_broadcast([P, 4, QUADS, slots])
-                        nc.vector.tensor_mul(out=target, in0=target, in1=value)
+            def four_knots(n):
+                return state["rows"][:, :, 4 * n : 4 * n + 4, :].rearrange("m q s x -> m s q x")
 
-                    actions.append(mark)
-                    actions.append(fill)
+            def mark(n):
+                if n == 0:
+                    state["rows"] = rows_pool.tile([P, QUADS, KNOTS, slots], BF16, name="rows")
+                nc.vector.tensor_scalar(
+                    out=four_knots(n), in0=by_quad(state["index"]), scalar1=float(n + 1), scalar2=None, op0=ALU.is_equal
+                )
+
+            def fill(n):
+                nc.vector.tensor_mul(out=four_knots(n), in0=four_knots(n), in1=by_quad(state["values"]))
+
+            actions = [lambda: mark(0)]
+            for n in range(KNOTS // 4):
+                if n + 1 < KNOTS // 4:
+                    actions.append(lambda n=n: mark(n + 1))
+                actions.append(lambda n=n: fill(n))
             return actions
 
-        def finish(state, alone):
+        def finish(state, shared):
             words = state["rows"][:].bitcast(F32)
-            actions = []
-            pending = []
+            turns = []
+            copies = []
+            stages = []
             for group in range(0, state["tiles"], TILES_PER_GROUP):
                 store = {}
 
-                def turn(pair, group=group, store=store):
-                    if pair == 0:
-                        store["basis"] = work.tile(
+                def turn(n, group=group, store=store):
+                    if n == 0:
+                        store["basis"] = pools["work"].tile(
                             [P, TILES_PER_GROUP, PASSES * P * PACK], BF16, align_bytes=64, name="basis"
                         )
-                    for n in range(2 * pair, 2 * pair + 2):
-                        flipped = transposed.tile([P, PASSES, PAIRS, P], F32, tag="transposed", name="flipped")
-                        for g in range(PASSES):
-                            for u in range(PAIRS):
-                                gu = PAIRS * g + u
-                                nc.tensor.transpose(
-                                    flipped[:, g, u, :],
-                                    words[:, CLASSES * gu : CLASSES * (gu + 1), :, group + n].rearrange("m c k -> m (c k)"),
-                                    identity_f32[:],
-                                )
-                        nc.scalar.copy(
-                            out=store["basis"][:, n, :].bitcast(F32).rearrange("p (g m u) -> p g m u", g=PASSES, u=PAIRS),
-                            in_=flipped[:].rearrange("p g u m -> p g m u"),
-                        )
+                    flipped = transposed.tile([P, PASSES, PAIRS, P], F32, tag="transposed", name="flipped")
+                    store[n] = flipped
+                    for g in range(PASSES):
+                        for u in range(PAIRS):
+                            gu = PAIRS * g + u
+                            nc.tensor.transpose(
+                                flipped[:, g, u, :],
+                                words[:, CLASSES * gu : CLASSES * (gu + 1), :, group + n].rearrange("m c k -> m (c k)"),
+                                identity_f32[:],
+                            )
+
+                def copy(n, store=store):
+                    copy_out = nc.vector.tensor_copy if shared and n % 2 == 1 else nc.scalar.copy
+                    copy_out(
+                        out=store["basis"][:, n, :].bitcast(F32).rearrange("p (g m u) -> p g m u", g=PASSES, u=PAIRS),
+                        in_=store[n][:].rearrange("p g u m -> p g m u"),
+                    )
 
                 def quantise(store=store):
-                    store["codes"] = work.tile([P, GROUP_COLS], U32, align_bytes=64, name="codes")
-                    store["scales"] = work.tile([P, GROUP_COLS], U8, align_bytes=64, name="scales")
+                    store["codes"] = pools["work"].tile([P, GROUP_COLS], U32, align_bytes=64, name="codes")
+                    store["scales"] = pools["work"].tile([P, GROUP_COLS], U8, align_bytes=64, name="scales")
                     nc.vector.quantize_mx(
                         out=store["codes"][:].bitcast(FP8X4), scales=store["scales"][:],
                         in_=store["basis"][:].rearrange("p s n -> p (s n)"),
@@ -508,43 +561,67 @@ def tile_kanlayer_t_kernel(tc, x, spline_coeffs, spline_knots, out):
                                 )
 
                 def send(group=group, store=store):
-                    result = work.tile([P, TILES_PER_GROUP, OUTS], F32, name="result")
+                    result = pools["work"].tile([P, TILES_PER_GROUP, OUTS], F32, name="result")
                     for pair in range(TILES_PER_GROUP // 2):
-                        if alone and pair == 1:
+                        if shared and pair == 1:
                             nc.vector.tensor_copy(out=result[:, 2 * pair : 2 * pair + 2, :], in_=store["acc"][pair][:])
                         else:
                             nc.scalar.copy(out=result[:, 2 * pair : 2 * pair + 2, :], in_=store["acc"][pair][:])
                     tile0 = state["first"] + group
                     nc.sync.dma_start(out=out_rows[:, tile0 : tile0 + TILES_PER_GROUP, :], in_=result[:])
 
-                actions.append(lambda turn=turn: turn(0))
-                if pending:
-                    actions.append(pending.pop(0))
-                actions.append(lambda turn=turn: turn(1))
-                if pending:
-                    actions.append(pending.pop(0))
-                if pending:
-                    actions.append(pending.pop(0))
-                pending.extend([quantise, multiply, send])
-            return actions + pending
+                for n in range(TILES_PER_GROUP):
+                    turns.append(lambda n=n, turn=turn: turn(n))
+                    copies.append(lambda n=n, copy=copy: copy(n))
+                stages.append((quantise, multiply, send))
+
+            actions = []
+            for n in range(state["tiles"] + 7):
+                for late, stage in ((6, 2), (4, 1), (3, 0)):
+                    group, rest = divmod(n - TILES_PER_GROUP + 1 - late, TILES_PER_GROUP)
+                    if rest == 0 and 0 <= group < len(stages):
+                        actions.append(stages[group][stage])
+                if n < state["tiles"]:
+                    actions.append(turns[n])
+                if 0 <= n - 1 < state["tiles"]:
+                    actions.append(copies[n - 1])
+            return actions
 
         states = []
         for n, tiles in enumerate(CHUNK_TILES):
-            states.append({"index": n, "first": sum(CHUNK_TILES[:n]), "tiles": tiles})
+            states.append({"number": n, "first": sum(CHUNK_TILES[:n]), "tiles": tiles})
 
-        for number in range(STEP_BUFS):
-            load(number)
-        for action in look_up(states[0]) + work_out(states[0]) + look_up(states[1]):
-            action()
-        for n, state in enumerate(states):
-            side = [spread(state)]
+        def phase(n, *more):
+            side = [spread(states[n]), *more]
             if n + 1 < len(states):
                 side.append(work_out(states[n + 1]))
             if n + 2 < len(states):
                 side.append(look_up(states[n + 2]))
             if n > 0:
-                side.append(finish(states[n - 1], False))
+                side.append(finish(states[n - 1], n == len(states) - 1))
             for action in interleave(*side):
                 action()
-        for action in finish(states[-1], True):
-            action()
+
+        with tc.tile_pool(name="setup", bufs=1) as setup:
+            knot = load_knots(nc, setup, spline_knots)
+            x_rows = setup.tile([P, ROW_TILES, FEATURES], BF16)
+            for tiles in (slice(0, QUARTER), slice(QUARTER, ROW_TILES)):
+                nc.sync.dma_start(out=x_rows[:, tiles, :], in_=x.rearrange("(m a) i -> m a i", a=ROW_TILES)[:, tiles, :])
+            park_x(nc, setup, transposed, identity, knot, x_rows, parked, 0)
+            for number in range(STEP_BUFS):
+                load(number)
+            table, threshold = build_table(nc, const, setup, transposed, identity_f32, knot)
+            for quarter in range(1, ROW_TILES // QUARTER):
+                park_x(nc, setup, transposed, identity, knot, x_rows, parked, quarter)
+            fetch, coefficient_steps = prepare_coefficients(setup)
+            fetch()
+            with tc.manual_schedule(engines={mybir.EngineType.DVE, mybir.EngineType.Activation, mybir.EngineType.PE}):
+                for action in look_up(states[0]) + interleave(work_out(states[0]), look_up(states[1])):
+                    action()
+                phase(0, coefficient_steps)
+        pools["work"] = ctx.enter_context(tc.tile_pool(name="work", bufs=2))
+        with tc.manual_schedule(engines={mybir.EngineType.DVE, mybir.EngineType.Activation, mybir.EngineType.PE}):
+            for n in range(1, len(states)):
+                phase(n)
+            for action in finish(states[-1], True):
+                action()

@@ -88,28 +88,28 @@ def build_table(nc, const, pool, psum, identity_f32, knot):
         for odd in range(2):
             first = 2 + odd + offsets[odd]
             nc.vector.tensor_copy(out=cell[:, n, odd : STEPS + 1 : 2], in_=span[:, first : first + 2 * half - 1 : 2])
-    changes = wide[:, 1 : 1 + GEO, 0:STEPS]
+    rows_of = pool.tile([P, GEO, STEP_ROWS], F32)
+    changes = rows_of[:, :, 0:STEPS]
     nc.vector.tensor_sub(out=changes, in0=cell[:, :, 1 : STEPS + 1], in1=cell[:, :, 0:STEPS])
     low_rows = slice(LOW_STEPS[0] - 1, LOW_STEPS[-1])
     rounded = pool.tile([P, GEO, len(LOW_STEPS)], BF16)
     nc.vector.tensor_copy(out=rounded[:], in_=changes[:, :, low_rows])
-    nc.vector.tensor_sub(out=wide[:, 1 : 1 + GEO, STEPS:STEP_ROWS], in0=changes[:, :, low_rows], in1=rounded[:])
-    level = wide[:, level_col, 0:STEP_ROWS]
+    nc.vector.tensor_sub(out=rows_of[:, :, STEPS:STEP_ROWS], in0=changes[:, :, low_rows], in1=rounded[:])
+    level = pool.tile([P, STEP_ROWS], F32)
     nc.vector.tensor_copy(out=level[:, 0:STEPS], in_=knot[:, 3 : 3 + STEPS])
     nc.vector.tensor_copy(out=level[:, STEPS:STEP_ROWS], in_=knot[:, 2 + LOW_STEPS[0] : 3 + LOW_STEPS[-1]])
     nc.vector.memset(wide[:, level_col, ONE_ROW : ONE_ROW + 1], -FAR)
     for c in range(TRIPLE):
-        rows = slice(STEP_ROWS * c, STEP_ROWS * (c + 1))
+        rows = slice(c, ONE_ROW, TRIPLE)
         mine = slice(1 + GEO * c, 1 + GEO * (c + 1))
-        if c > 0:
-            nc.vector.tensor_copy(out=wide[:, mine, rows], in_=wide[:, 1 : 1 + GEO, 0:STEP_ROWS])
-            nc.vector.tensor_copy(out=wide[:, level_col, rows], in_=level)
+        nc.vector.tensor_copy(out=wide[:, mine, rows], in_=rows_of[:])
+        nc.vector.tensor_copy(out=wide[:, level_col, rows], in_=level[:])
         nc.vector.tensor_copy(out=wide[:, mine, ONE_ROW : ONE_ROW + 1], in_=cell[:, :, 0:1])
         nc.vector.memset(wide[:, 1 + GEO * c : 1 + GEO * c + 4, X_ROW + c : X_ROW + c + 1], 1.0)
         for col, unit in ((0, 2.0 ** (CODE_BITS * c)), (LOOK, float(c == 1))):
             for n, change in enumerate((1.0, 2.0, 4.0, 1.0)):
                 if unit > 0:
-                    nc.vector.memset(wide[:, col, STEP_ROWS * c + n : STEP_ROWS * c + STEPS : 4], change * unit)
+                    nc.vector.memset(wide[:, col, TRIPLE * n + c : TRIPLE * STEPS : 4 * TRIPLE], change * unit)
 
     table = const.tile([P, LOOK + LAST], BF16)
     threshold = const.tile([P, 1], F32)
@@ -237,7 +237,7 @@ def tile_kanlayer_t_kernel(tc, x, spline_coeffs, spline_knots, out):
             target = x_steps[number % STEP_BUFS][:].bitcast(F32)
             for c in range(TRIPLE):
                 nc.sync.dma_start(
-                    out=target[STEP_ROWS * c : STEP_ROWS * (c + 1), :, :], in_=source[c].partition_broadcast(STEP_ROWS)
+                    out=target[c:ONE_ROW:TRIPLE, :, :], in_=source[c].partition_broadcast(STEP_ROWS)
                 )
             for c, first, last in ((0, ONE_ROW, X_ROW + 1), (1, X_ROW + 1, X_ROW + 2), (2, X_ROW + 2, P)):
                 nc.sync.dma_start(out=target[first:last, :, :], in_=source[c].partition_broadcast(last - first))

@@ -42,9 +42,9 @@ LOOK_SLOTS = GROUPS + 1
 CODE_BITS = 7
 FAR = 2.0**100
 
-CHUNK_TILES = (4, 12, 16, 16, 12, 4)
-SUB_TILES = 4
-STEP_BUFS = 4
+CHUNK_TILES = (8, 8, 8, 8, 8, 8, 8, 8)
+SUB_TILES = 8
+STEP_BUFS = 3
 QUARTER = 16
 PARK_HALF = 32
 PARK_TILES = 8
@@ -131,10 +131,8 @@ def park_x(nc, pool, psum, identity, knot, x_rows, parked, quarter):
     tiles = slice(QUARTER * quarter, QUARTER * (quarter + 1))
     clamped = pool.tile([P, QUARTER, FEATURES], BF16, name="clamped%d" % quarter)
 
-    engine = nc.vector if quarter == 0 else nc.gpsimd
-
     def clamp(out_columns, in_columns):
-        engine.tensor_scalar(
+        nc.vector.tensor_scalar(
             out=clamped[:, :, out_columns], in0=x_rows[:, tiles, in_columns],
             scalar1=knot[:, 38:39], scalar2=knot[:, 2:3], op0=ALU.min, op1=ALU.max,
         )
@@ -154,7 +152,7 @@ def park_x(nc, pool, psum, identity, knot, x_rows, parked, quarter):
     turned = pool.tile([P, 4, P], BF16, name="turned%d" % quarter)
     nc.scalar.copy(out=turned[:], in_=flipped[:])
     words = turned[:].bitcast(F32)
-    queue = nc.sync if quarter == 0 else nc.gpsimd
+    queue = nc.sync if quarter == 0 else nc.scalar
     size = QUARTER * P // 2
     at = quarter % 2 * size
     place = parked[:, quarter // 2, at : at + size].rearrange("r (n b w) -> r n b w", n=4, b=4)
@@ -204,7 +202,7 @@ def tile_kanlayer_t_kernel(tc, x, spline_coeffs, spline_knots, out):
 
             def fetch():
                 for h in range(halves):
-                    nc.gpsimd.dma_start(
+                    nc.scalar.dma_start(
                         out=natural[:, h, :].rearrange("q (i k) -> q i k", k=KNOTS),
                         in_=spline_coeffs[:, P * h : P * h + P, :].rearrange("i q k -> q i k"),
                     )
@@ -608,17 +606,22 @@ def tile_kanlayer_t_kernel(tc, x, spline_coeffs, spline_knots, out):
             for tiles in (slice(0, QUARTER), slice(QUARTER, ROW_TILES)):
                 nc.sync.dma_start(out=x_rows[:, tiles, :], in_=x.rearrange("(m a) i -> m a i", a=ROW_TILES)[:, tiles, :])
             park_x(nc, setup, transposed, identity, knot, x_rows, parked, 0)
-            for number in range(STEP_BUFS):
+            ready = [number for number in range(STEP_BUFS) if SUB_TILES * number < QUARTER]
+            for number in ready:
                 load(number)
             table, threshold = build_table(nc, const, setup, transposed, identity_f32, knot)
             for quarter in range(1, ROW_TILES // QUARTER):
                 park_x(nc, setup, transposed, identity, knot, x_rows, parked, quarter)
+            for number in range(len(ready), STEP_BUFS):
+                load(number)
             fetch, coefficient_steps = prepare_coefficients(setup)
             fetch()
             with tc.manual_schedule(engines={mybir.EngineType.DVE, mybir.EngineType.Activation, mybir.EngineType.PE}):
                 for action in look_up(states[0]) + interleave(work_out(states[0]), look_up(states[1])):
                     action()
-                phase(0, coefficient_steps)
+                phase(0)
+                for action in coefficient_steps:
+                    action()
         pools["work"] = ctx.enter_context(tc.tile_pool(name="work", bufs=2))
         with tc.manual_schedule(engines={mybir.EngineType.DVE, mybir.EngineType.Activation, mybir.EngineType.PE}):
             for n in range(1, len(states)):

@@ -29,10 +29,10 @@ GROUP_COLS = TILES_PER_GROUP * PASSES * P
 
 STEPS = 35
 LOW_STEPS = range(2, 6)
-STEP_ROWS = STEPS + len(LOW_STEPS)
+ONE_STEP = STEPS + len(LOW_STEPS)
+STEP_ROWS = ONE_STEP + 1
 TRIPLE = 3
-ONE_ROW = TRIPLE * STEP_ROWS
-X_ROW = ONE_ROW + 1
+X_ROW = TRIPLE * STEP_ROWS
 GROUPS = 5
 BLOCKS = 2 * GROUPS + 1
 GEO = 6
@@ -49,31 +49,40 @@ QUARTER = 16
 PARK_HALF = 32
 PARK_TILES = 8
 
+ROOM = "room"
+
 FLOPS = 2 * ROWS * FEATURES * KNOTS * OUTS
 
 
 def load_knots(nc, pool, spline_knots):
+    more = 7
+    ramp = pool.tile([P, more], F32)
+    for n in range(more):
+        nc.gpsimd.memset(ramp[:, n : n + 1], float(n + 1))
     knots_bf = pool.tile([P, KNOTS], BF16)
     nc.sync.dma_start(out=knots_bf[:], in_=spline_knots.partition_broadcast(P))
-    knot = pool.tile([P, KNOTS + 9], F32)
+    knot = pool.tile([P, 2 + KNOTS + more], F32)
     nc.vector.tensor_copy(out=knot[:, 2 : 2 + KNOTS], in_=knots_bf[:])
-    for i in range(2):
-        nc.vector.tensor_copy(out=knot[:, i : i + 1], in_=knots_bf[:, 0:1])
     step = pool.tile([P, 1], F32)
-    nc.vector.tensor_sub(out=step[:], in0=knot[:, 3:4], in1=knot[:, 2:3])
-    for n in range(1, 8):
-        at = 2 + KNOTS - 1 + n
-        nc.vector.tensor_scalar(
-            out=knot[:, at : at + 1], in0=step[:], scalar1=float(n), scalar2=knot[:, 1 + KNOTS : 2 + KNOTS],
-            op0=ALU.mult, op1=ALU.add,
-        )
+    nc.vector.tensor_sub(out=step[:], in0=knots_bf[:, 1:2], in1=knots_bf[:, 0:1])
+    nc.vector.tensor_copy(out=knot[:, 0:2], in_=knots_bf[:, 0:1].to_broadcast([P, 2]))
+    nc.vector.tensor_scalar(
+        out=knot[:, 2 + KNOTS : 2 + KNOTS + more], in0=ramp[:], scalar1=step[:], scalar2=knot[:, 1 + KNOTS : 2 + KNOTS],
+        op0=ALU.mult, op1=ALU.add,
+    )
     return knot
 
 
 def build_table(nc, const, pool, psum, identity_f32, knot):
     level_col = LOOK + 1
     wide = pool.tile([P, LOOK + 2, P], F32)
-    nc.vector.memset(wide[:], 0.0)
+    nc.gpsimd.memset(wide[:], 0.0)
+    for c in range(TRIPLE):
+        nc.gpsimd.memset(wide[:, 1 + GEO * c : 1 + GEO * c + 4, X_ROW + 2 * c : X_ROW + 2 * c + 1], 1.0)
+        for col, unit in ((0, 2.0 ** (CODE_BITS * c)), (LOOK, float(c == 1))):
+            for n, change in enumerate((1.0, 2.0, 4.0, 1.0)):
+                if unit > 0:
+                    nc.gpsimd.memset(wide[:, col, TRIPLE * n + c : TRIPLE * STEPS : 4 * TRIPLE], change * unit)
     span = pool.tile([P, KNOTS + 6], F32)
     nc.vector.tensor_sub(out=span[:], in0=knot[:, 3 : KNOTS + 9], in1=knot[:, 0 : KNOTS + 6])
     cell = pool.tile([P, GEO, STEPS + 1], F32)
@@ -94,22 +103,16 @@ def build_table(nc, const, pool, psum, identity_f32, knot):
     low_rows = slice(LOW_STEPS[0] - 1, LOW_STEPS[-1])
     rounded = pool.tile([P, GEO, len(LOW_STEPS)], BF16)
     nc.vector.tensor_copy(out=rounded[:], in_=changes[:, :, low_rows])
-    nc.vector.tensor_sub(out=rows_of[:, :, STEPS:STEP_ROWS], in0=changes[:, :, low_rows], in1=rounded[:])
+    nc.vector.tensor_sub(out=rows_of[:, :, STEPS:ONE_STEP], in0=changes[:, :, low_rows], in1=rounded[:])
+    nc.vector.tensor_copy(out=rows_of[:, :, ONE_STEP:STEP_ROWS], in_=cell[:, :, 0:1])
     level = pool.tile([P, STEP_ROWS], F32)
+    nc.vector.memset(level[:, ONE_STEP:STEP_ROWS], -FAR)
     nc.vector.tensor_copy(out=level[:, 0:STEPS], in_=knot[:, 3 : 3 + STEPS])
-    nc.vector.tensor_copy(out=level[:, STEPS:STEP_ROWS], in_=knot[:, 2 + LOW_STEPS[0] : 3 + LOW_STEPS[-1]])
-    nc.vector.memset(wide[:, level_col, ONE_ROW : ONE_ROW + 1], -FAR)
+    nc.vector.tensor_copy(out=level[:, STEPS:ONE_STEP], in_=knot[:, 2 + LOW_STEPS[0] : 3 + LOW_STEPS[-1]])
     for c in range(TRIPLE):
-        rows = slice(c, ONE_ROW, TRIPLE)
         mine = slice(1 + GEO * c, 1 + GEO * (c + 1))
-        nc.vector.tensor_copy(out=wide[:, mine, rows], in_=rows_of[:])
-        nc.vector.tensor_copy(out=wide[:, level_col, rows], in_=level[:])
-        nc.vector.tensor_copy(out=wide[:, mine, ONE_ROW : ONE_ROW + 1], in_=cell[:, :, 0:1])
-        nc.vector.memset(wide[:, 1 + GEO * c : 1 + GEO * c + 4, X_ROW + c : X_ROW + c + 1], 1.0)
-        for col, unit in ((0, 2.0 ** (CODE_BITS * c)), (LOOK, float(c == 1))):
-            for n, change in enumerate((1.0, 2.0, 4.0, 1.0)):
-                if unit > 0:
-                    nc.vector.memset(wide[:, col, TRIPLE * n + c : TRIPLE * STEPS : 4 * TRIPLE], change * unit)
+        nc.vector.tensor_copy(out=wide[:, mine, c:X_ROW:TRIPLE], in_=rows_of[:])
+        nc.vector.tensor_copy(out=wide[:, level_col, c:X_ROW:TRIPLE], in_=level[:])
 
     table = const.tile([P, LOOK + LAST], BF16)
     threshold = const.tile([P, 1], F32)
@@ -161,6 +164,22 @@ def park_x(nc, pool, psum, identity, knot, x_rows, parked, quarter):
     queue.dma_start(out=place[FEATURES].rearrange("n b w -> b n w"), in_=words[FEATURES - 1 : P : FEATURES])
 
 
+def fill_room(items, others):
+    rooms = sum(1 for item in items if item == ROOM)
+    merged = []
+    used = 0
+    seen = 0
+    for item in items:
+        if item == ROOM:
+            seen += 1
+            until = len(others) * seen // rooms
+            merged.extend(others[used:until])
+            used = until
+        else:
+            merged.append(item)
+    return merged + others[used:]
+
+
 def interleave(*lists):
     entries = []
     for which, items in enumerate(lists):
@@ -176,7 +195,7 @@ def tile_kanlayer_t_kernel(tc, x, spline_coeffs, spline_knots, out):
         planes = ctx.enter_context(tc.tile_pool(name="planes", bufs=1))
         keys = ctx.enter_context(tc.tile_pool(name="keys", bufs=1))
         carried = ctx.enter_context(tc.tile_pool(name="carried", bufs=2))
-        rows_pool = ctx.enter_context(tc.tile_pool(name="rows", bufs=2))
+        rows_pool = ctx.enter_context(tc.tile_pool(name="rows", bufs=3))
         transposed = ctx.enter_context(tc.psum_pool(name="transposed", bufs=4))
         lookups = ctx.enter_context(tc.psum_pool(name="lookups", bufs=2))
         sums = ctx.enter_context(tc.psum_pool(name="sums", bufs=2))
@@ -234,10 +253,12 @@ def tile_kanlayer_t_kernel(tc, x, spline_coeffs, spline_knots, out):
             source = parked[0 : TRIPLE * BLOCKS, tile0 // PARK_HALF, words].rearrange("(g c) w -> c g w", c=TRIPLE)
             target = x_steps[number % STEP_BUFS][:].bitcast(F32)
             for c in range(TRIPLE):
-                nc.sync.dma_start(
-                    out=target[c:ONE_ROW:TRIPLE, :, :], in_=source[c].partition_broadcast(STEP_ROWS)
-                )
-            for c, first, last in ((0, ONE_ROW, X_ROW + 1), (1, X_ROW + 1, X_ROW + 2), (2, X_ROW + 2, P)):
+                for first, last in ((0, 32), (32, STEP_ROWS)):
+                    nc.sync.dma_start(
+                        out=target[TRIPLE * first + c : TRIPLE * (last - 1) + c + 1 : TRIPLE, :, :],
+                        in_=source[c].partition_broadcast(last - first),
+                    )
+            for c, first, last in ((0, X_ROW, X_ROW + 2), (1, X_ROW + 2, X_ROW + 4), (2, X_ROW + 4, P)):
                 nc.sync.dma_start(out=target[first:last, :, :], in_=source[c].partition_broadcast(last - first))
 
         def look_up(state):
@@ -292,8 +313,9 @@ def tile_kanlayer_t_kernel(tc, x, spline_coeffs, spline_knots, out):
                 actions.append(lambda number=number: compare(number))
                 for pair in range(first, first + SUB_TILES, 2):
                     actions.append(lambda pair=pair, number=number: multiply(pair, number))
-                for pair in range(first, first + SUB_TILES, 2):
-                    actions.append(lambda pair=pair: evacuate(pair))
+                    if pair > first:
+                        actions.append(lambda pair=pair: evacuate(pair - 2))
+                actions.append(lambda first=first: evacuate(first + SUB_TILES - 2))
                 if SUB_TILES * (number + STEP_BUFS) < ROW_TILES:
                     actions.append(lambda number=number: load(number + STEP_BUFS))
             return actions
@@ -440,6 +462,7 @@ def tile_kanlayer_t_kernel(tc, x, spline_coeffs, spline_knots, out):
                 left_sums,
                 outer_roots,
                 right_sums,
+                ROOM,
                 lambda: own_cell(0),
                 outer_squares,
                 upper_product,
@@ -447,6 +470,7 @@ def tile_kanlayer_t_kernel(tc, x, spline_coeffs, spline_knots, out):
                 lower_product,
                 lambda: own_cell(2),
                 right_roots,
+                ROOM,
                 lambda: part(0, 0, 1),
                 lambda: part(1, 1, 1),
                 outer_ratios,
@@ -454,25 +478,39 @@ def tile_kanlayer_t_kernel(tc, x, spline_coeffs, spline_knots, out):
                 lambda: part(3, 3, 15),
                 middle_square,
                 parts_out,
+                ROOM,
+                ROOM,
                 inner_ratios,
                 low_ratio,
                 slot0_index,
                 quadratics,
+                ROOM,
                 swap_flag,
+                ROOM,
                 slot_index,
+                ROOM,
                 cubics,
                 both_quadratics,
                 cubics_out,
+                ROOM,
                 middle,
+                ROOM,
                 upper_sum,
+                ROOM,
                 other_sum,
                 third_value,
                 second_value,
+                ROOM,
+                ROOM,
                 take,
+                ROOM,
                 keep,
+                ROOM,
                 lambda: join(0),
                 lambda: join(1),
                 hand_over,
+                ROOM,
+                ROOM,
             ]
 
         def spread(state):
@@ -590,21 +628,27 @@ def tile_kanlayer_t_kernel(tc, x, spline_coeffs, spline_knots, out):
             states.append({"number": n, "first": sum(CHUNK_TILES[:n]), "tiles": tiles})
 
         def phase(n, *more):
-            side = [spread(states[n]), *more]
+            side = [spread(states[n])]
             if n + 1 < len(states):
-                side.append(work_out(states[n + 1]))
+                side = [fill_room(work_out(states[n + 1]), side[0])]
             if n + 2 < len(states):
                 side.append(look_up(states[n + 2]))
-            if n > 0:
-                side.append(finish(states[n - 1], n == len(states) - 1))
+            side.extend(more)
+            if n >= 2:
+                ending = finish(states[n - 1], n == len(states) - 1)
+                if n == 2:
+                    ending = finish(states[0], False) + ending
+                side.append(ending)
             for action in interleave(*side):
                 action()
 
+        pools["work"] = ctx.enter_context(tc.tile_pool(name="work", bufs=2))
         with tc.tile_pool(name="setup", bufs=1) as setup:
             knot = load_knots(nc, setup, spline_knots)
             x_rows = setup.tile([P, ROW_TILES, FEATURES], BF16)
-            for tiles in (slice(0, QUARTER), slice(QUARTER, ROW_TILES)):
-                nc.sync.dma_start(out=x_rows[:, tiles, :], in_=x.rearrange("(m a) i -> m a i", a=ROW_TILES)[:, tiles, :])
+            x_by_rows = x.rearrange("(m a) i -> m a i", a=ROW_TILES)
+            nc.sync.dma_start(out=x_rows[:, 0:QUARTER, :], in_=x_by_rows[:, 0:QUARTER, :])
+            nc.scalar.dma_start(out=x_rows[:, QUARTER:ROW_TILES, :], in_=x_by_rows[:, QUARTER:ROW_TILES, :])
             park_x(nc, setup, transposed, identity, knot, x_rows, parked, 0)
             ready = [number for number in range(STEP_BUFS) if SUB_TILES * number < QUARTER]
             for number in ready:
@@ -615,16 +659,14 @@ def tile_kanlayer_t_kernel(tc, x, spline_coeffs, spline_knots, out):
             for number in range(len(ready), STEP_BUFS):
                 load(number)
             fetch, coefficient_steps = prepare_coefficients(setup)
-            fetch()
             with tc.manual_schedule(engines={mybir.EngineType.DVE, mybir.EngineType.Activation, mybir.EngineType.PE}):
-                for action in look_up(states[0]) + interleave(work_out(states[0]), look_up(states[1])):
+                for action in look_up(states[0]) + interleave(fill_room(work_out(states[0]), []), look_up(states[1])):
                     action()
+                fetch()
                 phase(0)
-                for action in coefficient_steps:
-                    action()
-        pools["work"] = ctx.enter_context(tc.tile_pool(name="work", bufs=2))
+                phase(1, [lambda: None] * 10 + coefficient_steps)
         with tc.manual_schedule(engines={mybir.EngineType.DVE, mybir.EngineType.Activation, mybir.EngineType.PE}):
-            for n in range(1, len(states)):
+            for n in range(2, len(states)):
                 phase(n)
             for action in finish(states[-1], True):
                 action()

@@ -38,6 +38,7 @@ BLOCKS = 2 * GROUPS + 1
 GEO = 6
 LOOK = 1 + TRIPLE * GEO
 LAST = 1 + GEO
+HALF_BLOCKS = GROUPS + 1
 LOOK_SLOTS = GROUPS + 1
 CODE_BITS = 7
 FAR = 2.0**100
@@ -254,10 +255,11 @@ def tile_kanlayer_t_kernel(tc, x, spline_coeffs, spline_knots, out):
             target = x_steps[number % STEP_BUFS][:].bitcast(F32)
             for c in range(TRIPLE):
                 for first, last in ((0, 32), (32, STEP_ROWS)):
-                    nc.sync.dma_start(
-                        out=target[TRIPLE * first + c : TRIPLE * (last - 1) + c + 1 : TRIPLE, :, :],
-                        in_=source[c].partition_broadcast(last - first),
-                    )
+                    rows = slice(TRIPLE * first + c, TRIPLE * (last - 1) + c + 1, TRIPLE)
+                    for queue, blocks in ((nc.sync, slice(0, HALF_BLOCKS)), (nc.scalar, slice(HALF_BLOCKS, BLOCKS))):
+                        queue.dma_start(
+                            out=target[rows, blocks, :], in_=source[c, blocks].partition_broadcast(last - first)
+                        )
             for c, first, last in ((0, X_ROW, X_ROW + 2), (1, X_ROW + 2, X_ROW + 4), (2, X_ROW + 4, P)):
                 nc.sync.dma_start(out=target[first:last, :, :], in_=source[c].partition_broadcast(last - first))
 

@@ -206,6 +206,8 @@ def tile_kanlayer_t_kernel(tc, x, spline_coeffs, spline_knots, out):
         identity_f32 = const.tile([P, P], F32)
         make_identity(nc, identity_f32[:])
         x_steps = [const.tile([P, BLOCKS, SUB_TILES * P], BF16, name="x_steps%d" % n) for n in range(STEP_BUFS)]
+        bits = const.tile([P, 6, 2 * QUADS * max(CHUNK_TILES)], BF16)
+        nc.gpsimd.memset(bits[:, 1, :], 1.0)
         w_codes = const.tile([P, PASSES, OUTS], U32, align_bytes=64)
         w_scales = const.tile([P, PASSES, OUTS], U8, align_bytes=64)
 
@@ -248,7 +250,7 @@ def tile_kanlayer_t_kernel(tc, x, spline_coeffs, spline_knots, out):
 
             return fetch, [lambda: turn(0), lambda: turn(1), lambda: group(0), lambda: group(1), quantise]
 
-        def load(number):
+        def load(number, ahead=False):
             tile0 = SUB_TILES * number
             words = slice((tile0 % PARK_HALF) * P // 2, (tile0 % PARK_HALF + SUB_TILES) * P // 2)
             source = parked[0 : TRIPLE * BLOCKS, tile0 // PARK_HALF, words].rearrange("(g c) w -> c g w", c=TRIPLE)
@@ -256,7 +258,7 @@ def tile_kanlayer_t_kernel(tc, x, spline_coeffs, spline_knots, out):
             for c in range(TRIPLE):
                 for first, last in ((0, 32), (32, STEP_ROWS)):
                     rows = slice(TRIPLE * first + c, TRIPLE * (last - 1) + c + 1, TRIPLE)
-                    for queue, blocks in ((nc.sync, slice(0, HALF_BLOCKS)), (nc.scalar, slice(HALF_BLOCKS, BLOCKS))):
+                    for queue, blocks in ((nc.sync, slice(0, HALF_BLOCKS)), (nc.sync if ahead else nc.scalar, slice(HALF_BLOCKS, BLOCKS))):
                         queue.dma_start(
                             out=target[rows, blocks, :], in_=source[c, blocks].partition_broadcast(last - first)
                         )
@@ -269,8 +271,8 @@ def tile_kanlayer_t_kernel(tc, x, spline_coeffs, spline_knots, out):
             banks = {}
 
             def start():
-                state["cell"] = carried.tile([P, LOOK_SLOTS, slots], U32, name="cell")
-                state["geo"] = carried.tile([P, GEO, QUADS, slots], F32, name="geo")
+                state["cell"] = carried.tile([P, slots // 4, LOOK_SLOTS, 4], U32, name="cell")
+                state["geo"] = carried.tile([P, GEO, slots // 4, QUADS, 4], F32, name="geo")
 
             def compare(number):
                 steps = x_steps[number % STEP_BUFS]
@@ -299,13 +301,12 @@ def tile_kanlayer_t_kernel(tc, x, spline_coeffs, spline_knots, out):
 
             def evacuate(pair):
                 bank = banks[pair][:].rearrange("m w g a e -> m w g (a e)")
-                at = slice(2 * pair, 2 * pair + 4)
-                nc.scalar.activation(out=state["cell"][:, :, at], in_=bank[:, 0], func=ACT.Copy)
+                nc.scalar.activation(out=state["cell"][:, pair // 2], in_=bank[:, 0], func=ACT.Copy)
                 for c in range(TRIPLE):
                     count = LOOK_SLOTS if c == 0 else GROUPS
                     q0 = GROUPS * (2 - c)
                     nc.scalar.activation(
-                        out=state["geo"][:, :, q0 : q0 + count, at],
+                        out=state["geo"][:, :, pair // 2, q0 : q0 + count, :],
                         in_=bank[:, 1 + GEO * c : 1 + GEO * (c + 1), 0:count, :], func=ACT.Abs,
                     )
 
@@ -330,7 +331,7 @@ def tile_kanlayer_t_kernel(tc, x, spline_coeffs, spline_knots, out):
             t = {}
 
             def by_n():
-                return state["geo"][:].rearrange("m n q s -> m n (q s)")
+                return state["geo"][:].rearrange("m n a q x -> m n (a q x)")
 
             def twice(one):
                 return one.unsqueeze(1).to_broadcast([P, 2, lanes])
@@ -404,11 +405,11 @@ def tile_kanlayer_t_kernel(tc, x, spline_coeffs, spline_knots, out):
 
             def own_cell(c):
                 if c == 0:
-                    t["own"] = keys.tile([P, QUADS, slots], I32, name="own")
+                    t["own"] = keys.tile([P, slots // 4, QUADS, 4], I32, name="own")
                 count = LOOK_SLOTS if c == 0 else GROUPS
                 q0 = GROUPS * (2 - c)
                 vec.tensor_scalar(
-                    out=t["own"][:, q0 : q0 + count], in0=state["cell"][:, 0:count].bitcast(I32),
+                    out=t["own"][:, :, q0 : q0 + count, :], in0=state["cell"][:, :, 0:count, :].bitcast(I32),
                     scalar1=CODE_BITS * c, scalar2=2**CODE_BITS - 1, op0=ALU.logical_shift_right, op1=ALU.bitwise_and,
                 )
 
@@ -416,25 +417,24 @@ def tile_kanlayer_t_kernel(tc, x, spline_coeffs, spline_knots, out):
                 if at == 0:
                     t["parts"] = keys.tile([P, 4, lanes], I32, name="parts")
                 vec.tensor_scalar(
-                    out=t["parts"][:, at], in0=t["own"][:].rearrange("m q s -> m (q s)"), scalar1=shift, scalar2=mask,
+                    out=t["parts"][:, at], in0=t["own"][:].rearrange("m a q x -> m (a q x)"), scalar1=shift, scalar2=mask,
                     op0=ALU.logical_shift_right, op1=ALU.bitwise_and,
                 )
 
             def parts_out():
-                t["bits"] = keys.tile([P, 5, lanes], BF16, name="bits")
-                act(out=t["bits"][:, 1:5], in_=t["parts"][:].bitcast(U32), func=ACT.Copy)
-
-            def slot0_index():
-                t["index"] = carried.tile([P, 4, lanes], BF16, name="index")
-                act(out=t["index"][:, 0], in_=t["parts"][:, 3].bitcast(U32), func=ACT.Copy, bias=1.0)
+                act(out=bits[:, 2:6, 0:lanes], in_=t["parts"][:].bitcast(U32), func=ACT.Copy)
 
             def swap_flag():
-                vec.tensor_sub(out=t["bits"][:, 0], in0=t["bits"][:, 1], in1=t["bits"][:, 3])
+                vec.tensor_sub(out=bits[:, 0, 0:lanes], in0=bits[:, 2, 0:lanes], in1=bits[:, 4, 0:lanes])
+
+            def by_four(tile):
+                return tile.rearrange("m (l x) -> m l x", x=4)
 
             def slot_index():
+                t["index"] = carried.tile([P, lanes // 4, 4, 4], BF16, name="index")
                 vec.tensor_add(
-                    out=t["index"][:, 1:4], in0=t["bits"][:, 1:4],
-                    in1=t["bits"][:, 4].unsqueeze(1).to_broadcast([P, 3, lanes]),
+                    out=t["index"][:], in0=bits[:, 1:5, 0:lanes].rearrange("m s (l x) -> m l s x", x=4),
+                    in1=by_four(bits[:, 5, 0:lanes]).unsqueeze(2).to_broadcast([P, lanes // 4, 4, 4]),
                 )
 
             def pairs(tile):
@@ -442,7 +442,7 @@ def tile_kanlayer_t_kernel(tc, x, spline_coeffs, spline_knots, out):
 
             def take():
                 t["moved"] = keys.tile([P, 4, lanes], BF16, name="moved")
-                flags = t["bits"][:, 0:3:2].unsqueeze(2).to_broadcast([P, 2, 2, lanes])
+                flags = bits[:, 0:4:3, 0:lanes].unsqueeze(2).to_broadcast([P, 2, 2, lanes])
                 vec.tensor_mul(out=pairs(t["moved"][:]), in0=pairs(t["values"][:]), in1=flags)
 
             def keep():
@@ -450,10 +450,13 @@ def tile_kanlayer_t_kernel(tc, x, spline_coeffs, spline_knots, out):
 
             def join(h):
                 if h == 0:
-                    t["slot_values"] = carried.tile([P, 4, lanes], BF16, name="slot_values")
+                    t["slot_values"] = carried.tile([P, lanes // 4, 4, 4], BF16, name="slot_values")
+
+                def half(tile, which):
+                    return pairs(tile[:])[:, :, which].rearrange("m p (l x) -> m l p x", x=4)
+
                 vec.tensor_add(
-                    out=t["slot_values"][:, 2 * h : 2 * h + 2], in0=pairs(t["values"][:])[:, :, h],
-                    in1=pairs(t["moved"][:])[:, :, 1 - h],
+                    out=t["slot_values"][:, :, 2 * h : 2 * h + 2, :], in0=half(t["values"], h), in1=half(t["moved"], 1 - h)
                 )
 
             def hand_over():
@@ -484,7 +487,6 @@ def tile_kanlayer_t_kernel(tc, x, spline_coeffs, spline_knots, out):
                 ROOM,
                 inner_ratios,
                 low_ratio,
-                slot0_index,
                 quadratics,
                 ROOM,
                 swap_flag,
@@ -518,21 +520,21 @@ def tile_kanlayer_t_kernel(tc, x, spline_coeffs, spline_knots, out):
         def spread(state):
             slots = 2 * state["tiles"]
 
-            def by_quad(tile):
-                return tile[:].rearrange("m s (q x) -> m s q x", x=slots)
+            def by_lane(tile):
+                return tile[:].rearrange("m l s x -> m l (s x)")
 
             def four_knots(n):
-                return state["rows"][:, :, 4 * n : 4 * n + 4, :].rearrange("m q s x -> m s q x")
+                return state["rows"][:].rearrange("m a q k x -> m (a q) (k x)")[:, :, 16 * n : 16 * n + 16]
 
             def mark(n):
                 if n == 0:
-                    state["rows"] = rows_pool.tile([P, QUADS, KNOTS, slots], BF16, name="rows")
+                    state["rows"] = rows_pool.tile([P, slots // 4, QUADS, KNOTS, 4], BF16, name="rows")
                 nc.vector.tensor_scalar(
-                    out=four_knots(n), in0=by_quad(state["index"]), scalar1=float(n + 1), scalar2=None, op0=ALU.is_equal
+                    out=four_knots(n), in0=by_lane(state["index"]), scalar1=float(n + 1), scalar2=None, op0=ALU.is_equal
                 )
 
             def fill(n):
-                nc.vector.tensor_mul(out=four_knots(n), in0=four_knots(n), in1=by_quad(state["values"]))
+                nc.vector.tensor_mul(out=four_knots(n), in0=four_knots(n), in1=by_lane(state["values"]))
 
             actions = [lambda: mark(0)]
             for n in range(KNOTS // 4):
@@ -561,7 +563,7 @@ def tile_kanlayer_t_kernel(tc, x, spline_coeffs, spline_knots, out):
                             gu = PAIRS * g + u
                             nc.tensor.transpose(
                                 flipped[:, g, u, :],
-                                words[:, CLASSES * gu : CLASSES * (gu + 1), :, group + n].rearrange("m c k -> m (c k)"),
+                                words[:, (group + n) // 2, CLASSES * gu : CLASSES * (gu + 1), :, n % 2].rearrange("m c k -> m (c k)"),
                                 identity_f32[:],
                             )
 
@@ -654,12 +656,12 @@ def tile_kanlayer_t_kernel(tc, x, spline_coeffs, spline_knots, out):
             park_x(nc, setup, transposed, identity, knot, x_rows, parked, 0)
             ready = [number for number in range(STEP_BUFS) if SUB_TILES * number < QUARTER]
             for number in ready:
-                load(number)
+                load(number, True)
             table, threshold = build_table(nc, const, setup, transposed, identity_f32, knot)
             for quarter in range(1, ROW_TILES // QUARTER):
                 park_x(nc, setup, transposed, identity, knot, x_rows, parked, quarter)
             for number in range(len(ready), STEP_BUFS):
-                load(number)
+                load(number, True)
             fetch, coefficient_steps = prepare_coefficients(setup)
             with tc.manual_schedule(engines={mybir.EngineType.DVE, mybir.EngineType.Activation, mybir.EngineType.PE}):
                 for action in look_up(states[0]) + interleave(fill_room(work_out(states[0]), []), look_up(states[1])):

@@ -29,23 +29,22 @@ GROUP_COLS = TILES_PER_GROUP * PASSES * P
 
 STEPS = 35
 LOW_STEPS = range(2, 6)
-ONE_STEP = STEPS + len(LOW_STEPS)
-STEP_ROWS = ONE_STEP + 1
+STEP_ROWS = STEPS + len(LOW_STEPS)
 TRIPLE = 3
-X_ROW = TRIPLE * STEP_ROWS
+ONE_ROW = TRIPLE * STEP_ROWS
+X_ROW = ONE_ROW + 1
 GROUPS = 5
 BLOCKS = 2 * GROUPS + 1
 GEO = 6
 LOOK = 1 + TRIPLE * GEO
 LAST = 1 + GEO
-HALF_BLOCKS = GROUPS + 1
 LOOK_SLOTS = GROUPS + 1
 CODE_BITS = 7
 FAR = 2.0**100
 
-CHUNK_TILES = (8, 8, 8, 8, 8, 8, 8, 8)
-SUB_TILES = 8
-STEP_BUFS = 3
+CHUNK_TILES = (8, 12, 16, 16, 8, 4)
+SUB_TILES = 4
+STEP_BUFS = 4
 QUARTER = 16
 PARK_HALF = 32
 PARK_TILES = 8
@@ -74,12 +73,18 @@ def load_knots(nc, pool, spline_knots):
     return knot
 
 
-def build_table(nc, const, pool, psum, identity_f32, knot):
+def step_levels(nc, pool, knot):
+    level = pool.tile([P, STEP_ROWS], F32)
+    nc.vector.tensor_copy(out=level[:, 0:STEPS], in_=knot[:, 3 : 3 + STEPS])
+    nc.vector.tensor_copy(out=level[:, STEPS:STEP_ROWS], in_=knot[:, 2 + LOW_STEPS[0] : 3 + LOW_STEPS[-1]])
+    return level
+
+
+def build_table(nc, const, pool, psum, identity_f32, knot, level):
     level_col = LOOK + 1
     wide = pool.tile([P, LOOK + 2, P], F32)
     nc.gpsimd.memset(wide[:], 0.0)
     for c in range(TRIPLE):
-        nc.gpsimd.memset(wide[:, 1 + GEO * c : 1 + GEO * c + 4, X_ROW + 2 * c : X_ROW + 2 * c + 1], 1.0)
         for col, unit in ((0, 2.0 ** (CODE_BITS * c)), (LOOK, float(c == 1))):
             for n, change in enumerate((1.0, 2.0, 4.0, 1.0)):
                 if unit > 0:
@@ -104,16 +109,14 @@ def build_table(nc, const, pool, psum, identity_f32, knot):
     low_rows = slice(LOW_STEPS[0] - 1, LOW_STEPS[-1])
     rounded = pool.tile([P, GEO, len(LOW_STEPS)], BF16)
     nc.vector.tensor_copy(out=rounded[:], in_=changes[:, :, low_rows])
-    nc.vector.tensor_sub(out=rows_of[:, :, STEPS:ONE_STEP], in0=changes[:, :, low_rows], in1=rounded[:])
-    nc.vector.tensor_copy(out=rows_of[:, :, ONE_STEP:STEP_ROWS], in_=cell[:, :, 0:1])
-    level = pool.tile([P, STEP_ROWS], F32)
-    nc.vector.memset(level[:, ONE_STEP:STEP_ROWS], -FAR)
-    nc.vector.tensor_copy(out=level[:, 0:STEPS], in_=knot[:, 3 : 3 + STEPS])
-    nc.vector.tensor_copy(out=level[:, STEPS:ONE_STEP], in_=knot[:, 2 + LOW_STEPS[0] : 3 + LOW_STEPS[-1]])
+    nc.vector.tensor_sub(out=rows_of[:, :, STEPS:STEP_ROWS], in0=changes[:, :, low_rows], in1=rounded[:])
     for c in range(TRIPLE):
         mine = slice(1 + GEO * c, 1 + GEO * (c + 1))
-        nc.vector.tensor_copy(out=wide[:, mine, c:X_ROW:TRIPLE], in_=rows_of[:])
-        nc.vector.tensor_copy(out=wide[:, level_col, c:X_ROW:TRIPLE], in_=level[:])
+        nc.vector.tensor_copy(out=wide[:, mine, c:ONE_ROW:TRIPLE], in_=rows_of[:])
+        nc.vector.tensor_copy(out=wide[:, level_col, c:ONE_ROW:TRIPLE], in_=level[:])
+        nc.vector.tensor_copy(out=wide[:, mine, ONE_ROW:X_ROW], in_=cell[:, :, 0:1])
+        nc.vector.memset(wide[:, 1 + GEO * c : 1 + GEO * c + 4, X_ROW + c : X_ROW + c + 1], 1.0)
+    nc.vector.memset(wide[:, level_col, ONE_ROW:X_ROW], -FAR)
 
     table = const.tile([P, LOOK + LAST], BF16)
     threshold = const.tile([P, 1], F32)
@@ -131,14 +134,11 @@ def build_table(nc, const, pool, psum, identity_f32, knot):
     return table, threshold
 
 
-def park_x(nc, pool, psum, identity, knot, x_rows, parked, quarter):
-    tiles = slice(QUARTER * quarter, QUARTER * (quarter + 1))
-    clamped = pool.tile([P, QUARTER, FEATURES], BF16, name="clamped%d" % quarter)
-
+def clamp_x(nc, knot, source, target):
     def clamp(out_columns, in_columns):
         nc.vector.tensor_scalar(
-            out=clamped[:, :, out_columns], in0=x_rows[:, tiles, in_columns],
-            scalar1=knot[:, 38:39], scalar2=knot[:, 2:3], op0=ALU.min, op1=ALU.max,
+            out=target(out_columns), in0=source(in_columns), scalar1=knot[:, 38:39], scalar2=knot[:, 2:3],
+            op0=ALU.min, op1=ALU.max,
         )
 
     cuts = sorted(set(list(range(0, QUADS - 1, CLASSES)) + list(range(0, QUADS, GROUPS))))
@@ -150,6 +150,12 @@ def park_x(nc, pool, psum, identity, knot, x_rows, parked, quarter):
             count = q1 - q0
             clamp(slice(r, r + 3 * count - 2, 3), slice(i, i + count))
     clamp(slice(FEATURES - 2, FEATURES), slice(FEATURES - 5, FEATURES, 4))
+
+
+def park_x(nc, pool, psum, identity, knot, x_rows, parked, quarter):
+    tiles = slice(QUARTER * quarter, QUARTER * (quarter + 1))
+    clamped = pool.tile([P, QUARTER, FEATURES], BF16, name="clamped%d" % quarter)
+    clamp_x(nc, knot, lambda columns: x_rows[:, tiles, columns], lambda columns: clamped[:, :, columns])
     flipped = psum.tile([P, 4, P], BF16, tag="transposed", name="flipped_x")
     for n in range(4):
         nc.tensor.transpose(flipped[:, n, :], clamped[:, 4 * n : 4 * n + 4, :].rearrange("m a i -> m (a i)"), identity[:])
@@ -196,7 +202,7 @@ def tile_kanlayer_t_kernel(tc, x, spline_coeffs, spline_knots, out):
         planes = ctx.enter_context(tc.tile_pool(name="planes", bufs=1))
         keys = ctx.enter_context(tc.tile_pool(name="keys", bufs=1))
         carried = ctx.enter_context(tc.tile_pool(name="carried", bufs=2))
-        rows_pool = ctx.enter_context(tc.tile_pool(name="rows", bufs=3))
+        rows_pool = ctx.enter_context(tc.tile_pool(name="rows", bufs=2))
         transposed = ctx.enter_context(tc.psum_pool(name="transposed", bufs=4))
         lookups = ctx.enter_context(tc.psum_pool(name="lookups", bufs=2))
         sums = ctx.enter_context(tc.psum_pool(name="sums", bufs=2))
@@ -224,7 +230,7 @@ def tile_kanlayer_t_kernel(tc, x, spline_coeffs, spline_knots, out):
 
             def fetch():
                 for h in range(halves):
-                    nc.scalar.dma_start(
+                    nc.sync.dma_start(
                         out=natural[:, h, :].rearrange("q (i k) -> q i k", k=KNOTS),
                         in_=spline_coeffs[:, P * h : P * h + P, :].rearrange("i q k -> q i k"),
                     )
@@ -250,52 +256,40 @@ def tile_kanlayer_t_kernel(tc, x, spline_coeffs, spline_knots, out):
 
             return fetch, [lambda: turn(0), lambda: turn(1), lambda: group(0), lambda: group(1), quantise]
 
-        def load(number, ahead=False):
+        def load(number, whole=False):
             tile0 = SUB_TILES * number
             words = slice((tile0 % PARK_HALF) * P // 2, (tile0 % PARK_HALF + SUB_TILES) * P // 2)
             source = parked[0 : TRIPLE * BLOCKS, tile0 // PARK_HALF, words].rearrange("(g c) w -> c g w", c=TRIPLE)
             target = x_steps[number % STEP_BUFS][:].bitcast(F32)
+            last_row = P if whole else X_ROW + TRIPLE
             for c in range(TRIPLE):
-                for first, last in ((0, 32), (32, STEP_ROWS)):
-                    rows = slice(TRIPLE * first + c, TRIPLE * (last - 1) + c + 1, TRIPLE)
-                    for queue, blocks in ((nc.sync, slice(0, HALF_BLOCKS)), (nc.sync if ahead else nc.scalar, slice(HALF_BLOCKS, BLOCKS))):
-                        queue.dma_start(
-                            out=target[rows, blocks, :], in_=source[c, blocks].partition_broadcast(last - first)
-                        )
-            for c, first, last in ((0, X_ROW, X_ROW + 2), (1, X_ROW + 2, X_ROW + 4), (2, X_ROW + 4, P)):
+                blocks = slice(0, BLOCKS if whole or c < 2 else BLOCKS - 1)
+                nc.sync.dma_start(
+                    out=target[c:ONE_ROW:TRIPLE, blocks, :], in_=source[c, blocks].partition_broadcast(STEP_ROWS)
+                )
+            for c, first, last in ((0, ONE_ROW, X_ROW + 1), (1, X_ROW + 1, X_ROW + 2), (2, X_ROW + 2, last_row)):
                 nc.sync.dma_start(out=target[first:last, :, :], in_=source[c].partition_broadcast(last - first))
 
-        def look_up(state):
+        def lookup_steps(state):
             slots = 2 * state["tiles"]
-            actions = []
             banks = {}
 
-            def start():
+            def cell_and_geo():
                 state["cell"] = carried.tile([P, slots // 4, LOOK_SLOTS, 4], U32, name="cell")
                 state["geo"] = carried.tile([P, GEO, slots // 4, QUADS, 4], F32, name="geo")
 
-            def compare(number):
-                steps = x_steps[number % STEP_BUFS]
-                mine = steps[0:X_ROW, :, :]
-                nc.vector.tensor_scalar(
-                    out=mine, in0=mine, scalar1=threshold[0:X_ROW, :], scalar2=None, op0=ALU.is_ge
-                )
-
-            def multiply(pair, number):
-                steps = x_steps[number % STEP_BUFS]
+            def multiply(pair, steps_of):
                 bank = lookups.tile([P, LOOK, LOOK_SLOTS, 2, 2], F32, name="bank")
                 banks[pair] = bank
                 for half in range(2):
-                    tile = pair + half - SUB_TILES * number + state["first"]
-                    columns = slice(P * tile, P * (tile + 1))
                     for e in range(2):
                         for g in range(GROUPS):
                             nc.tensor.matmul(
-                                bank[:, :, g, half, e], lhsT=steps[:, GROUPS * e + g, columns],
+                                bank[:, :, g, half, e], lhsT=steps_of(pair + half, GROUPS * e + g),
                                 rhs=table[:, 0:LOOK], start=True, stop=True,
                             )
                         nc.tensor.matmul(
-                            bank[:, 0:LAST, GROUPS, half, e], lhsT=steps[:, BLOCKS - 1, columns],
+                            bank[:, 0:LAST, GROUPS, half, e], lhsT=steps_of(pair + half, BLOCKS - 1),
                             rhs=table[:, LOOK * e : LOOK * e + LAST], start=True, stop=True,
                         )
 
@@ -310,17 +304,86 @@ def tile_kanlayer_t_kernel(tc, x, spline_coeffs, spline_knots, out):
                         in_=bank[:, 1 + GEO * c : 1 + GEO * (c + 1), 0:count, :], func=ACT.Abs,
                     )
 
-            actions.append(start)
+            return cell_and_geo, multiply, evacuate
+
+        def look_up(state):
+            cell_and_geo, multiply, evacuate = lookup_steps(state)
+
+            def compare(number):
+                mine = x_steps[number % STEP_BUFS][0:X_ROW, :, :]
+                nc.vector.tensor_scalar(
+                    out=mine, in0=mine, scalar1=threshold[0:X_ROW, :], scalar2=None, op0=ALU.is_ge
+                )
+
+            def multiply_sub(pair, number):
+                first = SUB_TILES * number - state["first"]
+
+                def steps_of(tile, block):
+                    return x_steps[number % STEP_BUFS][:, block, P * (tile - first) : P * (tile - first + 1)]
+
+                multiply(pair, steps_of)
+
+            actions = [cell_and_geo]
             for first in range(0, state["tiles"], SUB_TILES):
                 number = (state["first"] + first) // SUB_TILES
                 actions.append(lambda number=number: compare(number))
                 for pair in range(first, first + SUB_TILES, 2):
-                    actions.append(lambda pair=pair, number=number: multiply(pair, number))
+                    actions.append(lambda pair=pair, number=number: multiply_sub(pair, number))
                     if pair > first:
                         actions.append(lambda pair=pair: evacuate(pair - 2))
                 actions.append(lambda first=first: evacuate(first + SUB_TILES - 2))
                 if SUB_TILES * (number + STEP_BUFS) < ROW_TILES:
                     actions.append(lambda number=number: load(number + STEP_BUFS))
+            return actions
+
+        def steps_by_rows(setup, x_rows, knot, level, tiles):
+            by_rows = rows_pool.tile([P, BLOCKS, P, tiles], BF16, tag="rows", name="by_rows")
+            features = setup.tile([P, BLOCKS, TRIPLE, tiles], BF16, name="features")
+            flat = features[:].rearrange("m b c x -> m (b c) x")
+            clamp_x(
+                nc, knot, lambda columns: x_rows[:, 0:tiles, columns].rearrange("m a i -> m i a"),
+                lambda columns: flat[:, columns, :],
+            )
+            nc.vector.tensor_copy(out=flat[:, FEATURES, :], in_=flat[:, FEATURES - 1, :])
+
+            def rows(first, last):
+                return by_rows[:, :, first:last, :].rearrange("m b r x -> m b (r x)")
+
+            source = features[:].rearrange("m b c x -> m b (c x)")
+            for n in range(STEP_ROWS):
+                nc.vector.tensor_scalar(
+                    out=rows(TRIPLE * n, TRIPLE * (n + 1)), in0=source, scalar1=level[:, n : n + 1], scalar2=None,
+                    op0=ALU.is_ge,
+                )
+            nc.vector.memset(rows(ONE_ROW, X_ROW), 1.0)
+            nc.vector.tensor_copy(out=rows(X_ROW, X_ROW + TRIPLE), in_=source)
+            nc.vector.memset(rows(X_ROW + TRIPLE, P), 0.0)
+            return by_rows
+
+        def turn_steps(by_rows, tiles):
+            turned = rows_pool.tile([P, BLOCKS, tiles // 2, P, 2], BF16, tag="rows", name="turned_steps")
+            words = by_rows[:].bitcast(F32)
+            for block in range(BLOCKS):
+                flipped = transposed.tile([P, tiles // 2, P], F32, tag="transposed", name="flipped_steps")
+                for pair in range(tiles // 2):
+                    nc.tensor.transpose(flipped[:, pair, :], words[:, block, :, pair], identity_f32[:])
+                nc.scalar.copy(
+                    out=turned[:, block].rearrange("p a m x -> p (a m x)").bitcast(F32),
+                    in_=flipped[:].rearrange("p a m -> p (a m)"),
+                )
+            return turned
+
+        def look_up_turned(state, turned):
+            tiles = state["tiles"]
+            cell_and_geo, multiply, evacuate = lookup_steps(state)
+            actions = [cell_and_geo]
+            for pair in range(0, tiles, 2):
+                actions.append(
+                    lambda pair=pair: multiply(pair, lambda tile, block: turned[:, block, tile // 2, :, tile % 2])
+                )
+                if pair > 0:
+                    actions.append(lambda pair=pair: evacuate(pair - 2))
+            actions.append(lambda: evacuate(tiles - 2))
             return actions
 
         def work_out(state):
@@ -638,39 +701,41 @@ def tile_kanlayer_t_kernel(tc, x, spline_coeffs, spline_knots, out):
             if n + 2 < len(states):
                 side.append(look_up(states[n + 2]))
             side.extend(more)
-            if n >= 2:
-                ending = finish(states[n - 1], n == len(states) - 1)
-                if n == 2:
-                    ending = finish(states[0], False) + ending
-                side.append(ending)
+            if n > 0:
+                side.append(finish(states[n - 1], n == len(states) - 1))
             for action in interleave(*side):
                 action()
 
-        pools["work"] = ctx.enter_context(tc.tile_pool(name="work", bufs=2))
         with tc.tile_pool(name="setup", bufs=1) as setup:
             knot = load_knots(nc, setup, spline_knots)
+            level = step_levels(nc, setup, knot)
             x_rows = setup.tile([P, ROW_TILES, FEATURES], BF16)
             x_by_rows = x.rearrange("(m a) i -> m a i", a=ROW_TILES)
             nc.sync.dma_start(out=x_rows[:, 0:QUARTER, :], in_=x_by_rows[:, 0:QUARTER, :])
             nc.scalar.dma_start(out=x_rows[:, QUARTER:ROW_TILES, :], in_=x_by_rows[:, QUARTER:ROW_TILES, :])
+            by_rows = steps_by_rows(setup, x_rows, knot, level, states[0]["tiles"])
             park_x(nc, setup, transposed, identity, knot, x_rows, parked, 0)
-            ready = [number for number in range(STEP_BUFS) if SUB_TILES * number < QUARTER]
+            first_load = states[0]["tiles"] // SUB_TILES
+            loads = range(first_load, first_load + STEP_BUFS)
+            ready = [number for number in loads if SUB_TILES * (number + 1) <= QUARTER]
             for number in ready:
                 load(number, True)
-            table, threshold = build_table(nc, const, setup, transposed, identity_f32, knot)
+            turned = turn_steps(by_rows, states[0]["tiles"])
+            table, threshold = build_table(nc, const, setup, transposed, identity_f32, knot, level)
+            fetch, coefficient_steps = prepare_coefficients(setup)
+            fetch()
             for quarter in range(1, ROW_TILES // QUARTER):
                 park_x(nc, setup, transposed, identity, knot, x_rows, parked, quarter)
-            for number in range(len(ready), STEP_BUFS):
+            for number in loads[len(ready) :]:
                 load(number, True)
-            fetch, coefficient_steps = prepare_coefficients(setup)
             with tc.manual_schedule(engines={mybir.EngineType.DVE, mybir.EngineType.Activation, mybir.EngineType.PE}):
-                for action in look_up(states[0]) + interleave(fill_room(work_out(states[0]), []), look_up(states[1])):
+                beside = interleave(fill_room(work_out(states[0]), []), look_up(states[1]))
+                for action in look_up_turned(states[0], turned) + beside:
                     action()
-                fetch()
-                phase(0)
-                phase(1, [lambda: None] * 10 + coefficient_steps)
+                phase(0, [lambda: None] * 5 + coefficient_steps)
+        pools["work"] = ctx.enter_context(tc.tile_pool(name="work", bufs=2))
         with tc.manual_schedule(engines={mybir.EngineType.DVE, mybir.EngineType.Activation, mybir.EngineType.PE}):
-            for n in range(2, len(states)):
+            for n in range(1, len(states)):
                 phase(n)
             for action in finish(states[-1], True):
                 action()

@@ -42,7 +42,7 @@ LOOK_SLOTS = GROUPS + 1
 CODE_BITS = 7
 FAR = 2.0**100
 
-CHUNK_TILES = (8, 12, 16, 16, 8, 4)
+CHUNK_TILES = (8, 8, 16, 16, 8, 8)
 SUB_TILES = 4
 STEP_BUFS = 4
 QUARTER = 16
@@ -155,20 +155,32 @@ def clamp_x(nc, knot, source, target):
 def park_x(nc, pool, psum, identity, knot, x_rows, parked, quarter):
     tiles = slice(QUARTER * quarter, QUARTER * (quarter + 1))
     clamped = pool.tile([P, QUARTER, FEATURES], BF16, name="clamped%d" % quarter)
-    clamp_x(nc, knot, lambda columns: x_rows[:, tiles, columns], lambda columns: clamped[:, :, columns])
-    flipped = psum.tile([P, 4, P], BF16, tag="transposed", name="flipped_x")
-    for n in range(4):
-        nc.tensor.transpose(flipped[:, n, :], clamped[:, 4 * n : 4 * n + 4, :].rearrange("m a i -> m (a i)"), identity[:])
     turned = pool.tile([P, 4, P], BF16, name="turned%d" % quarter)
-    nc.scalar.copy(out=turned[:], in_=flipped[:])
-    words = turned[:].bitcast(F32)
-    queue = nc.sync if quarter == 0 else nc.scalar
-    size = QUARTER * P // 2
-    at = quarter % 2 * size
-    place = parked[:, quarter // 2, at : at + size].rearrange("r (n b w) -> r n b w", n=4, b=4)
-    for b in range(4):
-        queue.dma_start(out=place[0:FEATURES, :, b, :], in_=words[FEATURES * b : FEATURES * (b + 1)])
-    queue.dma_start(out=place[FEATURES].rearrange("n b w -> b n w"), in_=words[FEATURES - 1 : P : FEATURES])
+    flips = []
+
+    def clamp():
+        clamp_x(nc, knot, lambda columns: x_rows[:, tiles, columns], lambda columns: clamped[:, :, columns])
+
+    def turn():
+        flips.append(psum.tile([P, 4, P], BF16, tag="transposed", name="flipped_x"))
+        for n in range(4):
+            nc.tensor.transpose(
+                flips[0][:, n, :], clamped[:, 4 * n : 4 * n + 4, :].rearrange("m a i -> m (a i)"), identity[:]
+            )
+
+    def copy():
+        nc.scalar.copy(out=turned[:], in_=flips[0][:])
+
+    def send():
+        words = turned[:].bitcast(F32)
+        size = QUARTER * P // 2
+        at = quarter % 2 * size
+        place = parked[:, quarter // 2, at : at + size].rearrange("r (n b w) -> r n b w", n=4, b=4)
+        for b in range(4):
+            nc.sync.dma_start(out=place[0:FEATURES, :, b, :], in_=words[FEATURES * b : FEATURES * (b + 1)])
+        nc.sync.dma_start(out=place[FEATURES].rearrange("n b w -> b n w"), in_=words[FEATURES - 1 : P : FEATURES])
+
+    return [clamp, turn, copy, send]
 
 
 def fill_room(items, others):
@@ -336,51 +348,74 @@ def tile_kanlayer_t_kernel(tc, x, spline_coeffs, spline_knots, out):
                     actions.append(lambda number=number: load(number + STEP_BUFS))
             return actions
 
-        def steps_by_rows(setup, x_rows, knot, level, tiles):
-            by_rows = rows_pool.tile([P, BLOCKS, P, tiles], BF16, tag="rows", name="by_rows")
-            features = setup.tile([P, BLOCKS, TRIPLE, tiles], BF16, name="features")
-            flat = features[:].rearrange("m b c x -> m (b c) x")
-            clamp_x(
-                nc, knot, lambda columns: x_rows[:, 0:tiles, columns].rearrange("m a i -> m i a"),
-                lambda columns: flat[:, columns, :],
-            )
-            nc.vector.tensor_copy(out=flat[:, FEATURES, :], in_=flat[:, FEATURES - 1, :])
+        def steps_by_turning(state, setup, x_rows, knot, level):
+            tiles = state["tiles"]
+            first = state["first"]
+            t = {}
 
-            def rows(first, last):
-                return by_rows[:, :, first:last, :].rearrange("m b r x -> m b (r x)")
+            def source():
+                return t["features"][:].rearrange("m b c x -> m b (c x)")
 
-            source = features[:].rearrange("m b c x -> m b (c x)")
-            for n in range(STEP_ROWS):
+            def rows(row0, row1):
+                return t["by_rows"][:, :, row0:row1, :].rearrange("m b r x -> m b (r x)")
+
+            def clamp():
+                t["features"] = setup.tile([P, BLOCKS, TRIPLE, tiles], BF16, name="features%d" % first)
+                flat = t["features"][:].rearrange("m b c x -> m (b c) x")
+                clamp_x(
+                    nc, knot, lambda columns: x_rows[:, first : first + tiles, columns].rearrange("m a i -> m i a"),
+                    lambda columns: flat[:, columns, :],
+                )
+                nc.vector.tensor_copy(out=flat[:, FEATURES, :], in_=flat[:, FEATURES - 1, :])
+
+            def step(n):
+                if n == 0:
+                    t["by_rows"] = rows_pool.tile([P, BLOCKS, P, tiles], BF16, tag="rows", name="by_rows")
                 nc.vector.tensor_scalar(
-                    out=rows(TRIPLE * n, TRIPLE * (n + 1)), in0=source, scalar1=level[:, n : n + 1], scalar2=None,
+                    out=rows(TRIPLE * n, TRIPLE * (n + 1)), in0=source(), scalar1=level[:, n : n + 1], scalar2=None,
                     op0=ALU.is_ge,
                 )
-            nc.vector.memset(rows(ONE_ROW, X_ROW), 1.0)
-            nc.vector.tensor_copy(out=rows(X_ROW, X_ROW + TRIPLE), in_=source)
-            nc.vector.memset(rows(X_ROW + TRIPLE, P), 0.0)
-            return by_rows
 
-        def turn_steps(by_rows, tiles):
-            turned = rows_pool.tile([P, BLOCKS, tiles // 2, P, 2], BF16, tag="rows", name="turned_steps")
-            words = by_rows[:].bitcast(F32)
-            for block in range(BLOCKS):
-                flipped = transposed.tile([P, tiles // 2, P], F32, tag="transposed", name="flipped_steps")
+            def others():
+                nc.vector.memset(rows(ONE_ROW, X_ROW), 1.0)
+                nc.vector.tensor_copy(out=rows(X_ROW, X_ROW + TRIPLE), in_=source())
+                nc.vector.memset(rows(X_ROW + TRIPLE, P), 0.0)
+
+            def turn(block):
+                if block == 0:
+                    state["turned"] = rows_pool.tile(
+                        [P, BLOCKS, tiles // 2, P, 2], BF16, tag="rows", name="turned_steps"
+                    )
+                words = t["by_rows"][:].bitcast(F32)
+                t[block] = transposed.tile([P, tiles // 2, P], F32, tag="transposed", name="flipped_steps")
                 for pair in range(tiles // 2):
-                    nc.tensor.transpose(flipped[:, pair, :], words[:, block, :, pair], identity_f32[:])
-                nc.scalar.copy(
-                    out=turned[:, block].rearrange("p a m x -> p (a m x)").bitcast(F32),
-                    in_=flipped[:].rearrange("p a m -> p (a m)"),
-                )
-            return turned
+                    nc.tensor.transpose(t[block][:, pair, :], words[:, block, :, pair], identity_f32[:])
 
-        def look_up_turned(state, turned):
+            def copy(block):
+                nc.scalar.copy(
+                    out=state["turned"][:, block].rearrange("p a m x -> p (a m x)").bitcast(F32),
+                    in_=t[block][:].rearrange("p a m -> p (a m)"),
+                )
+
+            making = [clamp] + [lambda n=n: step(n) for n in range(STEP_ROWS)] + [others]
+            turning = []
+            for block in range(BLOCKS):
+                turning.append(lambda block=block: turn(block))
+                if block > 0:
+                    turning.append(lambda block=block: copy(block - 1))
+            turning.append(lambda: copy(BLOCKS - 1))
+            return making, turning
+
+        def look_up_turned(state):
             tiles = state["tiles"]
             cell_and_geo, multiply, evacuate = lookup_steps(state)
+
+            def steps_of(tile, block):
+                return state["turned"][:, block, tile // 2, :, tile % 2]
+
             actions = [cell_and_geo]
             for pair in range(0, tiles, 2):
-                actions.append(
-                    lambda pair=pair: multiply(pair, lambda tile, block: turned[:, block, tile // 2, :, tile % 2])
-                )
+                actions.append(lambda pair=pair: multiply(pair, steps_of))
                 if pair > 0:
                     actions.append(lambda pair=pair: evacuate(pair - 2))
             actions.append(lambda: evacuate(tiles - 2))
@@ -713,24 +748,26 @@ def tile_kanlayer_t_kernel(tc, x, spline_coeffs, spline_knots, out):
             x_by_rows = x.rearrange("(m a) i -> m a i", a=ROW_TILES)
             nc.sync.dma_start(out=x_rows[:, 0:QUARTER, :], in_=x_by_rows[:, 0:QUARTER, :])
             nc.scalar.dma_start(out=x_rows[:, QUARTER:ROW_TILES, :], in_=x_by_rows[:, QUARTER:ROW_TILES, :])
-            by_rows = steps_by_rows(setup, x_rows, knot, level, states[0]["tiles"])
-            park_x(nc, setup, transposed, identity, knot, x_rows, parked, 0)
-            first_load = states[0]["tiles"] // SUB_TILES
-            loads = range(first_load, first_load + STEP_BUFS)
-            ready = [number for number in loads if SUB_TILES * (number + 1) <= QUARTER]
-            for number in ready:
-                load(number, True)
-            turned = turn_steps(by_rows, states[0]["tiles"])
-            table, threshold = build_table(nc, const, setup, transposed, identity_f32, knot, level)
-            fetch, coefficient_steps = prepare_coefficients(setup)
-            fetch()
-            for quarter in range(1, ROW_TILES // QUARTER):
+            parks = [
                 park_x(nc, setup, transposed, identity, knot, x_rows, parked, quarter)
-            for number in loads[len(ready) :]:
+                for quarter in range(1, ROW_TILES // QUARTER)
+            ]
+            first_steps, first_turn = steps_by_turning(states[0], setup, x_rows, knot, level)
+            for action in first_steps + parks[0]:
+                action()
+            table, threshold = build_table(nc, const, setup, transposed, identity_f32, knot, level)
+            first_load = QUARTER // SUB_TILES
+            for number in range(first_load, first_load + STEP_BUFS):
                 load(number, True)
+            fetch, coefficient_steps = prepare_coefficients(setup)
+            for action in first_turn:
+                action()
             with tc.manual_schedule(engines={mybir.EngineType.DVE, mybir.EngineType.Activation, mybir.EngineType.PE}):
-                beside = interleave(fill_room(work_out(states[0]), []), look_up(states[1]))
-                for action in look_up_turned(states[0], turned) + beside:
+                second_steps, second_turn = steps_by_turning(states[1], setup, x_rows, knot, level)
+                for action in interleave(second_steps, look_up_turned(states[0])):
+                    action()
+                second = second_turn + look_up_turned(states[1])
+                for action in interleave(fill_room(work_out(states[0]), []), second, [fetch] + parks[1] + parks[2]):
                     action()
                 phase(0, [lambda: None] * 5 + coefficient_steps)
         pools["work"] = ctx.enter_context(tc.tile_pool(name="work", bufs=2))

@@ -39,7 +39,7 @@ GEO = 6
 LOOK = 1 + TRIPLE * GEO
 LAST = 1 + GEO
 LOOK_SLOTS = GROUPS + 1
-CODE_BITS = 7
+CODE_BITS = 8
 FAR = 2.0**100
 
 CHUNK_TILES = (8, 8, 16, 16, 8, 8)
@@ -86,14 +86,14 @@ def build_table(nc, const, pool, psum, identity_f32, knot, level):
     nc.gpsimd.memset(wide[:], 0.0)
     for c in range(TRIPLE):
         for col, unit in ((0, 2.0 ** (CODE_BITS * c)), (LOOK, float(c == 1))):
-            for n, change in enumerate((1.0, 2.0, 4.0, 1.0)):
+            for n, change in enumerate((6.0, 5.0, 2.0, 3.0)):
                 if unit > 0:
                     nc.gpsimd.memset(wide[:, col, TRIPLE * n + c : TRIPLE * STEPS : 4 * TRIPLE], change * unit)
     span = pool.tile([P, KNOTS + 6], F32)
     nc.vector.tensor_sub(out=span[:], in0=knot[:, 3 : KNOTS + 9], in1=knot[:, 0 : KNOTS + 6])
     cell = pool.tile([P, GEO, STEPS + 1], F32)
     half = (STEPS + 1) // 2
-    for n, offsets in enumerate(((0, 1), (1, 0), (-1, 2), (2, -1))):
+    for n, offsets in enumerate(((0, 1), (-1, 2), (1, 0), (2, -1))):
         for odd in range(2):
             first = 2 + odd + offsets[odd]
             nc.vector.tensor_scalar_mul(
@@ -127,16 +127,16 @@ def build_table(nc, const, pool, psum, identity_f32, knot, level):
             nc.tensor.transpose(flipped[:, b, :], wide[:, first + b, :], identity_f32[:])
         in_table = min(count, level_col - first)
         if in_table > 0:
-            nc.vector.tensor_copy(out=table[:, first : first + in_table], in_=flipped[:, 0:in_table, 0])
+            nc.scalar.copy(out=table[:, first : first + in_table], in_=flipped[:, 0:in_table, 0])
         if count > in_table:
-            nc.vector.tensor_copy(out=threshold[:], in_=flipped[:, count - 1 : count, 0])
-    nc.vector.tensor_copy(out=table[:, LOOK + 1 : LOOK + LAST], in_=table[:, 1 + GEO : 1 + 2 * GEO])
+            nc.scalar.copy(out=threshold[:], in_=flipped[:, count - 1 : count, 0])
+    nc.scalar.copy(out=table[:, LOOK + 1 : LOOK + LAST], in_=table[:, 1 + GEO : 1 + 2 * GEO])
     return table, threshold
 
 
-def clamp_x(nc, knot, source, target):
+def clamp_x(engine, knot, source, target):
     def clamp(out_columns, in_columns):
-        nc.vector.tensor_scalar(
+        engine.tensor_scalar(
             out=target(out_columns), in0=source(in_columns), scalar1=knot[:, 38:39], scalar2=knot[:, 2:3],
             op0=ALU.min, op1=ALU.max,
         )
@@ -159,7 +159,10 @@ def park_x(nc, pool, psum, identity, knot, x_rows, parked, quarter):
     flips = []
 
     def clamp():
-        clamp_x(nc, knot, lambda columns: x_rows[:, tiles, columns], lambda columns: clamped[:, :, columns])
+        clamp_x(
+            nc.vector if quarter == 1 else nc.gpsimd, knot, lambda columns: x_rows[:, tiles, columns],
+            lambda columns: clamped[:, :, columns],
+        )
 
     def turn():
         flips.append(psum.tile([P, 4, P], BF16, tag="transposed", name="flipped_x"))
@@ -224,8 +227,6 @@ def tile_kanlayer_t_kernel(tc, x, spline_coeffs, spline_knots, out):
         identity_f32 = const.tile([P, P], F32)
         make_identity(nc, identity_f32[:])
         x_steps = [const.tile([P, BLOCKS, SUB_TILES * P], BF16, name="x_steps%d" % n) for n in range(STEP_BUFS)]
-        bits = const.tile([P, 6, 2 * QUADS * max(CHUNK_TILES)], BF16)
-        nc.gpsimd.memset(bits[:, 1, :], 1.0)
         w_codes = const.tile([P, PASSES, OUTS], U32, align_bytes=64)
         w_scales = const.tile([P, PASSES, OUTS], U8, align_bytes=64)
 
@@ -363,7 +364,7 @@ def tile_kanlayer_t_kernel(tc, x, spline_coeffs, spline_knots, out):
                 t["features"] = setup.tile([P, BLOCKS, TRIPLE, tiles], BF16, name="features%d" % first)
                 flat = t["features"][:].rearrange("m b c x -> m (b c) x")
                 clamp_x(
-                    nc, knot, lambda columns: x_rows[:, first : first + tiles, columns].rearrange("m a i -> m i a"),
+                    nc.vector, knot, lambda columns: x_rows[:, first : first + tiles, columns].rearrange("m a i -> m i a"),
                     lambda columns: flat[:, columns, :],
                 )
                 nc.vector.tensor_copy(out=flat[:, FEATURES, :], in_=flat[:, FEATURES - 1, :])
@@ -436,11 +437,11 @@ def tile_kanlayer_t_kernel(tc, x, spline_coeffs, spline_knots, out):
 
             def left_sums():
                 t["left"] = planes.tile([P, 2, lanes], F32, name="left")
-                vec.tensor_add(out=t["left"][:], in0=by_n()[:, 0:3:2], in1=twice(by_n()[:, 1]))
+                vec.tensor_add(out=t["left"][:], in0=by_n()[:, 0:2], in1=twice(by_n()[:, 2]))
 
             def right_sums():
                 t["right"] = planes.tile([P, 3, lanes], F32, name="right")
-                vec.tensor_add(out=t["right"][:, 0:2], in0=by_n()[:, 0:3:2], in1=twice(by_n()[:, 3]))
+                vec.tensor_add(out=t["right"][:, 0:2], in0=by_n()[:, 0:2], in1=twice(by_n()[:, 3]))
 
             def outer_roots():
                 t["outer"] = planes.tile([P, 2, lanes], F32, name="outer")
@@ -462,13 +463,10 @@ def tile_kanlayer_t_kernel(tc, x, spline_coeffs, spline_knots, out):
                 act(out=t["right"][:, 1], in_=t["right"][:, 1], func=ACT.Square)
 
             def outer_ratios():
-                vec.tensor_mul(out=t["outer"][:], in0=by_n()[:, 0:2], in1=t["outer"][:])
+                vec.tensor_mul(out=t["outer"][:], in0=by_n()[:, 0:3:2], in1=t["outer"][:])
 
             def inner_ratios():
-                vec.tensor_mul(out=t["right"][:, 0:2], in0=by_n()[:, 0:3:2], in1=t["right"][:, 0:2])
-
-            def low_ratio():
-                vec.tensor_mul(out=t["right"][:, 2], in0=by_n()[:, 1], in1=t["right"][:, 2])
+                vec.tensor_mul(out=t["right"][:], in0=by_n()[:, 0:3], in1=t["right"][:])
 
             def quadratics():
                 act(out=t["right"][:, 0:3:2], in_=t["right"][:, 0:3:2], func=ACT.Square)
@@ -511,36 +509,36 @@ def tile_kanlayer_t_kernel(tc, x, spline_coeffs, spline_knots, out):
                     scalar1=CODE_BITS * c, scalar2=2**CODE_BITS - 1, op0=ALU.logical_shift_right, op1=ALU.bitwise_and,
                 )
 
-            def part(at, shift, mask):
+            def part(at, shift):
                 if at == 0:
-                    t["parts"] = keys.tile([P, 4, lanes], I32, name="parts")
+                    t["parts"] = keys.tile([P, 2, lanes], I32, name="parts")
                 vec.tensor_scalar(
-                    out=t["parts"][:, at], in0=t["own"][:].rearrange("m a q x -> m (a q x)"), scalar1=shift, scalar2=mask,
+                    out=t["parts"][:, at], in0=t["own"][:].rearrange("m a q x -> m (a q x)"), scalar1=shift, scalar2=1,
                     op0=ALU.logical_shift_right, op1=ALU.bitwise_and,
                 )
 
             def parts_out():
-                act(out=bits[:, 2:6, 0:lanes], in_=t["parts"][:].bitcast(U32), func=ACT.Copy)
+                t["flags"] = keys.tile([P, 2, lanes], BF16, name="flags")
+                act(out=t["flags"][:], in_=t["parts"][:].bitcast(U32), func=ACT.Copy)
 
-            def swap_flag():
-                vec.tensor_sub(out=bits[:, 0, 0:lanes], in0=bits[:, 2, 0:lanes], in1=bits[:, 4, 0:lanes])
-
-            def by_four(tile):
-                return tile.rearrange("m (l x) -> m l x", x=4)
-
-            def slot_index():
-                t["index"] = carried.tile([P, lanes // 4, 4, 4], BF16, name="index")
-                vec.tensor_add(
-                    out=t["index"][:], in0=bits[:, 1:5, 0:lanes].rearrange("m s (l x) -> m l s x", x=4),
-                    in1=by_four(bits[:, 5, 0:lanes]).unsqueeze(2).to_broadcast([P, lanes // 4, 4, 4]),
+            def slot_number(s):
+                if s == 0:
+                    t["numbers"] = keys.tile([P, 4, lanes], U32, name="numbers")
+                act(
+                    out=t["numbers"][:, s], in_=t["own"][:].rearrange("m a q x -> m (a q x)").bitcast(U32),
+                    func=ACT.Copy, scale=1.0 / 16.0, bias=(4 - s) / 4.0 - 15.0 / 32.0,
                 )
+
+            def numbers_out():
+                t["index"] = carried.tile([P, lanes // 4, 4, 4], BF16, name="index")
+                act(out=t["index"][:], in_=t["numbers"][:].rearrange("m s (l x) -> m l s x", x=4), func=ACT.Copy)
 
             def pairs(tile):
                 return tile.rearrange("m (p h) n -> m p h n", h=2)
 
             def take():
                 t["moved"] = keys.tile([P, 4, lanes], BF16, name="moved")
-                flags = bits[:, 0:4:3, 0:lanes].unsqueeze(2).to_broadcast([P, 2, 2, lanes])
+                flags = t["flags"][:].unsqueeze(2).to_broadcast([P, 2, 2, lanes])
                 vec.tensor_mul(out=pairs(t["moved"][:]), in0=pairs(t["values"][:]), in1=flags)
 
             def keep():
@@ -574,22 +572,18 @@ def tile_kanlayer_t_kernel(tc, x, spline_coeffs, spline_knots, out):
                 lambda: own_cell(2),
                 right_roots,
                 ROOM,
-                lambda: part(0, 0, 1),
-                lambda: part(1, 1, 1),
+                lambda: part(0, 1),
                 outer_ratios,
-                lambda: part(2, 2, 1),
-                lambda: part(3, 3, 15),
+                lambda: part(1, 0),
                 middle_square,
                 parts_out,
                 ROOM,
                 ROOM,
                 inner_ratios,
-                low_ratio,
                 quadratics,
                 ROOM,
-                swap_flag,
+                lambda: slot_number(0),
                 ROOM,
-                slot_index,
                 ROOM,
                 cubics,
                 both_quadratics,
@@ -603,12 +597,16 @@ def tile_kanlayer_t_kernel(tc, x, spline_coeffs, spline_knots, out):
                 third_value,
                 second_value,
                 ROOM,
+                lambda: slot_number(1),
                 ROOM,
                 take,
+                lambda: slot_number(2),
                 ROOM,
                 keep,
+                lambda: slot_number(3),
                 ROOM,
                 lambda: join(0),
+                numbers_out,
                 lambda: join(1),
                 hand_over,
                 ROOM,
@@ -714,8 +712,8 @@ def tile_kanlayer_t_kernel(tc, x, spline_coeffs, spline_knots, out):
                 stages.append((quantise, multiply, send))
 
             actions = []
-            for n in range(state["tiles"] + 7):
-                for late, stage in ((6, 2), (4, 1), (3, 0)):
+            for n in range(state["tiles"] + 9):
+                for late, stage in ((8, 2), (6, 1), (4, 0)):
                     group, rest = divmod(n - TILES_PER_GROUP + 1 - late, TILES_PER_GROUP)
                     if rest == 0 and 0 <= group < len(stages):
                         actions.append(stages[group][stage])
@@ -737,7 +735,7 @@ def tile_kanlayer_t_kernel(tc, x, spline_coeffs, spline_knots, out):
                 side.append(look_up(states[n + 2]))
             side.extend(more)
             if n > 0:
-                side.append(finish(states[n - 1], n == len(states) - 1))
+                side.append(finish(states[n - 1], False))
             for action in interleave(*side):
                 action()
 
@@ -748,6 +746,7 @@ def tile_kanlayer_t_kernel(tc, x, spline_coeffs, spline_knots, out):
             x_by_rows = x.rearrange("(m a) i -> m a i", a=ROW_TILES)
             nc.sync.dma_start(out=x_rows[:, 0:QUARTER, :], in_=x_by_rows[:, 0:QUARTER, :])
             nc.scalar.dma_start(out=x_rows[:, QUARTER:ROW_TILES, :], in_=x_by_rows[:, QUARTER:ROW_TILES, :])
+            table, threshold = build_table(nc, const, setup, transposed, identity_f32, knot, level)
             parks = [
                 park_x(nc, setup, transposed, identity, knot, x_rows, parked, quarter)
                 for quarter in range(1, ROW_TILES // QUARTER)
@@ -755,7 +754,6 @@ def tile_kanlayer_t_kernel(tc, x, spline_coeffs, spline_knots, out):
             first_steps, first_turn = steps_by_turning(states[0], setup, x_rows, knot, level)
             for action in first_steps + parks[0]:
                 action()
-            table, threshold = build_table(nc, const, setup, transposed, identity_f32, knot, level)
             first_load = QUARTER // SUB_TILES
             for number in range(first_load, first_load + STEP_BUFS):
                 load(number, True)
@@ -774,5 +772,5 @@ def tile_kanlayer_t_kernel(tc, x, spline_coeffs, spline_knots, out):
         with tc.manual_schedule(engines={mybir.EngineType.DVE, mybir.EngineType.Activation, mybir.EngineType.PE}):
             for n in range(1, len(states)):
                 phase(n)
-            for action in finish(states[-1], True):
+            for action in finish(states[-1], False):
                 action()

from contextlib import ExitStack

import concourse.mybir as mybir
from concourse.masks import make_identity

F32 = mybir.dt.float32
BF16 = mybir.dt.bfloat16
I32 = mybir.dt.int32
U32 = mybir.dt.uint32
U8 = mybir.dt.uint8
FP8X4 = mybir.dt.float8_e4m3fn_x4
ALU = mybir.AluOpType
ACT = mybir.ActivationFunctionType

P = 128
PACK = 4
ROWS = 8192
FEATURES = 32
OUTS = 256
KNOTS = 32
DEGREE = 3
PASSES = 2
CLASSES = P // KNOTS
PAIRS = PACK // 2
QUADS = PASSES * PAIRS * CLASSES
ROW_TILES = ROWS // P
TILES_PER_GROUP = 4
GROUP_COLS = TILES_PER_GROUP * PASSES * P

STEPS = 35
LOW_STEPS = range(2, 6)
STEP_ROWS = STEPS + len(LOW_STEPS)
TRIPLE = 3
ONE_ROW = TRIPLE * STEP_ROWS
X_ROW = ONE_ROW + 1
GROUPS = 5
BLOCKS = 2 * GROUPS + 1
GEO = 6
LOOK = 1 + TRIPLE * GEO
LAST = 1 + GEO
LOOK_SLOTS = GROUPS + 1
CODE_BITS = 8
FAR = 2.0**100

CHUNK_TILES = (8, 8, 16, 16, 8, 8)
SUB_TILES = 4
STEP_BUFS = 4
QUARTER = 16
PARK_HALF = 32
PARK_TILES = 8

ROOM = "room"

FLOPS = 2 * ROWS * FEATURES * KNOTS * OUTS


def load_knots(nc, pool, spline_knots):
    more = 7
    ramp = pool.tile([P, more], F32)
    for n in range(more):
        nc.gpsimd.memset(ramp[:, n : n + 1], float(n + 1))
    knots_bf = pool.tile([P, KNOTS], BF16)
    nc.sync.dma_start(out=knots_bf[:], in_=spline_knots.partition_broadcast(P))
    knot = pool.tile([P, 2 + KNOTS + more], F32)
    nc.vector.tensor_copy(out=knot[:, 2 : 2 + KNOTS], in_=knots_bf[:])
    step = pool.tile([P, 1], F32)
    nc.vector.tensor_sub(out=step[:], in0=knots_bf[:, 1:2], in1=knots_bf[:, 0:1])
    nc.vector.tensor_copy(out=knot[:, 0:2], in_=knots_bf[:, 0:1].to_broadcast([P, 2]))
    nc.vector.tensor_scalar(
        out=knot[:, 2 + KNOTS : 2 + KNOTS + more], in0=ramp[:], scalar1=step[:], scalar2=knot[:, 1 + KNOTS : 2 + KNOTS],
        op0=ALU.mult, op1=ALU.add,
    )
    return knot


def step_levels(nc, pool, knot):
    level = pool.tile([P, STEP_ROWS], F32)
    nc.vector.tensor_copy(out=level[:, 0:STEPS], in_=knot[:, 3 : 3 + STEPS])
    nc.vector.tensor_copy(out=level[:, STEPS:STEP_ROWS], in_=knot[:, 2 + LOW_STEPS[0] : 3 + LOW_STEPS[-1]])
    return level


def build_table(nc, const, pool, psum, identity_f32, knot, level):
    level_col = LOOK + 1
    wide = pool.tile([P, LOOK + 2, P], F32)
    nc.gpsimd.memset(wide[:], 0.0)
    for c in range(TRIPLE):
        for col, unit in ((0, 2.0 ** (CODE_BITS * c)), (LOOK, float(c == 1))):
            for n, change in enumerate((6.0, 5.0, 2.0, 3.0)):
                if unit > 0:
                    nc.gpsimd.memset(wide[:, col, TRIPLE * n + c : TRIPLE * STEPS : 4 * TRIPLE], change * unit)
    span = pool.tile([P, KNOTS + 6], F32)
    nc.vector.tensor_sub(out=span[:], in0=knot[:, 3 : KNOTS + 9], in1=knot[:, 0 : KNOTS + 6])
    cell = pool.tile([P, GEO, STEPS + 1], F32)
    half = (STEPS + 1) // 2
    for n, offsets in enumerate(((0, 1), (-1, 2), (1, 0), (2, -1))):
        for odd in range(2):
            first = 2 + odd + offsets[odd]
            nc.vector.tensor_scalar_mul(
                out=cell[:, n, odd : STEPS + 1 : 2], in0=knot[:, first : first + 2 * half - 1 : 2], scalar1=-1.0
            )
    for n, offsets in ((4, (0, -2)), (5, (-2, 0))):
        for odd in range(2):
            first = 2 + odd + offsets[odd]
            nc.vector.tensor_copy(out=cell[:, n, odd : STEPS + 1 : 2], in_=span[:, first : first + 2 * half - 1 : 2])
    rows_of = pool.tile([P, GEO, STEP_ROWS], F32)
    changes = rows_of[:, :, 0:STEPS]
    nc.vector.tensor_sub(out=changes, in0=cell[:, :, 1 : STEPS + 1], in1=cell[:, :, 0:STEPS])
    low_rows = slice(LOW_STEPS[0] - 1, LOW_STEPS[-1])
    rounded = pool.tile([P, GEO, len(LOW_STEPS)], BF16)
    nc.vector.tensor_copy(out=rounded[:], in_=changes[:, :, low_rows])
    nc.vector.tensor_sub(out=rows_of[:, :, STEPS:STEP_ROWS], in0=changes[:, :, low_rows], in1=rounded[:])
    for c in range(TRIPLE):
        mine = slice(1 + GEO * c, 1 + GEO * (c + 1))
        nc.vector.tensor_copy(out=wide[:, mine, c:ONE_ROW:TRIPLE], in_=rows_of[:])
        nc.vector.tensor_copy(out=wide[:, level_col, c:ONE_ROW:TRIPLE], in_=level[:])
        nc.vector.tensor_copy(out=wide[:, mine, ONE_ROW:X_ROW], in_=cell[:, :, 0:1])
        nc.vector.memset(wide[:, 1 + GEO * c : 1 + GEO * c + 4, X_ROW + c : X_ROW + c + 1], 1.0)
    nc.vector.memset(wide[:, level_col, ONE_ROW:X_ROW], -FAR)

    table = const.tile([P, LOOK + LAST], BF16)
    threshold = const.tile([P, 1], F32)
    for first in range(0, LOOK + 2, 4):
        count = min(4, LOOK + 2 - first)
        flipped = psum.tile([P, 4, P], F32, tag="transposed", name="flipped_table")
        for b in range(count):
            nc.tensor.transpose(flipped[:, b, :], wide[:, first + b, :], identity_f32[:])
        in_table = min(count, level_col - first)
        if in_table > 0:
            nc.scalar.copy(out=table[:, first : first + in_table], in_=flipped[:, 0:in_table, 0])
        if count > in_table:
            nc.scalar.copy(out=threshold[:], in_=flipped[:, count - 1 : count, 0])
    nc.scalar.copy(out=table[:, LOOK + 1 : LOOK + LAST], in_=table[:, 1 + GEO : 1 + 2 * GEO])
    return table, threshold


def clamp_x(engine, knot, source, target):
    def clamp(out_columns, in_columns):
        engine.tensor_scalar(
            out=target(out_columns), in0=source(in_columns), scalar1=knot[:, 38:39], scalar2=knot[:, 2:3],
            op0=ALU.min, op1=ALU.max,
        )

    cuts = sorted(set(list(range(0, QUADS - 1, CLASSES)) + list(range(0, QUADS, GROUPS))))
    for q0, q1 in zip(cuts[:-1], cuts[1:]):
        g, c = q0 % GROUPS, 2 - q0 // GROUPS
        for e in range(2):
            r = 3 * (GROUPS * e + g) + c
            i = 8 * (q0 // CLASSES) + 4 * e + q0 % CLASSES
            count = q1 - q0
            clamp(slice(r, r + 3 * count - 2, 3), slice(i, i + count))
    clamp(slice(FEATURES - 2, FEATURES), slice(FEATURES - 5, FEATURES, 4))


def park_x(nc, pool, psum, identity, knot, x_rows, parked, quarter):
    tiles = slice(QUARTER * quarter, QUARTER * (quarter + 1))
    clamped = pool.tile([P, QUARTER, FEATURES], BF16, name="clamped%d" % quarter)
    turned = pool.tile([P, 4, P], BF16, name="turned%d" % quarter)
    flips = []

    def clamp():
        clamp_x(
            nc.vector if quarter == 1 else nc.gpsimd, knot, lambda columns: x_rows[:, tiles, columns],
            lambda columns: clamped[:, :, columns],
        )

    def turn():
        flips.append(psum.tile([P, 4, P], BF16, tag="transposed", name="flipped_x"))
        for n in range(4):
            nc.tensor.transpose(
                flips[0][:, n, :], clamped[:, 4 * n : 4 * n + 4, :].rearrange("m a i -> m (a i)"), identity[:]
            )

    def copy():
        nc.scalar.copy(out=turned[:], in_=flips[0][:])

    def send():
        words = turned[:].bitcast(F32)
        size = QUARTER * P // 2
        at = quarter % 2 * size
        place = parked[:, quarter // 2, at : at + size].rearrange("r (n b w) -> r n b w", n=4, b=4)
        for b in range(4):
            nc.sync.dma_start(out=place[0:FEATURES, :, b, :], in_=words[FEATURES * b : FEATURES * (b + 1)])
        nc.sync.dma_start(out=place[FEATURES].rearrange("n b w -> b n w"), in_=words[FEATURES - 1 : P : FEATURES])

    return [clamp, turn, copy, send]


def fill_room(items, others):
    rooms = sum(1 for item in items if item == ROOM)
    merged = []
    used = 0
    seen = 0
    for item in items:
        if item == ROOM:
            seen += 1
            until = len(others) * seen // rooms
            merged.extend(others[used:until])
            used = until
        else:
            merged.append(item)
    return merged + others[used:]


def interleave(*lists):
    entries = []
    for which, items in enumerate(lists):
        for n, item in enumerate(items):
            entries.append(((n + 0.5) / len(items), which, n, item))
    return [entry[3] for entry in sorted(entries, key=lambda entry: entry[:3])]


def tile_kanlayer_t_kernel(tc, x, spline_coeffs, spline_knots, out):
    nc = tc.nc
    with ExitStack() as ctx:
        const = ctx.enter_context(tc.tile_pool(name="const", bufs=1))
        planes = ctx.enter_context(tc.tile_pool(name="planes", bufs=1))
        keys = ctx.enter_context(tc.tile_pool(name="keys", bufs=1))
        carried = ctx.enter_context(tc.tile_pool(name="carried", bufs=2))
        rows_pool = ctx.enter_context(tc.tile_pool(name="rows", bufs=2))
        transposed = ctx.enter_context(tc.psum_pool(name="transposed", bufs=4))
        lookups = ctx.enter_context(tc.psum_pool(name="lookups", bufs=2))
        sums = ctx.enter_context(tc.psum_pool(name="sums", bufs=2))

        identity = const.tile([P, P], BF16)
        make_identity(nc, identity[:])
        identity_f32 = const.tile([P, P], F32)
        make_identity(nc, identity_f32[:])
        x_steps = [const.tile([P, BLOCKS, SUB_TILES * P], BF16, name="x_steps%d" % n) for n in range(STEP_BUFS)]
        w_codes = const.tile([P, PASSES, OUTS], U32, align_bytes=64)
        w_scales = const.tile([P, PASSES, OUTS], U8, align_bytes=64)

        out_rows = out.rearrange("(m a) o -> m a o", a=ROW_TILES)
        parked = out_rows[:, ROW_TILES - PARK_TILES : ROW_TILES, :].rearrange("(r h) a o -> r h (a o)", h=ROW_TILES // PARK_HALF)

        pools = {}

        def prepare_coefficients(setup):
            halves = OUTS // P
            natural = setup.tile([P, halves, FEATURES * KNOTS], BF16)
            grouped = setup.tile([P, PASSES, OUTS, PACK], BF16, align_bytes=64)
            flips = {}

            def fetch():
                for h in range(halves):
                    nc.sync.dma_start(
                        out=natural[:, h, :].rearrange("q (i k) -> q i k", k=KNOTS),
                        in_=spline_coeffs[:, P * h : P * h + P, :].rearrange("i q k -> q i k"),
                    )

            def turn(g):
                flips[g] = transposed.tile([P, PACK, OUTS], BF16, tag="transposed", name="flipped_w")
                for t in range(PACK):
                    for h in range(halves):
                        first = (PACK * g + t) * P
                        nc.tensor.transpose(
                            flips[g][:, t, P * h : P * h + P], natural[:, h, first : first + P], identity[:]
                        )

            def group(g):
                nc.scalar.copy(out=grouped[:, g, :, :], in_=flips[g][:].rearrange("p t o -> p o t"))

            def quantise():
                nc.vector.quantize_mx(
                    out=w_codes[:].rearrange("p g o -> p (g o)").bitcast(FP8X4),
                    scales=w_scales[:].rearrange("p g o -> p (g o)"),
                    in_=grouped[:].rearrange("p g o t -> p (g o t)"),
                )

            return fetch, [lambda: turn(0), lambda: turn(1), lambda: group(0), lambda: group(1), quantise]

        def load(number, whole=False):
            tile0 = SUB_TILES * number
            words = slice((tile0 % PARK_HALF) * P // 2, (tile0 % PARK_HALF + SUB_TILES) * P // 2)
            source = parked[0 : TRIPLE * BLOCKS, tile0 // PARK_HALF, words].rearrange("(g c) w -> c g w", c=TRIPLE)
            target = x_steps[number % STEP_BUFS][:].bitcast(F32)
            last_row = P if whole else X_ROW + TRIPLE
            for c in range(TRIPLE):
                blocks = slice(0, BLOCKS if whole or c < 2 else BLOCKS - 1)
                nc.sync.dma_start(
                    out=target[c:ONE_ROW:TRIPLE, blocks, :], in_=source[c, blocks].partition_broadcast(STEP_ROWS)
                )
            for c, first, last in ((0, ONE_ROW, X_ROW + 1), (1, X_ROW + 1, X_ROW + 2), (2, X_ROW + 2, last_row)):
                nc.sync.dma_start(out=target[first:last, :, :], in_=source[c].partition_broadcast(last - first))

        def lookup_steps(state):
            slots = 2 * state["tiles"]
            banks = {}

            def cell_and_geo():
                state["cell"] = carried.tile([P, slots // 4, LOOK_SLOTS, 4], U32, name="cell")
                state["geo"] = carried.tile([P, GEO, slots // 4, QUADS, 4], F32, name="geo")

            def multiply(pair, steps_of):
                bank = lookups.tile([P, LOOK, LOOK_SLOTS, 2, 2], F32, name="bank")
                banks[pair] = bank
                for half in range(2):
                    for e in range(2):
                        for g in range(GROUPS):
                            nc.tensor.matmul(
                                bank[:, :, g, half, e], lhsT=steps_of(pair + half, GROUPS * e + g),
                                rhs=table[:, 0:LOOK], start=True, stop=True,
                            )
                        nc.tensor.matmul(
                            bank[:, 0:LAST, GROUPS, half, e], lhsT=steps_of(pair + half, BLOCKS - 1),
                            rhs=table[:, LOOK * e : LOOK * e + LAST], start=True, stop=True,
                        )

            def evacuate(pair):
                bank = banks[pair][:].rearrange("m w g a e -> m w g (a e)")
                nc.scalar.activation(out=state["cell"][:, pair // 2], in_=bank[:, 0], func=ACT.Copy)
                for c in range(TRIPLE):
                    count = LOOK_SLOTS if c == 0 else GROUPS
                    q0 = GROUPS * (2 - c)
                    nc.scalar.activation(
                        out=state["geo"][:, :, pair // 2, q0 : q0 + count, :],
                        in_=bank[:, 1 + GEO * c : 1 + GEO * (c + 1), 0:count, :], func=ACT.Abs,
                    )

            return cell_and_geo, multiply, evacuate

        def look_up(state):
            cell_and_geo, multiply, evacuate = lookup_steps(state)

            def compare(number):
                mine = x_steps[number % STEP_BUFS][0:X_ROW, :, :]
                nc.vector.tensor_scalar(
                    out=mine, in0=mine, scalar1=threshold[0:X_ROW, :], scalar2=None, op0=ALU.is_ge
                )

            def multiply_sub(pair, number):
                first = SUB_TILES * number - state["first"]

                def steps_of(tile, block):
                    return x_steps[number % STEP_BUFS][:, block, P * (tile - first) : P * (tile - first + 1)]

                multiply(pair, steps_of)

            actions = [cell_and_geo]
            for first in range(0, state["tiles"], SUB_TILES):
                number = (state["first"] + first) // SUB_TILES
                actions.append(lambda number=number: compare(number))
                for pair in range(first, first + SUB_TILES, 2):
                    actions.append(lambda pair=pair, number=number: multiply_sub(pair, number))
                    if pair > first:
                        actions.append(lambda pair=pair: evacuate(pair - 2))
                actions.append(lambda first=first: evacuate(first + SUB_TILES - 2))
                if SUB_TILES * (number + STEP_BUFS) < ROW_TILES:
                    actions.append(lambda number=number: load(number + STEP_BUFS))
            return actions

        def steps_by_turning(state, setup, x_rows, knot, level):
            tiles = state["tiles"]
            first = state["first"]
            t = {}

            def source():
                return t["features"][:].rearrange("m b c x -> m b (c x)")

            def rows(row0, row1):
                return t["by_rows"][:, :, row0:row1, :].rearrange("m b r x -> m b (r x)")

            def clamp():
                t["features"] = setup.tile([P, BLOCKS, TRIPLE, tiles], BF16, name="features%d" % first)
                flat = t["features"][:].rearrange("m b c x -> m (b c) x")
                clamp_x(
                    nc.vector, knot, lambda columns: x_rows[:, first : first + tiles, columns].rearrange("m a i -> m i a"),
                    lambda columns: flat[:, columns, :],
                )
                nc.vector.tensor_copy(out=flat[:, FEATURES, :], in_=flat[:, FEATURES - 1, :])

            def step(n):
                if n == 0:
                    t["by_rows"] = rows_pool.tile([P, BLOCKS, P, tiles], BF16, tag="rows", name="by_rows")
                nc.vector.tensor_scalar(
                    out=rows(TRIPLE * n, TRIPLE * (n + 1)), in0=source(), scalar1=level[:, n : n + 1], scalar2=None,
                    op0=ALU.is_ge,
                )

            def others():
                nc.vector.memset(rows(ONE_ROW, X_ROW), 1.0)
                nc.vector.tensor_copy(out=rows(X_ROW, X_ROW + TRIPLE), in_=source())
                nc.vector.memset(rows(X_ROW + TRIPLE, P), 0.0)

            def turn(block):
                if block == 0:
                    state["turned"] = rows_pool.tile(
                        [P, BLOCKS, tiles // 2, P, 2], BF16, tag="rows", name="turned_steps"
                    )
                words = t["by_rows"][:].bitcast(F32)
                t[block] = transposed.tile([P, tiles // 2, P], F32, tag="transposed", name="flipped_steps")
                for pair in range(tiles // 2):
                    nc.tensor.transpose(t[block][:, pair, :], words[:, block, :, pair], identity_f32[:])

            def copy(block):
                nc.scalar.copy(
                    out=state["turned"][:, block].rearrange("p a m x -> p (a m x)").bitcast(F32),
                    in_=t[block][:].rearrange("p a m -> p (a m)"),
                )

            making = [clamp] + [lambda n=n: step(n) for n in range(STEP_ROWS)] + [others]
            turning = []
            for block in range(BLOCKS):
                turning.append(lambda block=block: turn(block))
                if block > 0:
                    turning.append(lambda block=block: copy(block - 1))
            turning.append(lambda: copy(BLOCKS - 1))
            return making, turning

        def look_up_turned(state):
            tiles = state["tiles"]
            cell_and_geo, multiply, evacuate = lookup_steps(state)

            def steps_of(tile, block):
                return state["turned"][:, block, tile // 2, :, tile % 2]

            actions = [cell_and_geo]
            for pair in range(0, tiles, 2):
                actions.append(lambda pair=pair: multiply(pair, steps_of))
                if pair > 0:
                    actions.append(lambda pair=pair: evacuate(pair - 2))
            actions.append(lambda: evacuate(tiles - 2))
            return actions

        def work_out(state):
            slots = 2 * state["tiles"]
            lanes = QUADS * slots
            vec = nc.vector
            act = nc.scalar.activation
            t = {}

            def by_n():
                return state["geo"][:].rearrange("m n a q x -> m n (a q x)")

            def twice(one):
                return one.unsqueeze(1).to_broadcast([P, 2, lanes])

            def left_sums():
                t["left"] = planes.tile([P, 2, lanes], F32, name="left")
                vec.tensor_add(out=t["left"][:], in0=by_n()[:, 0:2], in1=twice(by_n()[:, 2]))

            def right_sums():
                t["right"] = planes.tile([P, 3, lanes], F32, name="right")
                vec.tensor_add(out=t["right"][:, 0:2], in0=by_n()[:, 0:2], in1=twice(by_n()[:, 3]))

            def outer_roots():
                t["outer"] = planes.tile([P, 2, lanes], F32, name="outer")
                act(out=t["outer"][:], in_=by_n()[:, 4:6], func=ACT.Abs_reciprocal_sqrt)

            def outer_squares():
                act(out=t["outer"][:], in_=t["outer"][:], func=ACT.Square)

            def upper_product():
                vec.tensor_mul(out=t["right"][:, 0], in0=t["left"][:, 0], in1=t["right"][:, 0])

            def lower_product():
                vec.tensor_mul(out=t["right"][:, 2], in0=t["left"][:, 0], in1=t["left"][:, 1])

            def right_roots():
                act(out=t["right"][:], in_=t["right"][:], func=ACT.Abs_reciprocal_sqrt)

            def middle_square():
                act(out=t["right"][:, 1], in_=t["right"][:, 1], func=ACT.Square)

            def outer_ratios():
                vec.tensor_mul(out=t["outer"][:], in0=by_n()[:, 0:3:2], in1=t["outer"][:])

            def inner_ratios():
                vec.tensor_mul(out=t["right"][:], in0=by_n()[:, 0:3], in1=t["right"][:])

            def quadratics():
                act(out=t["right"][:, 0:3:2], in_=t["right"][:, 0:3:2], func=ACT.Square)

            def cubics():
                vec.tensor_mul(out=t["outer"][:], in0=t["right"][:, 0:3:2], in1=t["outer"][:])

            def cubics_out():
                t["values"] = keys.tile([P, 4, lanes], BF16, name="values")
                act(out=t["values"][:, 0:3:2], in_=t["outer"][:], func=ACT.Copy)

            def both_quadratics():
                vec.tensor_add(out=t["left"][:, 0], in0=t["right"][:, 0], in1=t["right"][:, 2])

            def middle():
                vec.scalar_tensor_tensor(
                    out=t["left"][:, 0], in0=t["left"][:, 0], scalar=1.0, in1=t["right"][:, 1],
                    op0=ALU.subtract, op1=ALU.mult,
                )

            def upper_sum():
                vec.tensor_sub(out=t["right"][:, 0], in0=t["right"][:, 0], in1=t["left"][:, 0])

            def other_sum():
                vec.tensor_add(out=t["left"][:, 1], in0=t["right"][:, 0], in1=t["outer"][:, 1])

            def third_value():
                vec.tensor_sub(out=t["values"][:, 3], in0=t["right"][:, 0], in1=t["outer"][:, 0])

            def second_value():
                act(out=t["values"][:, 1], in_=t["left"][:, 1], func=ACT.Copy, scale=-1.0, bias=1.0)

            def own_cell(c):
                if c == 0:
                    t["own"] = keys.tile([P, slots // 4, QUADS, 4], I32, name="own")
                count = LOOK_SLOTS if c == 0 else GROUPS
                q0 = GROUPS * (2 - c)
                vec.tensor_scalar(
                    out=t["own"][:, :, q0 : q0 + count, :], in0=state["cell"][:, :, 0:count, :].bitcast(I32),
                    scalar1=CODE_BITS * c, scalar2=2**CODE_BITS - 1, op0=ALU.logical_shift_right, op1=ALU.bitwise_and,
                )

            def part(at, shift):
                if at == 0:
                    t["parts"] = keys.tile([P, 2, lanes], I32, name="parts")
                vec.tensor_scalar(
                    out=t["parts"][:, at], in0=t["own"][:].rearrange("m a q x -> m (a q x)"), scalar1=shift, scalar2=1,
                    op0=ALU.logical_shift_right, op1=ALU.bitwise_and,
                )

            def parts_out():
                t["flags"] = keys.tile([P, 2, lanes], BF16, name="flags")
                act(out=t["flags"][:], in_=t["parts"][:].bitcast(U32), func=ACT.Copy)

            def slot_number(s):
                if s == 0:
                    t["numbers"] = keys.tile([P, 4, lanes], U32, name="numbers")
                act(
                    out=t["numbers"][:, s], in_=t["own"][:].rearrange("m a q x -> m (a q x)").bitcast(U32),
                    func=ACT.Copy, scale=1.0 / 16.0, bias=(4 - s) / 4.0 - 15.0 / 32.0,
                )

            def numbers_out():
                t["index"] = carried.tile([P, lanes // 4, 4, 4], BF16, name="index")
                act(out=t["index"][:], in_=t["numbers"][:].rearrange("m s (l x) -> m l s x", x=4), func=ACT.Copy)

            def pairs(tile):
                return tile.rearrange("m (p h) n -> m p h n", h=2)

            def take():
                t["moved"] = keys.tile([P, 4, lanes], BF16, name="moved")
                flags = t["flags"][:].unsqueeze(2).to_broadcast([P, 2, 2, lanes])
                vec.tensor_mul(out=pairs(t["moved"][:]), in0=pairs(t["values"][:]), in1=flags)

            def keep():
                vec.tensor_sub(out=t["values"][:], in0=t["values"][:], in1=t["moved"][:])

            def join(h):
                if h == 0:
                    t["slot_values"] = carried.tile([P, lanes // 4, 4, 4], BF16, name="slot_values")

                def half(tile, which):
                    return pairs(tile[:])[:, :, which].rearrange("m p (l x) -> m l p x", x=4)

                vec.tensor_add(
                    out=t["slot_values"][:, :, 2 * h : 2 * h + 2, :], in0=half(t["values"], h), in1=half(t["moved"], 1 - h)
                )

            def hand_over():
                state["values"] = t["slot_values"]
                state["index"] = t["index"]

            return [
                left_sums,
                outer_roots,
                right_sums,
                ROOM,
                lambda: own_cell(0),
                outer_squares,
                upper_product,
                lambda: own_cell(1),
                lower_product,
                lambda: own_cell(2),
                right_roots,
                ROOM,
                lambda: part(0, 1),
                outer_ratios,
                lambda: part(1, 0),
                middle_square,
                parts_out,
                ROOM,
                ROOM,
                inner_ratios,
                quadratics,
                ROOM,
                lambda: slot_number(0),
                ROOM,
                ROOM,
                cubics,
                both_quadratics,
                cubics_out,
                ROOM,
                middle,
                ROOM,
                upper_sum,
                ROOM,
                other_sum,
                third_value,
                second_value,
                ROOM,
                lambda: slot_number(1),
                ROOM,
                take,
                lambda: slot_number(2),
                ROOM,
                keep,
                lambda: slot_number(3),
                ROOM,
                lambda: join(0),
                numbers_out,
                lambda: join(1),
                hand_over,
                ROOM,
                ROOM,
            ]

        def spread(state):
            slots = 2 * state["tiles"]

            def by_lane(tile):
                return tile[:].rearrange("m l s x -> m l (s x)")

            def four_knots(n):
                return state["rows"][:].rearrange("m a q k x -> m (a q) (k x)")[:, :, 16 * n : 16 * n + 16]

            def mark(n):
                if n == 0:
                    state["rows"] = rows_pool.tile([P, slots // 4, QUADS, KNOTS, 4], BF16, name="rows")
                nc.vector.tensor_scalar(
                    out=four_knots(n), in0=by_lane(state["index"]), scalar1=float(n + 1), scalar2=None, op0=ALU.is_equal
                )

            def fill(n):
                nc.vector.tensor_mul(out=four_knots(n), in0=four_knots(n), in1=by_lane(state["values"]))

            actions = [lambda: mark(0)]
            for n in range(KNOTS // 4):
                if n + 1 < KNOTS // 4:
                    actions.append(lambda n=n: mark(n + 1))
                actions.append(lambda n=n: fill(n))
            return actions

        def finish(state, shared):
            words = state["rows"][:].bitcast(F32)
            turns = []
            copies = []
            stages = []
            for group in range(0, state["tiles"], TILES_PER_GROUP):
                store = {}

                def turn(n, group=group, store=store):
                    if n == 0:
                        store["basis"] = pools["work"].tile(
                            [P, TILES_PER_GROUP, PASSES * P * PACK], BF16, align_bytes=64, name="basis"
                        )
                    flipped = transposed.tile([P, PASSES, PAIRS, P], F32, tag="transposed", name="flipped")
                    store[n] = flipped
                    for g in range(PASSES):
                        for u in range(PAIRS):
                            gu = PAIRS * g + u
                            nc.tensor.transpose(
                                flipped[:, g, u, :],
                                words[:, (group + n) // 2, CLASSES * gu : CLASSES * (gu + 1), :, n % 2].rearrange("m c k -> m (c k)"),
                                identity_f32[:],
                            )

                def copy(n, store=store):
                    copy_out = nc.vector.tensor_copy if shared and n % 2 == 1 else nc.scalar.copy
                    copy_out(
                        out=store["basis"][:, n, :].bitcast(F32).rearrange("p (g m u) -> p g m u", g=PASSES, u=PAIRS),
                        in_=store[n][:].rearrange("p g u m -> p g m u"),
                    )

                def quantise(store=store):
                    store["codes"] = pools["work"].tile([P, GROUP_COLS], U32, align_bytes=64, name="codes")
                    store["scales"] = pools["work"].tile([P, GROUP_COLS], U8, align_bytes=64, name="scales")
                    nc.vector.quantize_mx(
                        out=store["codes"][:].bitcast(FP8X4), scales=store["scales"][:],
                        in_=store["basis"][:].rearrange("p s n -> p (s n)"),
                    )

                def multiply(store=store):
                    store["acc"] = []
                    for pair in range(TILES_PER_GROUP // 2):
                        acc = sums.tile([P, 2, OUTS], F32, name="acc")
                        store["acc"].append(acc)
                        for half in range(2):
                            for g in range(PASSES):
                                n = (2 * pair + half) * PASSES + g
                                nc.tensor.matmul_mx(
                                    out=acc[:, half, :],
                                    lhsT=store["codes"][:, P * n : P * n + P].bitcast(FP8X4),
                                    lhsT_scale=store["scales"][:, P * n : P * n + P],
                                    rhs=w_codes[:, g, :].bitcast(FP8X4),
                                    rhs_scale=w_scales[:, g, :],
                                    start=(g == 0),
                                    stop=(g == PASSES - 1),
                                )

                def send(group=group, store=store):
                    result = pools["work"].tile([P, TILES_PER_GROUP, OUTS], F32, name="result")
                    for pair in range(TILES_PER_GROUP // 2):
                        if shared and pair == 1:
                            nc.vector.tensor_copy(out=result[:, 2 * pair : 2 * pair + 2, :], in_=store["acc"][pair][:])
                        else:
                            nc.scalar.copy(out=result[:, 2 * pair : 2 * pair + 2, :], in_=store["acc"][pair][:])
                    tile0 = state["first"] + group
                    nc.sync.dma_start(out=out_rows[:, tile0 : tile0 + TILES_PER_GROUP, :], in_=result[:])

                for n in range(TILES_PER_GROUP):
                    turns.append(lambda n=n, turn=turn: turn(n))
                    copies.append(lambda n=n, copy=copy: copy(n))
                stages.append((quantise, multiply, send))

            actions = []
            for n in range(state["tiles"] + 9):
                for late, stage in ((8, 2), (6, 1), (4, 0)):
                    group, rest = divmod(n - TILES_PER_GROUP + 1 - late, TILES_PER_GROUP)
                    if rest == 0 and 0 <= group < len(stages):
                        actions.append(stages[group][stage])
                if n < state["tiles"]:
                    actions.append(turns[n])
                if 0 <= n - 1 < state["tiles"]:
                    actions.append(copies[n - 1])
            return actions

        states = []
        for n, tiles in enumerate(CHUNK_TILES):
            states.append({"number": n, "first": sum(CHUNK_TILES[:n]), "tiles": tiles})

        def phase(n, *more):
            side = [spread(states[n])]
            if n + 1 < len(states):
                side = [fill_room(work_out(states[n + 1]), side[0])]
            if n + 2 < len(states):
                side.append(look_up(states[n + 2]))
            side.extend(more)
            if n > 0:
                side.append(finish(states[n - 1], False))
            for action in interleave(*side):
                action()

        with tc.tile_pool(name="setup", bufs=1) as setup:
            knot = load_knots(nc, setup, spline_knots)
            level = step_levels(nc, setup, knot)
            x_rows = setup.tile([P, ROW_TILES, FEATURES], BF16)
            x_by_rows = x.rearrange("(m a) i -> m a i", a=ROW_TILES)
            nc.sync.dma_start(out=x_rows[:, 0:QUARTER, :], in_=x_by_rows[:, 0:QUARTER, :])
            nc.scalar.dma_start(out=x_rows[:, QUARTER:ROW_TILES, :], in_=x_by_rows[:, QUARTER:ROW_TILES, :])
            table, threshold = build_table(nc, const, setup, transposed, identity_f32, knot, level)
            parks = [
                park_x(nc, setup, transposed, identity, knot, x_rows, parked, quarter)
                for quarter in range(1, ROW_TILES // QUARTER)
            ]
            first_steps, first_turn = steps_by_turning(states[0], setup, x_rows, knot, level)
            for action in first_steps + parks[0]:
                action()
            first_load = QUARTER // SUB_TILES
            for number in range(first_load, first_load + STEP_BUFS):
                load(number, True)
            fetch, coefficient_steps = prepare_coefficients(setup)
            for action in first_turn:
                action()
            with tc.manual_schedule(engines={mybir.EngineType.DVE, mybir.EngineType.Activation, mybir.EngineType.PE}):
                second_steps, second_turn = steps_by_turning(states[1], setup, x_rows, knot, level)
                for action in interleave(second_steps, look_up_turned(states[0])):
                    action()
                second = second_turn + look_up_turned(states[1])
                for action in interleave(fill_room(work_out(states[0]), []), second, [fetch] + parks[1] + parks[2]):
                    action()
                phase(0, [lambda: None] * 5 + coefficient_steps)
        pools["work"] = ctx.enter_context(tc.tile_pool(name="work", bufs=2))
        with tc.manual_schedule(engines={mybir.EngineType.DVE, mybir.EngineType.Activation, mybir.EngineType.PE}):
            for n in range(1, len(states)):
                phase(n)
            for action in finish(states[-1], False):
                action()
